import numpy as np
import ml_dtypes


def mxq(x, axis, fmt="e4m3"):
    dtype, down = {"e4m3": (ml_dtypes.float8_e4m3fn, 7), "e5m2": (ml_dtypes.float8_e5m2, 14)}[fmt]
    v = np.moveaxis(np.asarray(x, np.float32).astype(ml_dtypes.bfloat16).astype(np.float64), axis, -1)
    blocks = v.reshape(v.shape[:-1] + (-1, 32))
    amax = np.abs(blocks).max(-1, keepdims=True)
    byte = np.maximum(np.where(amax > 0, np.frexp(amax)[1] - 1 + 127, 0) - down, 1)
    scale = np.exp2(byte - 127.0)
    codes = (blocks / scale).astype(np.float32).astype(dtype).astype(np.float64)
    return np.moveaxis((codes * scale).reshape(v.shape), -1, axis)


WIDE = False


def mx_kscale(k):
    if not WIDE:
        return np.ones(k)
    levels = np.array([10, -10, 5, -5, 0])
    if k % 512:
        return np.exp2(np.random.permutation(np.resize(levels, k // 32))).repeat(32)
    a = np.empty((k // 512, 16))
    for p in range(k // 512):
        a[p, :8] = np.random.permutation(np.resize(levels, 8))
        for g in range(8):
            far = levels[np.abs(levels - a[p, g]) >= 10]
            a[p, g + 8] = far[np.random.randint(len(far))]
    return np.exp2(a.ravel()).repeat(32)


BF16 = ml_dtypes.bfloat16


def bf(x):
    return np.asarray(x, np.float32).astype(BF16)


def f64(x):
    return np.asarray(x).astype(np.float64)


B, N, D, H, DH = 2, 512, 1024, 16, 64
INNER = H * DH
S = 2 * DH


def dpfp(u):
    u2 = np.concatenate([np.maximum(u, 0.0), np.maximum(-u, 0.0)], axis=-1)
    return u2 * np.roll(u2, 1, axis=-1)


def draw0():
    s, t = mx_kscale(D), mx_kscale(N)
    f = dpfp(np.random.standard_normal((B, H, N, DH)))
    return {"x": bf(np.random.standard_normal((B, N, D)) * s),
            "wv": bf(np.random.standard_normal((D, INNER)) / np.sqrt(D) / s[:, None]),
            "beta": bf(np.random.standard_normal((B, H, N)) * t),
            "vo": bf(np.random.standard_normal((B, H, N, DH)) * 0.3),
            "k_phi": bf(f / f.sum(-1, keepdims=True) / t[:, None]),
            "W": bf(np.random.standard_normal((B, H, S, DH)))}


def core(x, wv, beta, vo, k_phi, W):
    v = mxq(f64(x), 2, "e4m3") @ mxq(f64(wv), 0, "e4m3")
    v = v.reshape(B, N, H, DH).transpose(0, 2, 1, 3)
    dv = f64(beta)[..., None] * (v - f64(vo))
    return f64(W) + (mxq(f64(k_phi).transpose(0, 1, 3, 2), 3, "e4m3") @ mxq(dv, 2, "e4m3"))


def e4m3fn_bytes(y):
    return np.clip(np.asarray(y, np.float64), -448.0, 448.0).astype(np.float32).astype(ml_dtypes.float8_e4m3fn).view(np.uint8)


def e4m3fn_values(b):
    return np.asarray(b, np.uint8).view(ml_dtypes.float8_e4m3fn).astype(np.float64)


def setup_inputs():
    d = draw0()
    x0 = np.asarray(d['k_phi']).astype(np.float64)
    s = (np.max(np.abs(x0), axis=(0, 1, 3), keepdims=True) / 448.0).astype(np.float32)
    out = {}
    for k, v in d.items():
        if k == 'k_phi':
            out['k_phi_bytes'] = e4m3fn_bytes(x0 / s.astype(np.float64))
            out['k_phi_scale'] = s
        else:
            out[k] = v
    return out


def reference(x, wv, beta, vo, k_phi_bytes, k_phi_scale, W):
    return core(x, wv, beta, vo, e4m3fn_values(k_phi_bytes) * k_phi_scale.astype(np.float64), W)

@@ -1,0 +1,401 @@
+from contextlib import ExitStack
+
+import concourse.mybir as mybir
+from concourse.masks import make_identity
+
+B, N, D, H, DH = 2, 512, 1024, 16, 64
+S = 128
+FLOPS = 2 * B * N * D * H * DH + 2 * B * H * N * S * DH
+
+F32 = mybir.dt.float32
+BF16 = mybir.dt.bfloat16
+U32 = mybir.dt.uint32
+U8 = mybir.dt.uint8
+FP8 = mybir.dt.float8_e4m3fn
+FP8X4 = mybir.dt.float8_e4m3fn_x4
+MULT = mybir.AluOpType.mult
+ADD = mybir.AluOpType.add
+SUB = mybir.AluOpType.subtract
+COPY = mybir.ActivationFunctionType.Copy
+
+P = 128
+PACK = 4
+CHUNKS = ((0, 256), (256, 256), (512, 512))
+NCH = len(CHUNKS)
+C_OF = (0, 0, 1, 1, 2, 2, 2, 2)
+PAIRS = B * H // 2
+WIDEN_ON_V = (0,)
+COPY_ON_V = (0, 1, 2, 3)
+COPY_BY_PE = ()
+WCOPY_ON_S = ()
+XCOPY_ON_V = ()
+QUADS = PAIRS // 2
+
+
+def tile_dpfpattention_pb_kernel(tc, x, wv, beta, vo, k_bytes, k_scale, W, out):
+    nc = tc.nc
+    with ExitStack() as ctx:
+        keep = ctx.enter_context(tc.tile_pool(name="keep", bufs=1))
+        work = ctx.enter_context(tc.tile_pool(name="work", bufs=4))
+        psx = ctx.enter_context(tc.psum_pool(name="psx", bufs=2))
+        psv = ctx.enter_context(tc.psum_pool(name="psv", bufs=3))
+        pso = ctx.enter_context(tc.psum_pool(name="pso", bufs=1))
+        psb = ctx.enter_context(tc.psum_pool(name="psb", bufs=1))
+
+        ident = keep.tile([P, P], F32, name="ident")
+        identb = keep.tile([P, P], BF16, name="identb")
+        brow = keep.tile([P, N], BF16, name="brow")
+        pick = keep.tile([P, B * H, 16], BF16, name="pick")
+        ksc = keep.tile([P, PACK], F32, name="ksc")
+        xc = [[keep.tile([P, 2, 2 * P], U32, align_bytes=64, name="xc%d%d" % (b, u)) for u in range(2)] for b in range(B)]
+        xs = [[keep.tile([P, 2, 2 * P], U8, align_bytes=64, name="xs%d%d" % (b, u)) for u in range(2)] for b in range(B)]
+        wc = [keep.tile([P, 2, n], U32, align_bytes=64, name="wc%d" % c0) for c0, n in CHUNKS]
+        ws = [keep.tile([P, 2, n], U8, align_bytes=64, name="ws%d" % c0) for c0, n in CHUNKS]
+        kc = [keep.tile([P, 4 * S], U32, align_bytes=64, name="kc%d" % i) for i in range(QUADS)]
+        ks = [keep.tile([P, 4 * S], U8, align_bytes=64, name="ks%d" % i) for i in range(QUADS)]
+        dc = [keep.tile([P, 4 * DH], U32, align_bytes=64, name="dc%d" % i) for i in range(QUADS)]
+        ds = [keep.tile([P, 4 * DH], U8, align_bytes=64, name="ds%d" % i) for i in range(QUADS)]
+        kb = [keep.tile([P, 4, PACK * S], U8, name="kb%d" % q) for q in range(8)]
+        vs = [keep.tile([P, 4, PACK, DH], BF16, name="vs%d" % q) for q in range(8)]
+        wt = [keep.tile([P, 8, DH], BF16, name="wt%d" % q) for q in range(4)]
+        ot = [keep.tile([P, 8, DH], F32, name="ot%d" % q) for q in range(4)]
+        xr = [[keep.tile([P, 2, D], BF16, name="xr%d%d" % (b, u)) for u in range(2)] for b in range(B)]
+        wr = [keep.tile([P, 2, PACK, n], BF16, name="wr%d" % c0) for c0, n in CHUNKS]
+        wg = [keep.tile([P, 2, n, PACK], BF16, align_bytes=64, name="wg%d" % c0) for c0, n in CHUNKS]
+        bp = [psb.tile([P, PACK, H * 16], BF16, name="bp%d" % b) for b in range(B)]
+
+        make_identity(nc, identb[:])
+        nc.gpsimd.memset(brow[:], 0.0)
+        make_identity(nc, ident[:])
+        nc.vector.tensor_copy(out=pick[:], in_=identb[:, 0 : B * H].unsqueeze(2).to_broadcast([P, B * H, 16]))
+
+        def load_k(q):
+            b, h0 = q // 4, 4 * (q % 4)
+            nc.sync.dma_start(
+                out=kb[q][:],
+                in_=k_bytes[b, h0 : h0 + 4].rearrange("h (p t) s -> p h (t s)", t=PACK),
+            )
+
+        def load_vo(q):
+            b, h0 = q // 4, 4 * (q % 4)
+            nc.sync.dma_start(
+                out=vs[q][:].rearrange("p h t d -> p h (t d)"),
+                in_=vo[b, h0 : h0 + 4].rearrange("h (p t) d -> p h (t d)", t=PACK),
+            )
+
+        def load_x(b, h):
+            nc.sync.dma_start(
+                out=xr[b][h][:],
+                in_=x[b].rearrange("(m t) k -> m t k", t=PACK)[:, 2 * h : 2 * h + 2, :],
+            )
+
+        def load_wv(c):
+            c0, n = CHUNKS[c]
+            for g in range(2):
+                nc.sync.dma_start(
+                    out=wr[c][:, g],
+                    in_=wv.rearrange("(g p j) w -> g p j w", g=2, j=PACK)[g][:, :, c0 : c0 + n],
+                )
+
+        def load_w(q):
+            b, h0 = q // 2, 8 * (q % 2)
+            nc.sync.dma_start(out=wt[q][:], in_=W[b, h0 : h0 + 8].rearrange("h s d -> s h d"))
+
+        nc.sync.dma_start(out=ksc[:], in_=k_scale.rearrange("a c (p t) e -> p (a c t e)", t=PACK))
+        load_k(0)
+        load_k(1)
+        load_x(0, 0)
+        load_x(0, 1)
+        load_wv(0)
+        nc.sync.dma_start(out=brow[0 : B * H, :], in_=beta.rearrange("b h n -> (b h) n"))
+        load_k(2)
+        load_vo(0)
+        load_wv(1)
+        load_vo(1)
+        load_k(3)
+        load_wv(2)
+        load_k(4)
+        load_vo(2)
+        load_x(1, 0)
+        load_k(5)
+        load_x(1, 1)
+        load_vo(3)
+        load_k(6)
+        load_w(0)
+        load_vo(4)
+        load_k(7)
+        load_vo(5)
+        load_w(1)
+        load_vo(6)
+        load_vo(7)
+        load_w(2)
+        load_w(3)
+
+        kw_t = {}
+        kg_t = {}
+
+        def widen(i):
+            kw = work.tile([P, 2, PACK, S], BF16, name="kw", bufs=8)
+            kw_t[i] = kw
+            for h in range(2):
+                src = kb[i // 2]
+                for t in range(PACK):
+                    sv = src[:, 2 * (i % 2) + h, S * t : S * (t + 1)].bitcast(FP8)
+                    if i in WIDEN_ON_V:
+                        nc.vector.tensor_scalar(
+                            out=kw[:, h, t, :], in0=sv, scalar1=ksc[:, t : t + 1], scalar2=None, op0=MULT
+                        )
+                    else:
+                        nc.scalar.activation(out=kw[:, h, t, :], in_=sv, func=COPY, scale=ksc[:, t : t + 1])
+
+        def kcopy(i):
+            if i // 2 not in kg_t:
+                kg_t[i // 2] = work.tile([P, 4, S, PACK], BF16, align_bytes=64, name="kg", bufs=6)
+            dst = kg_t[i // 2][:, 2 * (i % 2) : 2 * (i % 2) + 2]
+            if i in COPY_BY_PE:
+                nc.scalar.copy(out=dst, in_=kp_t[i][:])
+                return
+            dst = dst.rearrange("p h (c i) t -> p h c t i", i=4)
+            src = kw_t[i][:].rearrange("p h t (c i) -> p h c t i", i=4)
+            if i in COPY_ON_V:
+                nc.vector.tensor_copy(out=dst, in_=src)
+            else:
+                nc.scalar.copy(out=dst, in_=src)
+
+        kp_t = {}
+
+        def kturn(i):
+            kp = psx.tile([P, 2, S, PACK], BF16, name="xt")
+            kp_t[i] = kp
+            for h in range(2):
+                nc.tensor.matmul(
+                    kp[:, h], lhsT=identb[:], rhs=kw_t[i][:, h].rearrange("p t s -> p s t"), start=True, stop=True
+                )
+
+        def kquant(q, a=0, e=4):
+            nc.vector.quantize_mx(
+                out=kc[q][:, S * a : S * e].bitcast(FP8X4),
+                scales=ks[q][:, S * a : S * e],
+                in_=kg_t[q][:, a:e].rearrange("p h s t -> p (h s t)"),
+            )
+
+        xg_t = {}
+        xt_t = {}
+
+        def xtrans(b, h, g):
+            xt = psx.tile([P, 2, 2, P], F32, name="xt")
+            xt_t[(b, h, g)] = xt
+            for tt in range(2):
+                words = xr[b][h][:, tt, 512 * g : 512 * (g + 1)].bitcast(F32)
+                for u in range(2):
+                    nc.tensor.transpose(xt[:, tt, u, :], words[:, u::2], ident[:])
+
+        def xcopy(b, h, g):
+            if g == 0:
+                xg_t[(b, h)] = work.tile([P, N * PACK], BF16, align_bytes=64, name="xg", bufs=2)
+            copy = nc.vector.tensor_copy if (b, h, g) in XCOPY_ON_V else nc.scalar.copy
+            copy(
+                out=xg_t[(b, h)][:, 1024 * g : 1024 * (g + 1)]
+                .bitcast(F32)
+                .rearrange("p (t m u) -> p t m u", t=2, u=2),
+                in_=xt_t[(b, h, g)][:].rearrange("p t u m -> p t m u"),
+            )
+
+        def xquant(b, h):
+            nc.vector.quantize_mx(
+                out=xc[b][h][:].rearrange("p g n -> p (g n)").bitcast(FP8X4),
+                scales=xs[b][h][:].rearrange("p g n -> p (g n)"),
+                in_=xg_t[(b, h)][:],
+            )
+
+        def wcopy(c, g):
+            dst = wg[c][:, g].rearrange("p (c i) j -> p c j i", i=4)
+            src = wr[c][:, g].rearrange("p j (c i) -> p c j i", i=4)
+            if (c, g) in WCOPY_ON_S:
+                nc.scalar.copy(out=dst, in_=src)
+            else:
+                nc.vector.tensor_copy(out=dst, in_=src)
+
+        def wquant(c):
+            nc.vector.quantize_mx(
+                out=wc[c][:].rearrange("p g w -> p (g w)").bitcast(FP8X4),
+                scales=ws[c][:].rearrange("p g w -> p (g w)"),
+                in_=wg[c][:].rearrange("p g w j -> p (g w j)"),
+            )
+
+        v_t = {}
+
+        def mm1(i):
+            b, j = i // 8, i % 8
+            c = C_OF[j]
+            o = 128 * j - CHUNKS[c][0]
+            v = psv.tile([P, PACK, P], F32, name="v")
+            v_t[i] = v
+            for t in range(PACK):
+                for g in range(2):
+                    nc.tensor.matmul_mx(
+                        out=v[:, t, :],
+                        lhsT=xc[b][t // 2][:, g, P * (t % 2) : P * (t % 2 + 1)].bitcast(FP8X4),
+                        lhsT_scale=xs[b][t // 2][:, g, P * (t % 2) : P * (t % 2 + 1)],
+                        rhs=wc[c][:, g, o : o + P].bitcast(FP8X4),
+                        rhs_scale=ws[c][:, g, o : o + P],
+                        start=(g == 0),
+                        stop=(g == 1),
+                    )
+
+        tm_t = {}
+        dg_t = {}
+
+        def pass1(i):
+            if i % 2 == 0:
+                tm_t[i // 2] = work.tile([P, PACK, 4 * DH], F32, name="tm", bufs=4)
+            h0 = 2 * (i % 2)
+            nc.vector.tensor_tensor(
+                out=tm_t[i // 2][:, :, DH * h0 : DH * (h0 + 2)].rearrange("p t (h d) -> p t h d", h=2),
+                in0=v_t[i][:].rearrange("p t (h d) -> p t h d", h=2),
+                in1=vs[i // 2][:, h0 : h0 + 2].rearrange("p h t d -> p t h d"),
+                op=SUB,
+            )
+
+        def pass2(q, a=0, e=4):
+            if a == 0:
+                dg_t[q] = work.tile([P, 4, DH, PACK], BF16, align_bytes=64, name="dg", bufs=4)
+            n = (e - a) * 16
+            nc.vector.tensor_tensor(
+                out=dg_t[q][:, a:e].rearrange("p h (c i) t -> p (h c) t i", i=4),
+                in0=tm_t[q][:, :, DH * a : DH * e].rearrange("p t (c i) -> p c t i", i=4),
+                in1=bp[q // 4][:, :, 16 * (4 * (q % 4) + a) : 16 * (4 * (q % 4) + e)]
+                .rearrange("p t c -> p c t")
+                .unsqueeze(3)
+                .to_broadcast([P, n, PACK, 4]),
+                op=MULT,
+            )
+
+        def dquant(q, a=0, e=4):
+            nc.vector.quantize_mx(
+                out=dc[q][:, DH * a : DH * e].bitcast(FP8X4),
+                scales=ds[q][:, DH * a : DH * e],
+                in_=dg_t[q][:, a:e].rearrange("p h d t -> p (h d t)"),
+            )
+
+        o_t = {}
+
+        def mm2(q, a=0, e=4):
+            if q % 2 == 0 and a == 0:
+                o_t[q // 2] = pso.tile([P, 8, DH], F32, name="o")
+            for h in range(a, e):
+                nc.tensor.matmul_mx(
+                    out=o_t[q // 2][:, 4 * (q % 2) + h, :],
+                    lhsT=kc[q][:, S * h : S * (h + 1)].bitcast(FP8X4),
+                    lhsT_scale=ks[q][:, S * h : S * (h + 1)],
+                    rhs=dc[q][:, DH * h : DH * (h + 1)].bitcast(FP8X4),
+                    rhs_scale=ds[q][:, DH * h : DH * (h + 1)],
+                    start=True,
+                    stop=True,
+                )
+
+        def finish(q, a, e):
+            nc.vector.tensor_tensor(out=ot[q][:, a:e, :], in0=o_t[q][:, a:e, :], in1=wt[q][:, a:e, :], op=ADD)
+            b, h0 = q // 2, 8 * (q % 2)
+            nc.sync.dma_start(
+                out=out[b, h0 + a : h0 + e].rearrange("h s d -> s h d"), in_=ot[q][:, a:e, :]
+            )
+
+        def bload(b):
+            for t in range(PACK):
+                nc.tensor.matmul(
+                    bp[b][:, t],
+                    lhsT=brow[:, t::PACK],
+                    rhs=pick[:, H * b : H * (b + 1)].rearrange("p h c -> p (h c)"),
+                    start=True,
+                    stop=True,
+                )
+
+        widen(0)
+        widen(1)
+        kcopy(0)
+        widen(2)
+        kcopy(1)
+        widen(3)
+        kquant(0)
+        kcopy(2)
+        kcopy(3)
+        xtrans(0, 0, 0)
+        xtrans(0, 0, 1)
+        xcopy(0, 0, 0)
+        xcopy(0, 0, 1)
+        kquant(1)
+        wcopy(0, 0)
+        xtrans(0, 1, 0)
+        xtrans(0, 1, 1)
+        xcopy(0, 1, 0)
+        xcopy(0, 1, 1)
+        wcopy(0, 1)
+        xquant(0, 0)
+        wquant(0)
+        bload(0)
+        xquant(0, 1)
+        mm1(0)
+        mm1(1)
+        widen(4)
+        wcopy(1, 0)
+        widen(5)
+        wcopy(1, 1)
+        for q in range(QUADS):
+            last = q == QUADS - 1
+            if q == 2:
+                bload(1)
+                xcopy(1, 0, 0)
+                xcopy(1, 0, 1)
+            for i in (2 * q + 4, 2 * q + 5):
+                if i in COPY_BY_PE:
+                    kturn(i)
+                if i + 2 < PAIRS:
+                    widen(i + 2)
+                if i < PAIRS and i not in COPY_ON_V:
+                    kcopy(i)
+            pass1(2 * q)
+            if q == 0:
+                wquant(1)
+                wcopy(2, 0)
+            if q == 3:
+                xquant(1, 1)
+            if not last:
+                mm1(2 * q + 2)
+            pass1(2 * q + 1)
+            if q == 0:
+                wcopy(2, 1)
+            if not last:
+                mm1(2 * q + 3)
+            if q in (1, 2):
+                xtrans(1, q - 1, 0)
+                xtrans(1, q - 1, 1)
+            if q == 2:
+                xcopy(1, 1, 0)
+                xcopy(1, 1, 1)
+            for i in (2 * q + 2, 2 * q + 3):
+                if q > 0 and i in COPY_ON_V:
+                    kcopy(i)
+            if q % 2 == 0 and q > 0:
+                finish(q // 2 - 1, 0, 8)
+            if last:
+                pass2(q, 0, 2)
+                kquant(q)
+                pass2(q, 2, 4)
+                finish(3, 0, 4)
+                dquant(q, 0, 2)
+                dquant(q, 2, 4)
+                mm2(q, 0, 2)
+                mm2(q, 2, 4)
+                finish(3, 4, 6)
+                finish(3, 6, 8)
+            else:
+                pass2(q)
+                if q == 2:
+                    xquant(1, 0)
+                if q == 0:
+                    wquant(2)
+                if q >= 2:
+                    kquant(q)
+                dquant(q)
+                mm2(q)

@@ -20,16 +20,14 @@ COPY = mybir.ActivationFunctionType.Copy
 
 P = 128
 PACK = 4
-CHUNKS = ((0, 256), (256, 256), (512, 512))
-NCH = len(CHUNKS)
-C_OF = (0, 0, 1, 1, 2, 2, 2, 2)
-PAIRS = B * H // 2
-WIDEN_ON_V = (0,)
-COPY_ON_V = (0, 1, 2, 3)
-COPY_BY_PE = ()
-WCOPY_ON_S = ()
-XCOPY_ON_V = ()
-QUADS = PAIRS // 2
+QUADS = B * H // 4
+QW = 4 * DH
+REP = DH // 4
+
+
+def batch_and_chunk(q):
+    o = q // 2
+    return o % 2, 2 * (o // 2) + q % 2
 
 
 def tile_dpfpattention_pb_kernel(tc, x, wv, beta, vo, k_bytes, k_scale, W, out):
@@ -38,183 +36,144 @@ def tile_dpfpattention_pb_kernel(tc, x, wv, beta, vo, k_bytes, k_scale, W, out):
         keep = ctx.enter_context(tc.tile_pool(name="keep", bufs=1))
         work = ctx.enter_context(tc.tile_pool(name="work", bufs=4))
         psx = ctx.enter_context(tc.psum_pool(name="psx", bufs=2))
-        psv = ctx.enter_context(tc.psum_pool(name="psv", bufs=3))
+        psv = ctx.enter_context(tc.psum_pool(name="psv", bufs=4))
         pso = ctx.enter_context(tc.psum_pool(name="pso", bufs=1))
         psb = ctx.enter_context(tc.psum_pool(name="psb", bufs=1))
+        ctx.enter_context(tc.manual_schedule())
 
         ident = keep.tile([P, P], F32, name="ident")
         identb = keep.tile([P, P], BF16, name="identb")
         brow = keep.tile([P, N], BF16, name="brow")
-        pick = keep.tile([P, B * H, 16], BF16, name="pick")
+        pick = keep.tile([P, B * H, REP], BF16, name="pick")
         ksc = keep.tile([P, PACK], F32, name="ksc")
         xc = [[keep.tile([P, 2, 2 * P], U32, align_bytes=64, name="xc%d%d" % (b, u)) for u in range(2)] for b in range(B)]
         xs = [[keep.tile([P, 2, 2 * P], U8, align_bytes=64, name="xs%d%d" % (b, u)) for u in range(2)] for b in range(B)]
-        wc = [keep.tile([P, 2, n], U32, align_bytes=64, name="wc%d" % c0) for c0, n in CHUNKS]
-        ws = [keep.tile([P, 2, n], U8, align_bytes=64, name="ws%d" % c0) for c0, n in CHUNKS]
-        kc = [keep.tile([P, 4 * S], U32, align_bytes=64, name="kc%d" % i) for i in range(QUADS)]
-        ks = [keep.tile([P, 4 * S], U8, align_bytes=64, name="ks%d" % i) for i in range(QUADS)]
-        dc = [keep.tile([P, 4 * DH], U32, align_bytes=64, name="dc%d" % i) for i in range(QUADS)]
-        ds = [keep.tile([P, 4 * DH], U8, align_bytes=64, name="ds%d" % i) for i in range(QUADS)]
-        kb = [keep.tile([P, 4, PACK * S], U8, name="kb%d" % q) for q in range(8)]
-        vs = [keep.tile([P, 4, PACK, DH], BF16, name="vs%d" % q) for q in range(8)]
-        wt = [keep.tile([P, 8, DH], BF16, name="wt%d" % q) for q in range(4)]
-        ot = [keep.tile([P, 8, DH], F32, name="ot%d" % q) for q in range(4)]
+        wc = [keep.tile([P, 2, QW], U32, align_bytes=64, name="wc%d" % c) for c in range(4)]
+        ws = [keep.tile([P, 2, QW], U8, align_bytes=64, name="ws%d" % c) for c in range(4)]
+        kc = [keep.tile([P, 2 * S], U32, align_bytes=64, name="kc%d" % i) for i in range(2 * QUADS)]
+        ks = [keep.tile([P, 2 * S], U8, align_bytes=64, name="ks%d" % i) for i in range(2 * QUADS)]
+        dc = [keep.tile([P, QW], U32, align_bytes=64, name="dc%d" % q) for q in range(QUADS)]
+        ds = [keep.tile([P, QW], U8, align_bytes=64, name="ds%d" % q) for q in range(QUADS)]
+        kb = [keep.tile([P, 4, PACK * S], U8, name="kb%d" % q) for q in range(QUADS)]
+        vs = [keep.tile([P, 4, PACK, DH], BF16, name="vs%d" % q) for q in range(QUADS)]
+        wt = [keep.tile([P, 8, DH], BF16, name="wt%d" % o) for o in range(QUADS // 2)]
+        ot = [keep.tile([P, 8, DH], F32, name="ot%d" % o) for o in range(QUADS // 2)]
         xr = [[keep.tile([P, 2, D], BF16, name="xr%d%d" % (b, u)) for u in range(2)] for b in range(B)]
-        wr = [keep.tile([P, 2, PACK, n], BF16, name="wr%d" % c0) for c0, n in CHUNKS]
-        wg = [keep.tile([P, 2, n, PACK], BF16, align_bytes=64, name="wg%d" % c0) for c0, n in CHUNKS]
-        bp = [psb.tile([P, PACK, H * 16], BF16, name="bp%d" % b) for b in range(B)]
+        wr = [[keep.tile([P, PACK, QW], BF16, name="wr%d%d" % (c, g)) for g in range(2)] for c in range(4)]
+        wg = [keep.tile([P, 2, QW, PACK], BF16, align_bytes=64, name="wg%d" % c) for c in range(4)]
 
-        make_identity(nc, identb[:])
-        nc.gpsimd.memset(brow[:], 0.0)
-        make_identity(nc, ident[:])
-        nc.vector.tensor_copy(out=pick[:], in_=identb[:, 0 : B * H].unsqueeze(2).to_broadcast([P, B * H, 16]))
+        def load_scale():
+            nc.sync.dma_start(out=ksc[:], in_=k_scale.rearrange("a c (p t) e -> p (a c t e)", t=PACK))
+
+        def load_beta():
+            nc.sync.dma_start(out=brow[0 : B * H, :], in_=beta.rearrange("b h n -> (b h) n"))
 
         def load_k(q):
-            b, h0 = q // 4, 4 * (q % 4)
+            b, c = batch_and_chunk(q)
+            h0 = 4 * c
             nc.sync.dma_start(
-                out=kb[q][:],
-                in_=k_bytes[b, h0 : h0 + 4].rearrange("h (p t) s -> p h (t s)", t=PACK),
+                out=kb[q][:], in_=k_bytes[b, h0 : h0 + 4].rearrange("h (p t) s -> p h (t s)", t=PACK)
             )
 
         def load_vo(q):
-            b, h0 = q // 4, 4 * (q % 4)
+            b, c = batch_and_chunk(q)
+            h0 = 4 * c
             nc.sync.dma_start(
                 out=vs[q][:].rearrange("p h t d -> p h (t d)"),
                 in_=vo[b, h0 : h0 + 4].rearrange("h (p t) d -> p h (t d)", t=PACK),
             )
 
-        def load_x(b, h):
+        def load_x(b, u):
             nc.sync.dma_start(
-                out=xr[b][h][:],
-                in_=x[b].rearrange("(m t) k -> m t k", t=PACK)[:, 2 * h : 2 * h + 2, :],
+                out=xr[b][u][:], in_=x[b].rearrange("(m t) k -> m t k", t=PACK)[:, 2 * u : 2 * u + 2, :]
             )
 
-        def load_wv(c):
-            c0, n = CHUNKS[c]
-            for g in range(2):
-                nc.sync.dma_start(
-                    out=wr[c][:, g],
-                    in_=wv.rearrange("(g p j) w -> g p j w", g=2, j=PACK)[g][:, :, c0 : c0 + n],
-                )
+        def load_wv(c, g):
+            nc.sync.dma_start(
+                out=wr[c][g][:],
+                in_=wv.rearrange("(g p j) w -> g p j w", g=2, j=PACK)[g][:, :, QW * c : QW * (c + 1)],
+            )
 
-        def load_w(q):
-            b, h0 = q // 2, 8 * (q % 2)
-            nc.sync.dma_start(out=wt[q][:], in_=W[b, h0 : h0 + 8].rearrange("h s d -> s h d"))
+        def load_w(o):
+            b, h0 = o % 2, 8 * (o // 2)
+            nc.sync.dma_start(out=wt[o][:], in_=W[b, h0 : h0 + 8].rearrange("h s d -> s h d"))
 
-        nc.sync.dma_start(out=ksc[:], in_=k_scale.rearrange("a c (p t) e -> p (a c t e)", t=PACK))
-        load_k(0)
-        load_k(1)
-        load_x(0, 0)
-        load_x(0, 1)
-        load_wv(0)
-        nc.sync.dma_start(out=brow[0 : B * H, :], in_=beta.rearrange("b h n -> (b h) n"))
-        load_k(2)
-        load_vo(0)
-        load_wv(1)
-        load_vo(1)
-        load_k(3)
-        load_wv(2)
-        load_k(4)
-        load_vo(2)
-        load_x(1, 0)
-        load_k(5)
-        load_x(1, 1)
-        load_vo(3)
-        load_k(6)
-        load_w(0)
-        load_vo(4)
-        load_k(7)
-        load_vo(5)
-        load_w(1)
-        load_vo(6)
-        load_vo(7)
-        load_w(2)
-        load_w(3)
+        def constants():
+            make_identity(nc, identb[:])
+            make_identity(nc, ident[:])
+            nc.vector.memset(brow[32:64, :], 0.0)
+            nc.vector.memset(brow[64:128, :], 0.0)
+            nc.scalar.activation(
+                out=pick[:], in_=identb[:, 0 : B * H].unsqueeze(2).to_broadcast([P, B * H, REP]), func=COPY
+            )
 
         kw_t = {}
         kg_t = {}
 
-        def widen(i):
-            kw = work.tile([P, 2, PACK, S], BF16, name="kw", bufs=8)
+        def widen(i, engine):
+            kw = work.tile([P, PACK, 2, S], BF16, name="kw", bufs=6)
             kw_t[i] = kw
             for h in range(2):
-                src = kb[i // 2]
                 for t in range(PACK):
-                    sv = src[:, 2 * (i % 2) + h, S * t : S * (t + 1)].bitcast(FP8)
-                    if i in WIDEN_ON_V:
+                    codes = kb[i // 2][:, 2 * (i % 2) + h, S * t : S * (t + 1)].bitcast(FP8)
+                    if engine == "V":
                         nc.vector.tensor_scalar(
-                            out=kw[:, h, t, :], in0=sv, scalar1=ksc[:, t : t + 1], scalar2=None, op0=MULT
+                            out=kw[:, t, h, :], in0=codes, scalar1=ksc[:, t : t + 1], scalar2=None, op0=MULT
                         )
                     else:
-                        nc.scalar.activation(out=kw[:, h, t, :], in_=sv, func=COPY, scale=ksc[:, t : t + 1])
+                        nc.scalar.activation(out=kw[:, t, h, :], in_=codes, func=COPY, scale=ksc[:, t : t + 1])
 
-        def kcopy(i):
-            if i // 2 not in kg_t:
-                kg_t[i // 2] = work.tile([P, 4, S, PACK], BF16, align_bytes=64, name="kg", bufs=6)
-            dst = kg_t[i // 2][:, 2 * (i % 2) : 2 * (i % 2) + 2]
-            if i in COPY_BY_PE:
-                nc.scalar.copy(out=dst, in_=kp_t[i][:])
-                return
-            dst = dst.rearrange("p h (c i) t -> p h c t i", i=4)
-            src = kw_t[i][:].rearrange("p h t (c i) -> p h c t i", i=4)
-            if i in COPY_ON_V:
-                nc.vector.tensor_copy(out=dst, in_=src)
-            else:
-                nc.scalar.copy(out=dst, in_=src)
-
-        kp_t = {}
-
-        def kturn(i):
-            kp = psx.tile([P, 2, S, PACK], BF16, name="xt")
-            kp_t[i] = kp
-            for h in range(2):
-                nc.tensor.matmul(
-                    kp[:, h], lhsT=identb[:], rhs=kw_t[i][:, h].rearrange("p t s -> p s t"), start=True, stop=True
+        def interleave(engine, dst, src):
+            if engine == "G":
+                nc.gpsimd.tensor_scalar(
+                    out=dst, in0=src.rearrange("p t n -> p n t"), scalar1=1.0, scalar2=0.0, op0=MULT, op1=ADD
                 )
+                return
+            copy = nc.vector.tensor_copy if engine == "V" else nc.scalar.copy
+            copy(out=dst.rearrange("p (c i) t -> p c t i", i=4), in_=src.rearrange("p t (c i) -> p c t i", i=4))
 
-        def kquant(q, a=0, e=4):
+        def kcopy(i, engine):
+            if i % 2 == 1:
+                kg_t[i] = work.tile([P, 2 * S, PACK], BF16, align_bytes=64, name="kg_odd", bufs=1)
+            else:
+                kg_t[i] = work.tile([P, 2 * S, PACK], BF16, align_bytes=64, name="kg_even", bufs=3)
+            interleave(engine, kg_t[i][:], kw_t[i][:].rearrange("p t h s -> p t (h s)"))
+
+        def kquant(i):
             nc.vector.quantize_mx(
-                out=kc[q][:, S * a : S * e].bitcast(FP8X4),
-                scales=ks[q][:, S * a : S * e],
-                in_=kg_t[q][:, a:e].rearrange("p h s t -> p (h s t)"),
+                out=kc[i][:].bitcast(FP8X4), scales=ks[i][:], in_=kg_t[i][:].rearrange("p n t -> p (n t)")
             )
 
         xg_t = {}
         xt_t = {}
 
-        def xtrans(b, h, g):
+        def xtrans(b, u, g):
             xt = psx.tile([P, 2, 2, P], F32, name="xt")
-            xt_t[(b, h, g)] = xt
+            xt_t[(b, u, g)] = xt
             for tt in range(2):
-                words = xr[b][h][:, tt, 512 * g : 512 * (g + 1)].bitcast(F32)
-                for u in range(2):
-                    nc.tensor.transpose(xt[:, tt, u, :], words[:, u::2], ident[:])
+                words = xr[b][u][:, tt, 512 * g : 512 * (g + 1)].bitcast(F32)
+                for e in range(2):
+                    nc.tensor.transpose(xt[:, tt, e, :], words[:, e::2], ident[:])
 
-        def xcopy(b, h, g):
+        def xcopy(b, u, g):
             if g == 0:
-                xg_t[(b, h)] = work.tile([P, N * PACK], BF16, align_bytes=64, name="xg", bufs=2)
-            copy = nc.vector.tensor_copy if (b, h, g) in XCOPY_ON_V else nc.scalar.copy
-            copy(
-                out=xg_t[(b, h)][:, 1024 * g : 1024 * (g + 1)]
+                xg_t[(b, u)] = work.tile([P, N * PACK], BF16, align_bytes=64, name="xg", bufs=2)
+            nc.scalar.copy(
+                out=xg_t[(b, u)][:, 1024 * g : 1024 * (g + 1)]
                 .bitcast(F32)
-                .rearrange("p (t m u) -> p t m u", t=2, u=2),
-                in_=xt_t[(b, h, g)][:].rearrange("p t u m -> p t m u"),
+                .rearrange("p (t m e) -> p t m e", t=2, e=2),
+                in_=xt_t[(b, u, g)][:].rearrange("p t e m -> p t m e"),
             )
 
-        def xquant(b, h):
+        def xquant(b, u):
             nc.vector.quantize_mx(
-                out=xc[b][h][:].rearrange("p g n -> p (g n)").bitcast(FP8X4),
-                scales=xs[b][h][:].rearrange("p g n -> p (g n)"),
-                in_=xg_t[(b, h)][:],
+                out=xc[b][u][:].rearrange("p g n -> p (g n)").bitcast(FP8X4),
+                scales=xs[b][u][:].rearrange("p g n -> p (g n)"),
+                in_=xg_t[(b, u)][:],
             )
 
-        def wcopy(c, g):
-            dst = wg[c][:, g].rearrange("p (c i) j -> p c j i", i=4)
-            src = wr[c][:, g].rearrange("p j (c i) -> p c j i", i=4)
-            if (c, g) in WCOPY_ON_S:
-                nc.scalar.copy(out=dst, in_=src)
-            else:
-                nc.vector.tensor_copy(out=dst, in_=src)
+        def wcopy(c, g, engine):
+            interleave(engine, wg[c][:, g], wr[c][g][:])
 
         def wquant(c):
             nc.vector.quantize_mx(
@@ -223,22 +182,35 @@ def tile_dpfpattention_pb_kernel(tc, x, wv, beta, vo, k_bytes, k_scale, W, out):
                 in_=wg[c][:].rearrange("p g w j -> p (g w j)"),
             )
 
+        bp_t = {}
+
+        def bspread(b):
+            pool = psb if b == 0 else psx
+            bp = pool.tile([P, PACK, H * REP], BF16, name="bp" if b == 0 else "xt")
+            bp_t[b] = bp
+            for t in range(PACK):
+                nc.tensor.matmul(
+                    bp[:, t],
+                    lhsT=brow[:, t::PACK],
+                    rhs=pick[:, H * b : H * (b + 1)].rearrange("p h c -> p (h c)"),
+                    start=True,
+                    stop=True,
+                )
+
         v_t = {}
 
-        def mm1(i):
-            b, j = i // 8, i % 8
-            c = C_OF[j]
-            o = 128 * j - CHUNKS[c][0]
-            v = psv.tile([P, PACK, P], F32, name="v")
-            v_t[i] = v
-            for t in range(PACK):
+        def mm1(q, u):
+            b, c = batch_and_chunk(q)
+            v = psv.tile([P, 2, QW], F32, name="v")
+            v_t[(q, u)] = v
+            for tt in range(2):
                 for g in range(2):
                     nc.tensor.matmul_mx(
-                        out=v[:, t, :],
-                        lhsT=xc[b][t // 2][:, g, P * (t % 2) : P * (t % 2 + 1)].bitcast(FP8X4),
-                        lhsT_scale=xs[b][t // 2][:, g, P * (t % 2) : P * (t % 2 + 1)],
-                        rhs=wc[c][:, g, o : o + P].bitcast(FP8X4),
-                        rhs_scale=ws[c][:, g, o : o + P],
+                        out=v[:, tt, :],
+                        lhsT=xc[b][u][:, g, P * tt : P * (tt + 1)].bitcast(FP8X4),
+                        lhsT_scale=xs[b][u][:, g, P * tt : P * (tt + 1)],
+                        rhs=wc[c][:, g, :].bitcast(FP8X4),
+                        rhs_scale=ws[c][:, g, :],
                         start=(g == 0),
                         stop=(g == 1),
                     )
@@ -246,28 +218,28 @@ def tile_dpfpattention_pb_kernel(tc, x, wv, beta, vo, k_bytes, k_scale, W, out):
         tm_t = {}
         dg_t = {}
 
-        def pass1(i):
-            if i % 2 == 0:
-                tm_t[i // 2] = work.tile([P, PACK, 4 * DH], F32, name="tm", bufs=4)
-            h0 = 2 * (i % 2)
+        def subtract(q, u):
+            if u == 0:
+                tm_t[q] = work.tile([P, PACK, QW], F32, name="tm", bufs=3)
             nc.vector.tensor_tensor(
-                out=tm_t[i // 2][:, :, DH * h0 : DH * (h0 + 2)].rearrange("p t (h d) -> p t h d", h=2),
-                in0=v_t[i][:].rearrange("p t (h d) -> p t h d", h=2),
-                in1=vs[i // 2][:, h0 : h0 + 2].rearrange("p h t d -> p t h d"),
+                out=tm_t[q][:, 2 * u : 2 * u + 2, :].rearrange("p t (h d) -> p t h d", h=4),
+                in0=v_t[(q, u)][:].rearrange("p t (h d) -> p t h d", h=4),
+                in1=vs[q][:, :, 2 * u : 2 * u + 2, :].rearrange("p h t d -> p t h d"),
                 op=SUB,
             )
 
-        def pass2(q, a=0, e=4):
-            if a == 0:
-                dg_t[q] = work.tile([P, 4, DH, PACK], BF16, align_bytes=64, name="dg", bufs=4)
-            n = (e - a) * 16
+        def weigh(q, a=0, e=4):
+            if q not in dg_t:
+                dg_t[q] = work.tile([P, 4, DH, PACK], BF16, align_bytes=64, name="dg", bufs=3)
+            b, c = batch_and_chunk(q)
+            h0 = 4 * c
             nc.vector.tensor_tensor(
                 out=dg_t[q][:, a:e].rearrange("p h (c i) t -> p (h c) t i", i=4),
                 in0=tm_t[q][:, :, DH * a : DH * e].rearrange("p t (c i) -> p c t i", i=4),
-                in1=bp[q // 4][:, :, 16 * (4 * (q % 4) + a) : 16 * (4 * (q % 4) + e)]
+                in1=bp_t[b][:, :, REP * (h0 + a) : REP * (h0 + e)]
                 .rearrange("p t c -> p c t")
                 .unsqueeze(3)
-                .to_broadcast([P, n, PACK, 4]),
+                .to_broadcast([P, (e - a) * REP, PACK, 4]),
                 op=MULT,
             )
 
@@ -284,118 +256,140 @@ def tile_dpfpattention_pb_kernel(tc, x, wv, beta, vo, k_bytes, k_scale, W, out):
             if q % 2 == 0 and a == 0:
                 o_t[q // 2] = pso.tile([P, 8, DH], F32, name="o")
             for h in range(a, e):
+                i, hh = 2 * q + h // 2, h % 2
                 nc.tensor.matmul_mx(
                     out=o_t[q // 2][:, 4 * (q % 2) + h, :],
-                    lhsT=kc[q][:, S * h : S * (h + 1)].bitcast(FP8X4),
-                    lhsT_scale=ks[q][:, S * h : S * (h + 1)],
+                    lhsT=kc[i][:, S * hh : S * (hh + 1)].bitcast(FP8X4),
+                    lhsT_scale=ks[i][:, S * hh : S * (hh + 1)],
                     rhs=dc[q][:, DH * h : DH * (h + 1)].bitcast(FP8X4),
                     rhs_scale=ds[q][:, DH * h : DH * (h + 1)],
                     start=True,
                     stop=True,
                 )
 
-        def finish(q, a, e):
-            nc.vector.tensor_tensor(out=ot[q][:, a:e, :], in0=o_t[q][:, a:e, :], in1=wt[q][:, a:e, :], op=ADD)
-            b, h0 = q // 2, 8 * (q % 2)
-            nc.sync.dma_start(
-                out=out[b, h0 + a : h0 + e].rearrange("h s d -> s h d"), in_=ot[q][:, a:e, :]
-            )
+        def finish(o, a=0, e=8):
+            nc.vector.tensor_tensor(out=ot[o][:, a:e, :], in0=o_t[o][:, a:e, :], in1=wt[o][:, a:e, :], op=ADD)
+            b, h0 = o % 2, 8 * (o // 2)
+            nc.sync.dma_start(out=out[b, h0 + a : h0 + e].rearrange("h s d -> s h d"), in_=ot[o][:, a:e, :])
 
-        def bload(b):
-            for t in range(PACK):
-                nc.tensor.matmul(
-                    bp[b][:, t],
-                    lhsT=brow[:, t::PACK],
-                    rhs=pick[:, H * b : H * (b + 1)].rearrange("p h c -> p (h c)"),
-                    start=True,
-                    stop=True,
-                )
+        constants()
+        load_scale()
+        load_k(0)
+        load_x(0, 0)
+        load_wv(0, 0)
+        load_wv(0, 1)
+        load_k(1)
+        load_x(0, 1)
+        load_wv(1, 0)
+        load_vo(0)
+        load_wv(1, 1)
+        load_beta()
+        load_k(2)
+        load_x(1, 0)
+        load_vo(1)
+        load_x(1, 1)
+        load_vo(2)
+        load_k(3)
+        load_wv(2, 0)
+        load_wv(2, 1)
+        load_vo(3)
+        load_w(0)
+        load_k(4)
+        load_wv(3, 0)
+        load_wv(3, 1)
+        load_vo(4)
+        for q in range(5, QUADS):
+            load_k(q)
+            load_vo(q)
+            load_w(q - 4)
 
-        widen(0)
-        widen(1)
-        kcopy(0)
-        widen(2)
-        kcopy(1)
-        widen(3)
-        kquant(0)
-        kcopy(2)
-        kcopy(3)
+        widen(0, "V")
+        widen(1, "S")
+        kcopy(0, "V")
         xtrans(0, 0, 0)
         xtrans(0, 0, 1)
         xcopy(0, 0, 0)
         xcopy(0, 0, 1)
-        kquant(1)
-        wcopy(0, 0)
+        kcopy(1, "V")
+        wcopy(0, 0, "V")
+        kquant(0)
+        wcopy(0, 1, "V")
+        xquant(0, 0)
+        wquant(0)
+        widen(2, "S")
         xtrans(0, 1, 0)
         xtrans(0, 1, 1)
         xcopy(0, 1, 0)
         xcopy(0, 1, 1)
-        wcopy(0, 1)
-        xquant(0, 0)
-        wquant(0)
-        bload(0)
+        mm1(0, 0)
+        widen(3, "S")
+        kcopy(2, "V")
+        wcopy(1, 0, "V")
         xquant(0, 1)
-        mm1(0)
-        mm1(1)
-        widen(4)
-        wcopy(1, 0)
-        widen(5)
-        wcopy(1, 1)
-        for q in range(QUADS):
-            last = q == QUADS - 1
-            if q == 2:
-                bload(1)
-                xcopy(1, 0, 0)
-                xcopy(1, 0, 1)
-            for i in (2 * q + 4, 2 * q + 5):
-                if i in COPY_BY_PE:
-                    kturn(i)
-                if i + 2 < PAIRS:
-                    widen(i + 2)
-                if i < PAIRS and i not in COPY_ON_V:
-                    kcopy(i)
-            pass1(2 * q)
-            if q == 0:
-                wquant(1)
-                wcopy(2, 0)
-            if q == 3:
-                xquant(1, 1)
-            if not last:
-                mm1(2 * q + 2)
-            pass1(2 * q + 1)
-            if q == 0:
-                wcopy(2, 1)
-            if not last:
-                mm1(2 * q + 3)
-            if q in (1, 2):
-                xtrans(1, q - 1, 0)
-                xtrans(1, q - 1, 1)
-            if q == 2:
+        mm1(0, 1)
+        bspread(0)
+        kquant(2)
+        subtract(0, 0)
+        wcopy(1, 1, "V")
+        subtract(0, 1)
+        widen(5, "S")
+        widen(4, "S")
+        xtrans(1, 0, 0)
+        xtrans(1, 0, 1)
+        xcopy(1, 0, 0)
+        xcopy(1, 0, 1)
+        wquant(1)
+        mm1(1, 0)
+        mm1(1, 1)
+        kquant(1)
+        for q in range(1, QUADS):
+            kcopy(2 * q + 1, "G")
+            if q == 1:
+                kcopy(4, "S")
+                xtrans(1, 1, 0)
+                xtrans(1, 1, 1)
                 xcopy(1, 1, 0)
                 xcopy(1, 1, 1)
-            for i in (2 * q + 2, 2 * q + 3):
-                if q > 0 and i in COPY_ON_V:
-                    kcopy(i)
-            if q % 2 == 0 and q > 0:
-                finish(q // 2 - 1, 0, 8)
-            if last:
-                pass2(q, 0, 2)
-                kquant(q)
-                pass2(q, 2, 4)
-                finish(3, 0, 4)
-                dquant(q, 0, 2)
-                dquant(q, 2, 4)
-                mm2(q, 0, 2)
-                mm2(q, 2, 4)
-                finish(3, 4, 6)
-                finish(3, 6, 8)
-            else:
-                pass2(q)
-                if q == 2:
-                    xquant(1, 0)
-                if q == 0:
-                    wquant(2)
-                if q >= 2:
-                    kquant(q)
-                dquant(q)
-                mm2(q)
+                bspread(1)
+            if q == 1:
+                widen(7, "S")
+            if 4 <= q < QUADS - 1:
+                widen(2 * q + 3, "S")
+            if q in (2, 3):
+                wcopy(q, 0, "S")
+                wcopy(q, 1, "S")
+            if q >= 3:
+                kcopy(2 * q, "S")
+            if 2 <= q < QUADS - 1:
+                widen(2 * q + 2, "S")
+            if q == 2:
+                widen(9, "S")
+            weigh(q - 1)
+            subtract(q, 0)
+            subtract(q, 1)
+            if q >= 3 and q % 2 == 1:
+                finish(q // 2 - 1)
+            if q == 1:
+                xquant(1, 0)
+                xquant(1, 1)
+            if q in (3, 4):
+                wquant(q - 1)
+            if q + 1 < QUADS:
+                mm1(q + 1, 0)
+                mm1(q + 1, 1)
+            dquant(q - 1)
+            if q >= 3:
+                kquant(2 * q - 2)
+            kquant(2 * q + 1)
+            mm2(q - 1)
+        q = QUADS - 1
+        weigh(q, 2, 4)
+        weigh(q, 0, 2)
+        dquant(q, 2, 4)
+        finish(3, 0, 4)
+        mm2(q, 2, 4)
+        kquant(2 * q)
+        dquant(q, 0, 2)
+        mm2(q, 0, 2)
+        finish(3, 6, 8)
+        finish(3, 4, 6)

@@ -22,6 +22,7 @@ P = 128
 PACK = 4
 QUADS = B * H // 4
 QW = 4 * DH
+WV_LOADS = ((0, QW), (QW, QW), (2 * QW, 2 * QW))
 REP = DH // 4
 
 
@@ -48,10 +49,10 @@ def tile_dpfpattention_pb_kernel(tc, x, wv, beta, vo, k_bytes, k_scale, W, out):
         ksc = keep.tile([P, PACK], F32, name="ksc")
         xc = [[keep.tile([P, 2, 2 * P], U32, align_bytes=64, name="xc%d%d" % (b, u)) for u in range(2)] for b in range(B)]
         xs = [[keep.tile([P, 2, 2 * P], U8, align_bytes=64, name="xs%d%d" % (b, u)) for u in range(2)] for b in range(B)]
-        wc = [keep.tile([P, 2, QW], U32, align_bytes=64, name="wc%d" % c) for c in range(4)]
-        ws = [keep.tile([P, 2, QW], U8, align_bytes=64, name="ws%d" % c) for c in range(4)]
-        kc = [keep.tile([P, 2 * S], U32, align_bytes=64, name="kc%d" % i) for i in range(2 * QUADS)]
-        ks = [keep.tile([P, 2 * S], U8, align_bytes=64, name="ks%d" % i) for i in range(2 * QUADS)]
+        wc = keep.tile([P, 8 * QW], U32, align_bytes=64, name="wc")
+        ws = keep.tile([P, 8 * QW], U8, align_bytes=64, name="ws")
+        kc = keep.tile([P, B * H * S], U32, align_bytes=64, name="kc")
+        ks = keep.tile([P, B * H * S], U8, align_bytes=64, name="ks")
         dc = [keep.tile([P, QW], U32, align_bytes=64, name="dc%d" % q) for q in range(QUADS)]
         ds = [keep.tile([P, QW], U8, align_bytes=64, name="ds%d" % q) for q in range(QUADS)]
         kb = [keep.tile([P, 4, PACK * S], U8, name="kb%d" % q) for q in range(QUADS)]
@@ -59,8 +60,7 @@ def tile_dpfpattention_pb_kernel(tc, x, wv, beta, vo, k_bytes, k_scale, W, out):
         wt = [keep.tile([P, 8, DH], BF16, name="wt%d" % o) for o in range(QUADS // 2)]
         ot = [keep.tile([P, 8, DH], F32, name="ot%d" % o) for o in range(QUADS // 2)]
         xr = [[keep.tile([P, 2, D], BF16, name="xr%d%d" % (b, u)) for u in range(2)] for b in range(B)]
-        wr = [[keep.tile([P, PACK, QW], BF16, name="wr%d%d" % (c, g)) for g in range(2)] for c in range(4)]
-        wg = [keep.tile([P, 2, QW, PACK], BF16, align_bytes=64, name="wg%d" % c) for c in range(4)]
+        wr = [keep.tile([P, 2, PACK, n], BF16, name="wr%d" % c0) for c0, n in WV_LOADS]
 
         def load_scale():
             nc.sync.dma_start(out=ksc[:], in_=k_scale.rearrange("a c (p t) e -> p (a c t e)", t=PACK))
@@ -88,10 +88,11 @@ def tile_dpfpattention_pb_kernel(tc, x, wv, beta, vo, k_bytes, k_scale, W, out):
                 out=xr[b][u][:], in_=x[b].rearrange("(m t) k -> m t k", t=PACK)[:, 2 * u : 2 * u + 2, :]
             )
 
-        def load_wv(c, g):
+        def load_wv(part, g):
+            c0, n = WV_LOADS[part]
             nc.sync.dma_start(
-                out=wr[c][g][:],
-                in_=wv.rearrange("(g p j) w -> g p j w", g=2, j=PACK)[g][:, :, QW * c : QW * (c + 1)],
+                out=wr[part][:, g],
+                in_=wv.rearrange("(g p j) w -> g p j w", g=2, j=PACK)[g][:, :, c0 : c0 + n],
             )
 
         def load_w(o):
@@ -107,21 +108,27 @@ def tile_dpfpattention_pb_kernel(tc, x, wv, beta, vo, k_bytes, k_scale, W, out):
                 out=pick[:], in_=identb[:, 0 : B * H].unsqueeze(2).to_broadcast([P, B * H, REP]), func=COPY
             )
 
+        def staging(columns, gate):
+            if gate:
+                return work.tile([P, columns, PACK], BF16, align_bytes=64, name="gate_" + gate, bufs=1)
+            return work.tile([P, columns, PACK], BF16, align_bytes=64, name="stage%d" % columns, bufs=3)
+
         kw_t = {}
         kg_t = {}
 
-        def widen(i, engine):
-            kw = work.tile([P, PACK, 2, S], BF16, name="kw", bufs=6)
-            kw_t[i] = kw
+        def widen(i, engine, first=None, n=1):
+            first = i if first is None else first
+            if first not in kw_t:
+                kw_t[first] = work.tile([P, PACK, 2 * n, S], BF16, name="kw%d" % n, bufs=4 if n == 1 else 2)
+            kw = kw_t[first]
             for h in range(2):
                 for t in range(PACK):
                     codes = kb[i // 2][:, 2 * (i % 2) + h, S * t : S * (t + 1)].bitcast(FP8)
+                    dst = kw[:, t, 2 * (i - first) + h, :]
                     if engine == "V":
-                        nc.vector.tensor_scalar(
-                            out=kw[:, t, h, :], in0=codes, scalar1=ksc[:, t : t + 1], scalar2=None, op0=MULT
-                        )
+                        nc.vector.tensor_scalar(out=dst, in0=codes, scalar1=ksc[:, t : t + 1], scalar2=None, op0=MULT)
                     else:
-                        nc.scalar.activation(out=kw[:, t, h, :], in_=codes, func=COPY, scale=ksc[:, t : t + 1])
+                        nc.scalar.activation(out=dst, in_=codes, func=COPY, scale=ksc[:, t : t + 1])
 
         def interleave(engine, dst, src):
             if engine == "G":
@@ -132,16 +139,16 @@ def tile_dpfpattention_pb_kernel(tc, x, wv, beta, vo, k_bytes, k_scale, W, out):
             copy = nc.vector.tensor_copy if engine == "V" else nc.scalar.copy
             copy(out=dst.rearrange("p (c i) t -> p c t i", i=4), in_=src.rearrange("p t (c i) -> p c t i", i=4))
 
-        def kcopy(i, engine):
-            if i % 2 == 1:
-                kg_t[i] = work.tile([P, 2 * S, PACK], BF16, align_bytes=64, name="kg_odd", bufs=1)
-            else:
-                kg_t[i] = work.tile([P, 2 * S, PACK], BF16, align_bytes=64, name="kg_even", bufs=3)
-            interleave(engine, kg_t[i][:], kw_t[i][:].rearrange("p t h s -> p t (h s)"))
+        def kcopy(first, engine, n=1, gate=None):
+            kg_t[first] = staging(2 * n * S, gate)
+            interleave(engine, kg_t[first][:], kw_t[first][:].rearrange("p t h s -> p t (h s)"))
 
-        def kquant(i):
+        def kquant(first, a=0, e=1):
+            cols = slice(2 * S * (first + a), 2 * S * (first + e))
             nc.vector.quantize_mx(
-                out=kc[i][:].bitcast(FP8X4), scales=ks[i][:], in_=kg_t[i][:].rearrange("p n t -> p (n t)")
+                out=kc[:, cols].bitcast(FP8X4),
+                scales=ks[:, cols],
+                in_=kg_t[first][:, 2 * S * a : 2 * S * e, :].rearrange("p n t -> p (n t)"),
             )
 
         xg_t = {}
@@ -155,11 +162,12 @@ def tile_dpfpattention_pb_kernel(tc, x, wv, beta, vo, k_bytes, k_scale, W, out):
                 for e in range(2):
                     nc.tensor.transpose(xt[:, tt, e, :], words[:, e::2], ident[:])
 
-        def xcopy(b, u, g):
+        def xcopy(b, u, g, gate=None):
             if g == 0:
-                xg_t[(b, u)] = work.tile([P, N * PACK], BF16, align_bytes=64, name="xg", bufs=2)
+                xg_t[(b, u)] = staging(N, gate)
             nc.scalar.copy(
-                out=xg_t[(b, u)][:, 1024 * g : 1024 * (g + 1)]
+                out=xg_t[(b, u)][:, 2 * P * g : 2 * P * (g + 1), :]
+                .rearrange("p n j -> p (n j)")
                 .bitcast(F32)
                 .rearrange("p (t m e) -> p t m e", t=2, e=2),
                 in_=xt_t[(b, u, g)][:].rearrange("p t e m -> p t m e"),
@@ -169,17 +177,42 @@ def tile_dpfpattention_pb_kernel(tc, x, wv, beta, vo, k_bytes, k_scale, W, out):
             nc.vector.quantize_mx(
                 out=xc[b][u][:].rearrange("p g n -> p (g n)").bitcast(FP8X4),
                 scales=xs[b][u][:].rearrange("p g n -> p (g n)"),
-                in_=xg_t[(b, u)][:],
+                in_=xg_t[(b, u)][:].rearrange("p n j -> p (n j)"),
             )
 
-        def wcopy(c, g, engine):
-            interleave(engine, wg[c][:, g], wr[c][g][:])
+        wg_t = {}
 
-        def wquant(c):
+        def wstage(first, n, gate=None):
+            tile = staging(n * QW, gate)
+            for j in range(first, first + n):
+                wg_t[j] = (tile, first)
+
+        def wcopy(j, engine):
+            tile, first = wg_t[j]
+            c, g = j // 2, j % 2
+            part = min(c, 2)
+            rows = wr[part][:, g, :, QW * (c - part) : QW * (c - part + 1)]
+            interleave(engine, tile[:, QW * (j - first) : QW * (j - first + 1), :], rows)
+
+        def wcopy_chunk_on_gpsimd(c):
+            tile, first = wg_t[2 * c]
+            part = min(c, 2)
+            nc.gpsimd.tensor_scalar(
+                out=tile[:].rearrange("p (g n) j -> p g n j", g=2),
+                in0=wr[part][:, :, :, QW * (c - part) : QW * (c - part + 1)].rearrange("p g j n -> p g n j"),
+                scalar1=1.0,
+                scalar2=0.0,
+                op0=MULT,
+                op1=ADD,
+            )
+
+        def wquant(j, n):
+            tile, first = wg_t[j]
+            cols = slice(QW * j, QW * (j + n))
             nc.vector.quantize_mx(
-                out=wc[c][:].rearrange("p g w -> p (g w)").bitcast(FP8X4),
-                scales=ws[c][:].rearrange("p g w -> p (g w)"),
-                in_=wg[c][:].rearrange("p g w j -> p (g w j)"),
+                out=wc[:, cols].bitcast(FP8X4),
+                scales=ws[:, cols],
+                in_=tile[:, QW * (j - first) : QW * (j - first + n), :].rearrange("p n j -> p (n j)"),
             )
 
         bp_t = {}
@@ -209,8 +242,8 @@ def tile_dpfpattention_pb_kernel(tc, x, wv, beta, vo, k_bytes, k_scale, W, out):
                         out=v[:, tt, :],
                         lhsT=xc[b][u][:, g, P * tt : P * (tt + 1)].bitcast(FP8X4),
                         lhsT_scale=xs[b][u][:, g, P * tt : P * (tt + 1)],
-                        rhs=wc[c][:, g, :].bitcast(FP8X4),
-                        rhs_scale=ws[c][:, g, :],
+                        rhs=wc[:, QW * (2 * c + g) : QW * (2 * c + g + 1)].bitcast(FP8X4),
+                        rhs_scale=ws[:, QW * (2 * c + g) : QW * (2 * c + g + 1)],
                         start=(g == 0),
                         stop=(g == 1),
                     )
@@ -220,7 +253,7 @@ def tile_dpfpattention_pb_kernel(tc, x, wv, beta, vo, k_bytes, k_scale, W, out):
 
         def subtract(q, u):
             if u == 0:
-                tm_t[q] = work.tile([P, PACK, QW], F32, name="tm", bufs=3)
+                tm_t[q] = work.tile([P, PACK, QW], F32, name="tm", bufs=4)
             nc.vector.tensor_tensor(
                 out=tm_t[q][:, 2 * u : 2 * u + 2, :].rearrange("p t (h d) -> p t h d", h=4),
                 in0=v_t[(q, u)][:].rearrange("p t (h d) -> p t h d", h=4),
@@ -254,13 +287,16 @@ def tile_dpfpattention_pb_kernel(tc, x, wv, beta, vo, k_bytes, k_scale, W, out):
 
         def mm2(q, a=0, e=4):
             if q % 2 == 0 and a == 0:
-                o_t[q // 2] = pso.tile([P, 8, DH], F32, name="o")
+                o_t[q] = pso.tile([P, 8, DH], F32, name="o")
+                o_t[q + 1] = o_t[q]
+            if q == QUADS - 1 and a == 0:
+                o_t[q] = psv.tile([P, 8, DH], F32, name="v")
             for h in range(a, e):
-                i, hh = 2 * q + h // 2, h % 2
+                cols = slice(S * (4 * q + h), S * (4 * q + h + 1))
                 nc.tensor.matmul_mx(
-                    out=o_t[q // 2][:, 4 * (q % 2) + h, :],
-                    lhsT=kc[i][:, S * hh : S * (hh + 1)].bitcast(FP8X4),
-                    lhsT_scale=ks[i][:, S * hh : S * (hh + 1)],
+                    out=o_t[q][:, 4 * (q % 2) + h, :],
+                    lhsT=kc[:, cols].bitcast(FP8X4),
+                    lhsT_scale=ks[:, cols],
                     rhs=dc[q][:, DH * h : DH * (h + 1)].bitcast(FP8X4),
                     rhs_scale=ds[q][:, DH * h : DH * (h + 1)],
                     start=True,
@@ -268,7 +304,7 @@ def tile_dpfpattention_pb_kernel(tc, x, wv, beta, vo, k_bytes, k_scale, W, out):
                 )
 
         def finish(o, a=0, e=8):
-            nc.vector.tensor_tensor(out=ot[o][:, a:e, :], in0=o_t[o][:, a:e, :], in1=wt[o][:, a:e, :], op=ADD)
+            nc.vector.tensor_tensor(out=ot[o][:, a:e, :], in0=o_t[2 * o + a // 4][:, a:e, :], in1=wt[o][:, a:e, :], op=ADD)
             b, h0 = o % 2, 8 * (o // 2)
             nc.sync.dma_start(out=out[b, h0 + a : h0 + e].rearrange("h s d -> s h d"), in_=ot[o][:, a:e, :])
 
@@ -278,25 +314,23 @@ def tile_dpfpattention_pb_kernel(tc, x, wv, beta, vo, k_bytes, k_scale, W, out):
         load_x(0, 0)
         load_wv(0, 0)
         load_wv(0, 1)
-        load_k(1)
         load_x(0, 1)
         load_wv(1, 0)
         load_vo(0)
+        load_k(1)
         load_wv(1, 1)
         load_beta()
-        load_k(2)
         load_x(1, 0)
         load_vo(1)
         load_x(1, 1)
-        load_vo(2)
-        load_k(3)
+        load_k(2)
         load_wv(2, 0)
+        load_vo(2)
         load_wv(2, 1)
         load_vo(3)
-        load_w(0)
+        load_k(3)
         load_k(4)
-        load_wv(3, 0)
-        load_wv(3, 1)
+        load_w(0)
         load_vo(4)
         for q in range(5, QUADS):
             load_k(q)
@@ -310,86 +344,128 @@ def tile_dpfpattention_pb_kernel(tc, x, wv, beta, vo, k_bytes, k_scale, W, out):
         xtrans(0, 0, 1)
         xcopy(0, 0, 0)
         xcopy(0, 0, 1)
-        kcopy(1, "V")
-        wcopy(0, 0, "V")
+        kcopy(1, "S")
+        wstage(0, 2)
+        wcopy(0, "V")
         kquant(0)
-        wcopy(0, 1, "V")
+        wcopy(1, "V")
         xquant(0, 0)
-        wquant(0)
-        widen(2, "S")
+        wquant(0, 2)
         xtrans(0, 1, 0)
         xtrans(0, 1, 1)
         xcopy(0, 1, 0)
         xcopy(0, 1, 1)
         mm1(0, 0)
-        widen(3, "S")
-        kcopy(2, "V")
-        wcopy(1, 0, "V")
+        kquant(1)
+        wstage(2, 2, gate="a")
+        wcopy(2, "V")
         xquant(0, 1)
         mm1(0, 1)
         bspread(0)
-        kquant(2)
+        widen(2, "S")
+        widen(3, "S")
         subtract(0, 0)
-        wcopy(1, 1, "V")
+        wcopy(3, "V")
         subtract(0, 1)
-        widen(5, "S")
-        widen(4, "S")
+        wquant(2, 2)
         xtrans(1, 0, 0)
         xtrans(1, 0, 1)
         xcopy(1, 0, 0)
         xcopy(1, 0, 1)
-        wquant(1)
         mm1(1, 0)
         mm1(1, 1)
-        kquant(1)
-        for q in range(1, QUADS):
-            kcopy(2 * q + 1, "G")
-            if q == 1:
-                kcopy(4, "S")
-                xtrans(1, 1, 0)
-                xtrans(1, 1, 1)
-                xcopy(1, 1, 0)
-                xcopy(1, 1, 1)
-                bspread(1)
-            if q == 1:
-                widen(7, "S")
-            if 4 <= q < QUADS - 1:
-                widen(2 * q + 3, "S")
-            if q in (2, 3):
-                wcopy(q, 0, "S")
-                wcopy(q, 1, "S")
-            if q >= 3:
-                kcopy(2 * q, "S")
-            if 2 <= q < QUADS - 1:
-                widen(2 * q + 2, "S")
-            if q == 2:
-                widen(9, "S")
-            weigh(q - 1)
-            subtract(q, 0)
-            subtract(q, 1)
-            if q >= 3 and q % 2 == 1:
-                finish(q // 2 - 1)
-            if q == 1:
-                xquant(1, 0)
-                xquant(1, 1)
-            if q in (3, 4):
-                wquant(q - 1)
-            if q + 1 < QUADS:
-                mm1(q + 1, 0)
-                mm1(q + 1, 1)
-            dquant(q - 1)
-            if q >= 3:
-                kquant(2 * q - 2)
-            kquant(2 * q + 1)
-            mm2(q - 1)
-        q = QUADS - 1
-        weigh(q, 2, 4)
-        weigh(q, 0, 2)
-        dquant(q, 2, 4)
+
+        kcopy(2, "G", gate="a")
+        xtrans(1, 1, 0)
+        xtrans(1, 1, 1)
+        kcopy(3, "S")
+        xcopy(1, 1, 0, gate="b")
+        xcopy(1, 1, 1)
+        weigh(0)
+        subtract(1, 0)
+        subtract(1, 1)
+        xquant(1, 0)
+        kquant(2)
+        mm1(2, 0)
+        dquant(0)
+        kquant(3)
+        xquant(1, 1)
+        mm1(2, 1)
+        mm1(3, 0)
+        mm1(3, 1)
+        bspread(1)
+        mm2(0)
+
+        wstage(4, 2, gate="b")
+        wcopy_chunk_on_gpsimd(2)
+        widen(4, "S", 4, 3)
+        wstage(6, 2)
+        wcopy(6, "S")
+        wcopy(7, "S")
+        widen(5, "S", 4, 3)
+        widen(6, "S", 4, 3)
+        weigh(1)
+        subtract(2, 0)
+        subtract(2, 1)
+        subtract(3, 0)
+        subtract(3, 1)
+        dquant(1)
+        wquant(6, 2)
+        wquant(4, 2)
+        for q in (4, 5):
+            mm1(q, 0)
+            mm1(q, 1)
+        mm2(1)
+        for o in (2, 3):
+            first = 4 * o - 4
+            kcopy(first, "G", 3, gate="b")
+            widen(first + 3, "S")
+            if o == 2:
+                widen(first + 4, "S", first + 4, 3)
+                kcopy(first + 3, "S")
+                widen(first + 5, "S", first + 4, 3)
+                widen(first + 6, "S", first + 4, 3)
+            else:
+                widen(12, "S")
+                kcopy(first + 3, "S")
+            weigh(2 * o - 2)
+            weigh(2 * o - 1)
+            subtract(2 * o, 0)
+            subtract(2 * o, 1)
+            subtract(2 * o + 1, 0)
+            subtract(2 * o + 1, 1)
+            finish(o - 2)
+            if o == 3:
+                widen(13, "S")
+                kcopy(12, "S")
+                widen(15, "S")
+                kcopy(13, "S")
+                widen(14, "S")
+            dquant(2 * o - 2)
+            dquant(2 * o - 1)
+            kquant(first + 3)
+            kquant(first, 0, 1)
+            kquant(first, 1, 3)
+            if o == 2:
+                for q in (6, 7):
+                    mm1(q, 0)
+                    mm1(q, 1)
+            mm2(2 * o - 2)
+            mm2(2 * o - 1)
+        kcopy(15, "G", gate="b")
+        kcopy(14, "S")
+        weigh(6)
+        weigh(7)
+        finish(2)
+        dquant(6)
+        kquant(12)
+        kquant(13)
+        mm2(6)
+        dquant(7)
+        kquant(14)
+        mm2(7, 0, 2)
+        kquant(15)
+        mm2(7, 2, 4)
         finish(3, 0, 4)
-        mm2(q, 2, 4)
-        kquant(2 * q)
-        dquant(q, 0, 2)
-        mm2(q, 0, 2)
-        finish(3, 6, 8)
         finish(3, 4, 6)
+        finish(3, 6, 8)

@@ -116,15 +116,14 @@ def tile_dpfpattention_pb_kernel(tc, x, wv, beta, vo, k_bytes, k_scale, W, out):
         kw_t = {}
         kg_t = {}
 
-        def widen(i, engine, first=None, n=1):
-            first = i if first is None else first
+        def widen(group, engine, a=0, e=None):
+            first, n = group
             if first not in kw_t:
-                kw_t[first] = work.tile([P, PACK, 2 * n, S], BF16, name="kw%d" % n, bufs=4 if n == 1 else 2)
-            kw = kw_t[first]
-            for h in range(2):
+                kw_t[first] = work.tile([P, PACK, n, S], BF16, name="kw%d" % n, bufs=2 if n > 2 else 3)
+            for h in range(a, n if e is None else e):
                 for t in range(PACK):
-                    codes = kb[i // 2][:, 2 * (i % 2) + h, S * t : S * (t + 1)].bitcast(FP8)
-                    dst = kw[:, t, 2 * (i - first) + h, :]
+                    codes = kb[(first + h) // 4][:, (first + h) % 4, S * t : S * (t + 1)].bitcast(FP8)
+                    dst = kw_t[first][:, t, h, :]
                     if engine == "V":
                         nc.vector.tensor_scalar(out=dst, in0=codes, scalar1=ksc[:, t : t + 1], scalar2=None, op0=MULT)
                     else:
@@ -139,17 +138,23 @@ def tile_dpfpattention_pb_kernel(tc, x, wv, beta, vo, k_bytes, k_scale, W, out):
             copy = nc.vector.tensor_copy if engine == "V" else nc.scalar.copy
             copy(out=dst.rearrange("p (c i) t -> p c t i", i=4), in_=src.rearrange("p t (c i) -> p c t i", i=4))
 
-        def kcopy(first, engine, n=1, gate=None):
-            kg_t[first] = staging(2 * n * S, gate)
+        def kcopy(group, engine, gate=None):
+            first, n = group
+            kg_t[first] = staging(n * S, gate)
             interleave(engine, kg_t[first][:], kw_t[first][:].rearrange("p t h s -> p t (h s)"))
 
-        def kquant(first, a=0, e=1):
-            cols = slice(2 * S * (first + a), 2 * S * (first + e))
-            nc.vector.quantize_mx(
-                out=kc[:, cols].bitcast(FP8X4),
-                scales=ks[:, cols],
-                in_=kg_t[first][:, 2 * S * a : 2 * S * e, :].rearrange("p n t -> p (n t)"),
-            )
+        def kquant(group):
+            first, n = group
+            a = 0
+            for heads in (1, 2, 4):
+                if n & heads:
+                    cols = slice(S * (first + a), S * (first + a + heads))
+                    nc.vector.quantize_mx(
+                        out=kc[:, cols].bitcast(FP8X4),
+                        scales=ks[:, cols],
+                        in_=kg_t[first][:, S * a : S * (a + heads), :].rearrange("p n t -> p (n t)"),
+                    )
+                    a += heads
 
         xg_t = {}
         xt_t = {}
@@ -276,6 +281,33 @@ def tile_dpfpattention_pb_kernel(tc, x, wv, beta, vo, k_bytes, k_scale, W, out):
                 op=MULT,
             )
 
+        half_t = {}
+
+        factors = keep.tile([P, 2, PACK], F32, name="factors")
+
+        def fetch_factors(q, a):
+            b, c = batch_and_chunk(q)
+            h0 = 4 * c + a
+            nc.scalar.copy(
+                out=factors[:], in_=bp_t[b][:, :, REP * h0 : REP * (h0 + 2) : REP].rearrange("p t h -> p h t")
+            )
+
+        def weigh_half_on_gpsimd(q, a, gate):
+            half_t[q] = staging(2 * DH, gate)
+            nc.gpsimd.tensor_tensor(
+                out=half_t[q][:].rearrange("p (h d) t -> p h d t", h=2),
+                in0=tm_t[q][:, :, DH * a : DH * (a + 2)].rearrange("p t (h d) -> p h d t", h=2),
+                in1=factors[:].unsqueeze(2).to_broadcast([P, 2, DH, PACK]),
+                op=MULT,
+            )
+
+        def dquant_half(q, a):
+            nc.vector.quantize_mx(
+                out=dc[q][:, DH * a : DH * (a + 2)].bitcast(FP8X4),
+                scales=ds[q][:, DH * a : DH * (a + 2)],
+                in_=half_t[q][:].rearrange("p n t -> p (n t)"),
+            )
+
         def dquant(q, a=0, e=4):
             nc.vector.quantize_mx(
                 out=dc[q][:, DH * a : DH * e].bitcast(FP8X4),
@@ -312,17 +344,17 @@ def tile_dpfpattention_pb_kernel(tc, x, wv, beta, vo, k_bytes, k_scale, W, out):
         load_scale()
         load_k(0)
         load_x(0, 0)
+        load_beta()
+        load_k(1)
         load_wv(0, 0)
-        load_wv(0, 1)
         load_x(0, 1)
+        load_wv(0, 1)
         load_wv(1, 0)
         load_vo(0)
-        load_k(1)
         load_wv(1, 1)
-        load_beta()
         load_x(1, 0)
-        load_vo(1)
         load_x(1, 1)
+        load_vo(1)
         load_k(2)
         load_wv(2, 0)
         load_vo(2)
@@ -337,97 +369,103 @@ def tile_dpfpattention_pb_kernel(tc, x, wv, beta, vo, k_bytes, k_scale, W, out):
             load_vo(q)
             load_w(q - 4)
 
-        widen(0, "V")
-        widen(1, "S")
-        kcopy(0, "V")
+        widen((0, 2), "V")
+        widen((2, 2), "S")
+        kcopy((0, 2), "V")
         xtrans(0, 0, 0)
         xtrans(0, 0, 1)
         xcopy(0, 0, 0)
         xcopy(0, 0, 1)
-        kcopy(1, "S")
+        kcopy((2, 2), "V")
+        kquant((0, 2))
         wstage(0, 2)
         wcopy(0, "V")
-        kquant(0)
-        wcopy(1, "V")
+        kquant((2, 2))
         xquant(0, 0)
-        wquant(0, 2)
+        widen((4, 2), "S")
         xtrans(0, 1, 0)
         xtrans(0, 1, 1)
         xcopy(0, 1, 0)
         xcopy(0, 1, 1)
+        wcopy(1, "V")
+        kcopy((4, 2), "V")
+        wquant(0, 2)
+        bspread(0)
         mm1(0, 0)
-        kquant(1)
-        wstage(2, 2, gate="a")
-        wcopy(2, "V")
         xquant(0, 1)
         mm1(0, 1)
-        bspread(0)
-        widen(2, "S")
-        widen(3, "S")
+        kquant((4, 2))
+        wstage(2, 2, gate="a")
+        wcopy(2, "S")
+        wcopy(3, "S")
+        widen((6, 2), "S")
         subtract(0, 0)
-        wcopy(3, "V")
         subtract(0, 1)
         wquant(2, 2)
         xtrans(1, 0, 0)
         xtrans(1, 0, 1)
-        xcopy(1, 0, 0)
-        xcopy(1, 0, 1)
         mm1(1, 0)
         mm1(1, 1)
+        xcopy(1, 0, 0)
+        xcopy(1, 0, 1)
 
-        kcopy(2, "G", gate="a")
+        kcopy((6, 2), "G", gate="a")
         xtrans(1, 1, 0)
         xtrans(1, 1, 1)
-        kcopy(3, "S")
+        widen((8, 7), "S", 0, 1)
         xcopy(1, 1, 0, gate="b")
         xcopy(1, 1, 1)
+        widen((8, 7), "S", 1, 2)
         weigh(0)
         subtract(1, 0)
         subtract(1, 1)
         xquant(1, 0)
-        kquant(2)
         mm1(2, 0)
+        mm1(3, 0)
+        kquant((6, 2))
         dquant(0)
-        kquant(3)
         xquant(1, 1)
         mm1(2, 1)
-        mm1(3, 0)
         mm1(3, 1)
         bspread(1)
         mm2(0)
 
-        wstage(4, 2, gate="b")
-        wcopy_chunk_on_gpsimd(2)
-        widen(4, "S", 4, 3)
-        wstage(6, 2)
-        wcopy(6, "S")
-        wcopy(7, "S")
-        widen(5, "S", 4, 3)
-        widen(6, "S", 4, 3)
+        wstage(6, 2, gate="b")
+        wcopy_chunk_on_gpsimd(3)
+        wstage(4, 2)
+        wcopy(4, "S")
+        wcopy(5, "S")
+        widen((8, 7), "S", 2, 7)
         weigh(1)
         subtract(2, 0)
-        subtract(2, 1)
         subtract(3, 0)
+        subtract(2, 1)
         subtract(3, 1)
         dquant(1)
-        wquant(6, 2)
         wquant(4, 2)
+        wquant(6, 2)
         for q in (4, 5):
             mm1(q, 0)
             mm1(q, 1)
         mm2(1)
         for o in (2, 3):
-            first = 4 * o - 4
-            kcopy(first, "G", 3, gate="b")
-            widen(first + 3, "S")
+            big = (8 * o - 8, 7)
+            single = (8 * o - 1, 1)
+            kcopy(big, "G", gate="b")
+            widen(single, "S")
             if o == 2:
-                widen(first + 4, "S", first + 4, 3)
-                kcopy(first + 3, "S")
-                widen(first + 5, "S", first + 4, 3)
-                widen(first + 6, "S", first + 4, 3)
+                widen((16, 7), "S", 0, 1)
+                kcopy(single, "S")
+                widen((16, 7), "S", 1, 7)
             else:
-                widen(12, "S")
-                kcopy(first + 3, "S")
+                fetch_factors(7, 2)
+                widen((24, 4), "S")
+                kcopy(single, "S")
+                kcopy((24, 4), "S")
+                widen((28, 2), "S")
+                widen((30, 2), "S")
+                kcopy((28, 2), "S")
+                kcopy((30, 2), "S")
             weigh(2 * o - 2)
             weigh(2 * o - 1)
             subtract(2 * o, 0)
@@ -435,36 +473,29 @@ def tile_dpfpattention_pb_kernel(tc, x, wv, beta, vo, k_bytes, k_scale, W, out):
             subtract(2 * o + 1, 0)
             subtract(2 * o + 1, 1)
             finish(o - 2)
-            if o == 3:
-                widen(13, "S")
-                kcopy(12, "S")
-                widen(15, "S")
-                kcopy(13, "S")
-                widen(14, "S")
             dquant(2 * o - 2)
             dquant(2 * o - 1)
-            kquant(first + 3)
-            kquant(first, 0, 1)
-            kquant(first, 1, 3)
+            kquant(single)
+            if o == 3:
+                kquant((24, 4))
+            kquant(big)
             if o == 2:
                 for q in (6, 7):
                     mm1(q, 0)
                     mm1(q, 1)
             mm2(2 * o - 2)
             mm2(2 * o - 1)
-        kcopy(15, "G", gate="b")
-        kcopy(14, "S")
+        weigh_half_on_gpsimd(7, 2, "b")
         weigh(6)
-        weigh(7)
+        weigh(7, 0, 2)
         finish(2)
         dquant(6)
-        kquant(12)
-        kquant(13)
         mm2(6)
-        dquant(7)
-        kquant(14)
+        kquant((28, 2))
+        dquant(7, 0, 2)
         mm2(7, 0, 2)
-        kquant(15)
+        kquant((30, 2))
+        dquant_half(7, 2)
         mm2(7, 2, 4)
         finish(3, 0, 4)
         finish(3, 4, 6)

@@ -111,7 +111,7 @@ def tile_dpfpattention_pb_kernel(tc, x, wv, beta, vo, k_bytes, k_scale, W, out):
         def staging(columns, gate):
             if gate:
                 return work.tile([P, columns, PACK], BF16, align_bytes=64, name="gate_" + gate, bufs=1)
-            return work.tile([P, columns, PACK], BF16, align_bytes=64, name="stage%d" % columns, bufs=3)
+            return work.tile([P, columns, PACK], BF16, align_bytes=64, name="stage%d" % columns, bufs=4)
 
         kw_t = {}
         kg_t = {}
@@ -119,7 +119,7 @@ def tile_dpfpattention_pb_kernel(tc, x, wv, beta, vo, k_bytes, k_scale, W, out):
         def widen(group, engine, a=0, e=None):
             first, n = group
             if first not in kw_t:
-                kw_t[first] = work.tile([P, PACK, n, S], BF16, name="kw%d" % n, bufs=2 if n > 2 else 3)
+                kw_t[first] = work.tile([P, PACK, n, S], BF16, name="kw%d" % n, bufs=2 if n > 2 else 4)
             for h in range(a, n if e is None else e):
                 for t in range(PACK):
                     codes = kb[(first + h) // 4][:, (first + h) % 4, S * t : S * (t + 1)].bitcast(FP8)
@@ -142,6 +142,26 @@ def tile_dpfpattention_pb_kernel(tc, x, wv, beta, vo, k_bytes, k_scale, W, out):
             first, n = group
             kg_t[first] = staging(n * S, gate)
             interleave(engine, kg_t[first][:], kw_t[first][:].rearrange("p t h s -> p t (h s)"))
+
+        turned_t = {}
+
+        def kturn(group):
+            first, n = group
+            bank = psx.tile([P, n * S, PACK], BF16, name="xt")
+            turned_t[first] = bank
+            for h in range(n):
+                nc.tensor.matmul(
+                    bank[:, S * h : S * (h + 1), :].rearrange("p s t -> p t s"),
+                    lhsT=identb[:],
+                    rhs=kw_t[first][:, :, h, :],
+                    start=True,
+                    stop=True,
+                )
+
+        def kfetch(group, gate=None):
+            first, n = group
+            kg_t[first] = staging(n * S, gate)
+            nc.scalar.copy(out=kg_t[first][:], in_=turned_t[first][:])
 
         def kquant(group):
             first, n = group
@@ -222,15 +242,14 @@ def tile_dpfpattention_pb_kernel(tc, x, wv, beta, vo, k_bytes, k_scale, W, out):
 
         bp_t = {}
 
-        def bspread(b):
-            pool = psb if b == 0 else psx
-            bp = pool.tile([P, PACK, H * REP], BF16, name="bp" if b == 0 else "xt")
-            bp_t[b] = bp
+        def bspread(half):
+            bp = psb.tile([P, PACK, B, 8 * REP], BF16, name="bp")
+            bp_t[half] = bp
             for t in range(PACK):
                 nc.tensor.matmul(
                     bp[:, t],
                     lhsT=brow[:, t::PACK],
-                    rhs=pick[:, H * b : H * (b + 1)].rearrange("p h c -> p (h c)"),
+                    rhs=pick[:].rearrange("p (b h) c -> p b (h c)", b=B)[:, :, 8 * REP * half : 8 * REP * (half + 1)],
                     start=True,
                     stop=True,
                 )
@@ -270,11 +289,11 @@ def tile_dpfpattention_pb_kernel(tc, x, wv, beta, vo, k_bytes, k_scale, W, out):
             if q not in dg_t:
                 dg_t[q] = work.tile([P, 4, DH, PACK], BF16, align_bytes=64, name="dg", bufs=3)
             b, c = batch_and_chunk(q)
-            h0 = 4 * c
+            h0 = 4 * (c % 2)
             nc.vector.tensor_tensor(
                 out=dg_t[q][:, a:e].rearrange("p h (c i) t -> p (h c) t i", i=4),
                 in0=tm_t[q][:, :, DH * a : DH * e].rearrange("p t (c i) -> p c t i", i=4),
-                in1=bp_t[b][:, :, REP * (h0 + a) : REP * (h0 + e)]
+                in1=bp_t[c // 2][:, :, b, REP * (h0 + a) : REP * (h0 + e)]
                 .rearrange("p t c -> p c t")
                 .unsqueeze(3)
                 .to_broadcast([P, (e - a) * REP, PACK, 4]),
@@ -287,9 +306,9 @@ def tile_dpfpattention_pb_kernel(tc, x, wv, beta, vo, k_bytes, k_scale, W, out):
 
         def fetch_factors(q, a):
             b, c = batch_and_chunk(q)
-            h0 = 4 * c + a
+            h0 = 4 * (c % 2) + a
             nc.scalar.copy(
-                out=factors[:], in_=bp_t[b][:, :, REP * h0 : REP * (h0 + 2) : REP].rearrange("p t h -> p h t")
+                out=factors[:], in_=bp_t[c // 2][:, :, b, REP * h0 : REP * (h0 + 2) : REP].rearrange("p t h -> p h t")
             )
 
         def weigh_half_on_gpsimd(q, a, gate):
@@ -412,10 +431,10 @@ def tile_dpfpattention_pb_kernel(tc, x, wv, beta, vo, k_bytes, k_scale, W, out):
         kcopy((6, 2), "G", gate="a")
         xtrans(1, 1, 0)
         xtrans(1, 1, 1)
-        widen((8, 7), "S", 0, 1)
+        widen((8, 6), "S", 0, 1)
         xcopy(1, 1, 0, gate="b")
         xcopy(1, 1, 1)
-        widen((8, 7), "S", 1, 2)
+        widen((8, 6), "S", 1, 2)
         weigh(0)
         subtract(1, 0)
         subtract(1, 1)
@@ -427,7 +446,6 @@ def tile_dpfpattention_pb_kernel(tc, x, wv, beta, vo, k_bytes, k_scale, W, out):
         xquant(1, 1)
         mm1(2, 1)
         mm1(3, 1)
-        bspread(1)
         mm2(0)
 
         wstage(6, 2, gate="b")
@@ -435,7 +453,7 @@ def tile_dpfpattention_pb_kernel(tc, x, wv, beta, vo, k_bytes, k_scale, W, out):
         wstage(4, 2)
         wcopy(4, "S")
         wcopy(5, "S")
-        widen((8, 7), "S", 2, 7)
+        widen((8, 6), "S", 2, 6)
         weigh(1)
         subtract(2, 0)
         subtract(3, 0)
@@ -449,25 +467,30 @@ def tile_dpfpattention_pb_kernel(tc, x, wv, beta, vo, k_bytes, k_scale, W, out):
             mm1(q, 1)
         mm2(1)
         for o in (2, 3):
-            big = (8 * o - 8, 7)
-            single = (8 * o - 1, 1)
+            big = (8 * o - 8, 6)
             kcopy(big, "G", gate="b")
-            widen(single, "S")
             if o == 2:
-                widen((16, 7), "S", 0, 1)
-                kcopy(single, "S")
-                widen((16, 7), "S", 1, 7)
+                widen((14, 2), "S")
+                kturn((14, 2))
+                widen((16, 6), "S")
+                kfetch((14, 2))
             else:
-                fetch_factors(7, 2)
-                widen((24, 4), "S")
-                kcopy(single, "S")
-                kcopy((24, 4), "S")
-                widen((28, 2), "S")
-                widen((30, 2), "S")
-                kcopy((28, 2), "S")
+                for first in range(22, 34, 2):
+                    if first < 32:
+                        widen((first, 2), "S")
+                    if first >= 26:
+                        kfetch((first - 4, 2))
+                    if first < 30:
+                        kturn((first, 2))
+                    if first == 24:
+                        fetch_factors(7, 2)
+                        mm2(2)
+                        mm2(3)
                 kcopy((30, 2), "S")
             weigh(2 * o - 2)
             weigh(2 * o - 1)
+            if o == 2:
+                bspread(1)
             subtract(2 * o, 0)
             subtract(2 * o, 1)
             subtract(2 * o + 1, 0)
@@ -475,21 +498,22 @@ def tile_dpfpattention_pb_kernel(tc, x, wv, beta, vo, k_bytes, k_scale, W, out):
             finish(o - 2)
             dquant(2 * o - 2)
             dquant(2 * o - 1)
-            kquant(single)
+            kquant((8 * o - 2, 2))
             if o == 3:
-                kquant((24, 4))
+                kquant((24, 2))
             kquant(big)
             if o == 2:
                 for q in (6, 7):
                     mm1(q, 0)
                     mm1(q, 1)
-            mm2(2 * o - 2)
-            mm2(2 * o - 1)
+        mm2(4)
+        mm2(5)
         weigh_half_on_gpsimd(7, 2, "b")
         weigh(6)
         weigh(7, 0, 2)
         finish(2)
         dquant(6)
+        kquant((26, 2))
         mm2(6)
         kquant((28, 2))
         dquant(7, 0, 2)

@@ -53,8 +53,8 @@ def tile_dpfpattention_pb_kernel(tc, x, wv, beta, vo, k_bytes, k_scale, W, out):
         ws = keep.tile([P, 8 * QW], U8, align_bytes=64, name="ws")
         kc = keep.tile([P, B * H * S], U32, align_bytes=64, name="kc")
         ks = keep.tile([P, B * H * S], U8, align_bytes=64, name="ks")
-        dc = [keep.tile([P, QW], U32, align_bytes=64, name="dc%d" % q) for q in range(QUADS)]
-        ds = [keep.tile([P, QW], U8, align_bytes=64, name="ds%d" % q) for q in range(QUADS)]
+        dc = keep.tile([P, B * H * DH], U32, align_bytes=64, name="dc")
+        ds = keep.tile([P, B * H * DH], U8, align_bytes=64, name="ds")
         kb = [keep.tile([P, 4, PACK * S], U8, name="kb%d" % q) for q in range(QUADS)]
         vs = [keep.tile([P, 4, PACK, DH], BF16, name="vs%d" % q) for q in range(QUADS)]
         wt = [keep.tile([P, 8, DH], BF16, name="wt%d" % o) for o in range(QUADS // 2)]
@@ -138,10 +138,18 @@ def tile_dpfpattention_pb_kernel(tc, x, wv, beta, vo, k_bytes, k_scale, W, out):
             copy = nc.vector.tensor_copy if engine == "V" else nc.scalar.copy
             copy(out=dst.rearrange("p (c i) t -> p c t i", i=4), in_=src.rearrange("p t (c i) -> p c t i", i=4))
 
-        def kcopy(group, engine, gate=None):
+        def kstage(first, n, gate=None):
+            tile = staging(n * S, gate)
+            for h in range(first, first + n):
+                kg_t[h] = (tile, first)
+
+        def kstaged(first, n):
+            tile, base = kg_t[first]
+            return tile[:, S * (first - base) : S * (first - base + n), :]
+
+        def kcopy(group, engine):
             first, n = group
-            kg_t[first] = staging(n * S, gate)
-            interleave(engine, kg_t[first][:], kw_t[first][:].rearrange("p t h s -> p t (h s)"))
+            interleave(engine, kstaged(first, n), kw_t[first][:].rearrange("p t h s -> p t (h s)"))
 
         turned_t = {}
 
@@ -158,23 +166,15 @@ def tile_dpfpattention_pb_kernel(tc, x, wv, beta, vo, k_bytes, k_scale, W, out):
                     stop=True,
                 )
 
-        def kfetch(group, gate=None):
+        def kfetch(group):
             first, n = group
-            kg_t[first] = staging(n * S, gate)
-            nc.scalar.copy(out=kg_t[first][:], in_=turned_t[first][:])
+            nc.scalar.copy(out=kstaged(first, n), in_=turned_t[first][:])
 
-        def kquant(group):
-            first, n = group
-            a = 0
-            for heads in (1, 2, 4):
-                if n & heads:
-                    cols = slice(S * (first + a), S * (first + a + heads))
-                    nc.vector.quantize_mx(
-                        out=kc[:, cols].bitcast(FP8X4),
-                        scales=ks[:, cols],
-                        in_=kg_t[first][:, S * a : S * (a + heads), :].rearrange("p n t -> p (n t)"),
-                    )
-                    a += heads
+        def kquant(first, n):
+            cols = slice(S * first, S * (first + n))
+            nc.vector.quantize_mx(
+                out=kc[:, cols].bitcast(FP8X4), scales=ks[:, cols], in_=kstaged(first, n).rearrange("p n t -> p (n t)")
+            )
 
         xg_t = {}
         xt_t = {}
@@ -223,7 +223,7 @@ def tile_dpfpattention_pb_kernel(tc, x, wv, beta, vo, k_bytes, k_scale, W, out):
             tile, first = wg_t[2 * c]
             part = min(c, 2)
             nc.gpsimd.tensor_scalar(
-                out=tile[:].rearrange("p (g n) j -> p g n j", g=2),
+                out=tile[:, QW * (2 * c - first) : QW * (2 * c - first + 2), :].rearrange("p (g n) j -> p g n j", g=2),
                 in0=wr[part][:, :, :, QW * (c - part) : QW * (c - part + 1)].rearrange("p g j n -> p g n j"),
                 scalar1=1.0,
                 scalar2=0.0,
@@ -276,63 +276,54 @@ def tile_dpfpattention_pb_kernel(tc, x, wv, beta, vo, k_bytes, k_scale, W, out):
         dg_t = {}
 
         def subtract(q, u):
-            if u == 0:
-                tm_t[q] = work.tile([P, PACK, QW], F32, name="tm", bufs=4)
+            o = q // 2
+            if o not in tm_t:
+                tm_t[o] = work.tile([P, PACK, 2 * QW], F32, name="tm", bufs=2)
             nc.vector.tensor_tensor(
-                out=tm_t[q][:, 2 * u : 2 * u + 2, :].rearrange("p t (h d) -> p t h d", h=4),
+                out=tm_t[o][:, 2 * u : 2 * u + 2, QW * (q % 2) : QW * (q % 2 + 1)].rearrange("p t (h d) -> p t h d", h=4),
                 in0=v_t[(q, u)][:].rearrange("p t (h d) -> p t h d", h=4),
                 in1=vs[q][:, :, 2 * u : 2 * u + 2, :].rearrange("p h t d -> p t h d"),
                 op=SUB,
             )
 
-        def weigh(q, a=0, e=4):
-            if q not in dg_t:
-                dg_t[q] = work.tile([P, 4, DH, PACK], BF16, align_bytes=64, name="dg", bufs=3)
-            b, c = batch_and_chunk(q)
-            h0 = 4 * (c % 2)
+        def weigh(o, a=0, e=8):
+            if o not in dg_t:
+                dg_t[o] = work.tile([P, 8, DH, PACK], BF16, align_bytes=64, name="dg", bufs=2)
             nc.vector.tensor_tensor(
-                out=dg_t[q][:, a:e].rearrange("p h (c i) t -> p (h c) t i", i=4),
-                in0=tm_t[q][:, :, DH * a : DH * e].rearrange("p t (c i) -> p c t i", i=4),
-                in1=bp_t[c // 2][:, :, b, REP * (h0 + a) : REP * (h0 + e)]
+                out=dg_t[o][:, a:e].rearrange("p h (c i) t -> p (h c) t i", i=4),
+                in0=tm_t[o][:, :, DH * a : DH * e].rearrange("p t (c i) -> p c t i", i=4),
+                in1=bp_t[o // 2][:, :, o % 2, REP * a : REP * e]
                 .rearrange("p t c -> p c t")
                 .unsqueeze(3)
                 .to_broadcast([P, (e - a) * REP, PACK, 4]),
                 op=MULT,
             )
 
-        half_t = {}
-
         factors = keep.tile([P, 2, PACK], F32, name="factors")
+        rest_t = {}
 
-        def fetch_factors(q, a):
-            b, c = batch_and_chunk(q)
-            h0 = 4 * (c % 2) + a
+        def fetch_factors(o, a):
             nc.scalar.copy(
-                out=factors[:], in_=bp_t[c // 2][:, :, b, REP * h0 : REP * (h0 + 2) : REP].rearrange("p t h -> p h t")
+                out=factors[:],
+                in_=bp_t[o // 2][:, :, o % 2, REP * a : REP * (a + 2) : REP].rearrange("p t h -> p h t"),
             )
 
-        def weigh_half_on_gpsimd(q, a, gate):
-            half_t[q] = staging(2 * DH, gate)
+        def weigh_on_gpsimd(o, a, gate):
+            rest_t[o] = staging(2 * DH, gate)
             nc.gpsimd.tensor_tensor(
-                out=half_t[q][:].rearrange("p (h d) t -> p h d t", h=2),
-                in0=tm_t[q][:, :, DH * a : DH * (a + 2)].rearrange("p t (h d) -> p h d t", h=2),
+                out=rest_t[o][:].rearrange("p (h d) t -> p h d t", h=2),
+                in0=tm_t[o][:, :, DH * a : DH * (a + 2)].rearrange("p t (h d) -> p h d t", h=2),
                 in1=factors[:].unsqueeze(2).to_broadcast([P, 2, DH, PACK]),
                 op=MULT,
             )
 
-        def dquant_half(q, a):
-            nc.vector.quantize_mx(
-                out=dc[q][:, DH * a : DH * (a + 2)].bitcast(FP8X4),
-                scales=ds[q][:, DH * a : DH * (a + 2)],
-                in_=half_t[q][:].rearrange("p n t -> p (n t)"),
-            )
-
-        def dquant(q, a=0, e=4):
-            nc.vector.quantize_mx(
-                out=dc[q][:, DH * a : DH * e].bitcast(FP8X4),
-                scales=ds[q][:, DH * a : DH * e],
-                in_=dg_t[q][:, a:e].rearrange("p h d t -> p (h d t)"),
-            )
+        def dquant(o, a=0, e=8, from_gpsimd=False):
+            cols = slice(DH * (8 * o + a), DH * (8 * o + e))
+            if from_gpsimd:
+                values = rest_t[o][:].rearrange("p n t -> p (n t)")
+            else:
+                values = dg_t[o][:, a:e].rearrange("p h d t -> p (h d t)")
+            nc.vector.quantize_mx(out=dc[:, cols].bitcast(FP8X4), scales=ds[:, cols], in_=values)
 
         o_t = {}
 
@@ -348,8 +339,8 @@ def tile_dpfpattention_pb_kernel(tc, x, wv, beta, vo, k_bytes, k_scale, W, out):
                     out=o_t[q][:, 4 * (q % 2) + h, :],
                     lhsT=kc[:, cols].bitcast(FP8X4),
                     lhsT_scale=ks[:, cols],
-                    rhs=dc[q][:, DH * h : DH * (h + 1)].bitcast(FP8X4),
-                    rhs_scale=ds[q][:, DH * h : DH * (h + 1)],
+                    rhs=dc[:, DH * (4 * q + h) : DH * (4 * q + h + 1)].bitcast(FP8X4),
+                    rhs_scale=ds[:, DH * (4 * q + h) : DH * (4 * q + h + 1)],
                     start=True,
                     stop=True,
                 )
@@ -390,16 +381,16 @@ def tile_dpfpattention_pb_kernel(tc, x, wv, beta, vo, k_bytes, k_scale, W, out):
 
         widen((0, 2), "V")
         widen((2, 2), "S")
+        kstage(0, 4)
         kcopy((0, 2), "V")
         xtrans(0, 0, 0)
         xtrans(0, 0, 1)
         xcopy(0, 0, 0)
         xcopy(0, 0, 1)
         kcopy((2, 2), "V")
-        kquant((0, 2))
         wstage(0, 2)
         wcopy(0, "V")
-        kquant((2, 2))
+        kquant(0, 4)
         xquant(0, 0)
         widen((4, 2), "S")
         xtrans(0, 1, 0)
@@ -407,13 +398,14 @@ def tile_dpfpattention_pb_kernel(tc, x, wv, beta, vo, k_bytes, k_scale, W, out):
         xcopy(0, 1, 0)
         xcopy(0, 1, 1)
         wcopy(1, "V")
+        kstage(4, 2)
         kcopy((4, 2), "V")
         wquant(0, 2)
         bspread(0)
         mm1(0, 0)
         xquant(0, 1)
         mm1(0, 1)
-        kquant((4, 2))
+        kquant(4, 2)
         wstage(2, 2, gate="a")
         wcopy(2, "S")
         wcopy(3, "S")
@@ -428,98 +420,93 @@ def tile_dpfpattention_pb_kernel(tc, x, wv, beta, vo, k_bytes, k_scale, W, out):
         xcopy(1, 0, 0)
         xcopy(1, 0, 1)
 
-        kcopy((6, 2), "G", gate="a")
+        kstage(6, 2, gate="a")
+        kcopy((6, 2), "G")
         xtrans(1, 1, 0)
         xtrans(1, 1, 1)
         widen((8, 6), "S", 0, 1)
         xcopy(1, 1, 0, gate="b")
         xcopy(1, 1, 1)
-        widen((8, 6), "S", 1, 2)
-        weigh(0)
+        widen((8, 6), "S", 1, 3)
+        weigh(0, 0, 4)
         subtract(1, 0)
         subtract(1, 1)
         xquant(1, 0)
         mm1(2, 0)
         mm1(3, 0)
-        kquant((6, 2))
-        dquant(0)
+        kquant(6, 2)
+        dquant(0, 0, 4)
         xquant(1, 1)
         mm1(2, 1)
         mm1(3, 1)
         mm2(0)
 
-        wstage(6, 2, gate="b")
+        wstage(4, 4, gate="b")
         wcopy_chunk_on_gpsimd(3)
-        wstage(4, 2)
         wcopy(4, "S")
         wcopy(5, "S")
-        widen((8, 6), "S", 2, 6)
-        weigh(1)
+        widen((8, 6), "S", 3, 6)
+        weigh(0, 4, 8)
         subtract(2, 0)
         subtract(3, 0)
         subtract(2, 1)
         subtract(3, 1)
-        dquant(1)
-        wquant(4, 2)
-        wquant(6, 2)
+        dquant(0, 4, 8)
+        wquant(4, 4)
         for q in (4, 5):
             mm1(q, 0)
             mm1(q, 1)
         mm2(1)
         for o in (2, 3):
-            big = (8 * o - 8, 6)
-            kcopy(big, "G", gate="b")
+            first = 8 * o - 8
+            kstage(first, 8, gate="b")
+            kcopy((first, 6), "G")
+            widen((first + 6, 2), "S")
             if o == 2:
-                widen((14, 2), "S")
-                kturn((14, 2))
-                widen((16, 6), "S")
-                kfetch((14, 2))
+                widen((16, 6), "S", 0, 1)
+                kcopy((14, 2), "S")
+                widen((16, 6), "S", 1, 6)
             else:
-                for first in range(22, 34, 2):
-                    if first < 32:
-                        widen((first, 2), "S")
-                    if first >= 26:
-                        kfetch((first - 4, 2))
-                    if first < 30:
-                        kturn((first, 2))
-                    if first == 24:
-                        fetch_factors(7, 2)
-                        mm2(2)
-                        mm2(3)
+                fetch_factors(3, 6)
+                widen((24, 2), "S")
+                kturn((24, 2))
+                kcopy((22, 2), "S")
+                widen((26, 2), "S")
+                kturn((26, 2))
+                kstage(24, 4)
+                kfetch((24, 2))
+                widen((28, 2), "S")
+                kfetch((26, 2))
+                widen((30, 2), "S")
+                kstage(28, 4)
+                kcopy((28, 2), "S")
                 kcopy((30, 2), "S")
-            weigh(2 * o - 2)
-            weigh(2 * o - 1)
+            weigh(o - 1)
             if o == 2:
                 bspread(1)
-            subtract(2 * o, 0)
-            subtract(2 * o, 1)
-            subtract(2 * o + 1, 0)
-            subtract(2 * o + 1, 1)
+            for q in (2 * o, 2 * o + 1):
+                subtract(q, 0)
+                subtract(q, 1)
             finish(o - 2)
-            dquant(2 * o - 2)
-            dquant(2 * o - 1)
-            kquant((8 * o - 2, 2))
-            if o == 3:
-                kquant((24, 2))
-            kquant(big)
+            dquant(o - 1)
+            kquant(first, 8)
             if o == 2:
                 for q in (6, 7):
                     mm1(q, 0)
                     mm1(q, 1)
-        mm2(4)
-        mm2(5)
-        weigh_half_on_gpsimd(7, 2, "b")
-        weigh(6)
-        weigh(7, 0, 2)
+            mm2(2 * o - 2)
+            mm2(2 * o - 1)
+        weigh_on_gpsimd(3, 6, "b")
+        weigh(3, 0, 6)
         finish(2)
-        dquant(6)
-        kquant((26, 2))
+        dquant(3, 0, 4)
+        kquant(24, 4)
         mm2(6)
-        kquant((28, 2))
-        dquant(7, 0, 2)
+        dquant(3, 4, 6)
+        kquant(28, 2)
         mm2(7, 0, 2)
-        kquant((30, 2))
-        dquant_half(7, 2)
+        dquant(3, 6, 8, from_gpsimd=True)
+        kquant(30, 2)
         mm2(7, 2, 4)
         finish(3, 0, 4)
         finish(3, 4, 6)

@@ -331,12 +331,13 @@ def tile_dpfpattention_pb_kernel(tc, x, wv, beta, vo, k_bytes, k_scale, W, out):
             if q % 2 == 0 and a == 0:
                 o_t[q] = pso.tile([P, 8, DH], F32, name="o")
                 o_t[q + 1] = o_t[q]
-            if q == QUADS - 1 and a == 0:
-                o_t[q] = psv.tile([P, 8, DH], F32, name="v")
+            if q == QUADS - 1:
+                o_t[(q, a)] = psv.tile([P, 8, DH], F32, name="v")
+            bank = o_t[(q, a)] if q == QUADS - 1 else o_t[q]
             for h in range(a, e):
                 cols = slice(S * (4 * q + h), S * (4 * q + h + 1))
                 nc.tensor.matmul_mx(
-                    out=o_t[q][:, 4 * (q % 2) + h, :],
+                    out=bank[:, 4 * (q % 2) + h, :],
                     lhsT=kc[:, cols].bitcast(FP8X4),
                     lhsT_scale=ks[:, cols],
                     rhs=dc[:, DH * (4 * q + h) : DH * (4 * q + h + 1)].bitcast(FP8X4),
@@ -346,7 +347,9 @@ def tile_dpfpattention_pb_kernel(tc, x, wv, beta, vo, k_bytes, k_scale, W, out):
                 )
 
         def finish(o, a=0, e=8):
-            nc.vector.tensor_tensor(out=ot[o][:, a:e, :], in0=o_t[2 * o + a // 4][:, a:e, :], in1=wt[o][:, a:e, :], op=ADD)
+            q = 2 * o + a // 4
+            bank = o_t[(q, a - 4)] if q == QUADS - 1 else o_t[q]
+            nc.vector.tensor_tensor(out=ot[o][:, a:e, :], in0=bank[:, a:e, :], in1=wt[o][:, a:e, :], op=ADD)
             b, h0 = o % 2, 8 * (o // 2)
             nc.sync.dma_start(out=out[b, h0 + a : h0 + e].rearrange("h s d -> s h d"), in_=ot[o][:, a:e, :])
 
@@ -467,20 +470,13 @@ def tile_dpfpattention_pb_kernel(tc, x, wv, beta, vo, k_bytes, k_scale, W, out):
                 kcopy((14, 2), "S")
                 widen((16, 6), "S", 1, 6)
             else:
-                fetch_factors(3, 6)
-                widen((24, 2), "S")
-                kturn((24, 2))
+                widen((24, 4), "S", 0, 1)
                 kcopy((22, 2), "S")
-                widen((26, 2), "S")
-                kturn((26, 2))
+                widen((24, 4), "S", 1, 4)
+                widen((29, 3), "S")
                 kstage(24, 4)
-                kfetch((24, 2))
-                widen((28, 2), "S")
-                kfetch((26, 2))
-                widen((30, 2), "S")
-                kstage(28, 4)
-                kcopy((28, 2), "S")
-                kcopy((30, 2), "S")
+                kcopy((24, 4), "S")
+                widen((28, 1), "S")
             weigh(o - 1)
             if o == 2:
                 bspread(1)
@@ -496,18 +492,19 @@ def tile_dpfpattention_pb_kernel(tc, x, wv, beta, vo, k_bytes, k_scale, W, out):
                     mm1(q, 1)
             mm2(2 * o - 2)
             mm2(2 * o - 1)
-        weigh_on_gpsimd(3, 6, "b")
-        weigh(3, 0, 6)
+        kstage(28, 4, gate="b")
+        kcopy((29, 3), "G")
+        kcopy((28, 1), "S")
+        weigh(3)
         finish(2)
         dquant(3, 0, 4)
         kquant(24, 4)
         mm2(6)
-        dquant(3, 4, 6)
-        kquant(28, 2)
-        mm2(7, 0, 2)
-        dquant(3, 6, 8, from_gpsimd=True)
+        dquant(3, 4, 8)
         kquant(30, 2)
         mm2(7, 2, 4)
+        kquant(28, 2)
+        mm2(7, 0, 2)
         finish(3, 0, 4)
-        finish(3, 4, 6)
         finish(3, 6, 8)
+        finish(3, 4, 6)

@@ -75,6 +75,11 @@ def tile_dpfpattention_pb_kernel(tc, x, wv, beta, vo, k_bytes, k_scale, W, out):
                 out=kb[q][:], in_=k_bytes[b, h0 : h0 + 4].rearrange("h (p t) s -> p h (t s)", t=PACK)
             )
 
+        def load_first_k_pair(a):
+            nc.sync.dma_start(
+                out=kb[0][:, a : a + 2], in_=k_bytes[0, a : a + 2].rearrange("h (p t) s -> p h (t s)", t=PACK)
+            )
+
         def load_vo(q):
             b, c = batch_and_chunk(q)
             h0 = 4 * c
@@ -179,8 +184,11 @@ def tile_dpfpattention_pb_kernel(tc, x, wv, beta, vo, k_bytes, k_scale, W, out):
         xg_t = {}
         xt_t = {}
 
-        def xtrans(b, u, g):
-            xt = psx.tile([P, 2, 2, P], F32, name="xt")
+        def xtrans(b, u, g, spare_bank=False):
+            if spare_bank:
+                xt = pso.tile([P, 2, 2, P], F32, name="o")
+            else:
+                xt = psx.tile([P, 2, 2, P], F32, name="xt")
             xt_t[(b, u, g)] = xt
             for tt in range(2):
                 words = xr[b][u][:, tt, 512 * g : 512 * (g + 1)].bitcast(F32)
@@ -212,12 +220,12 @@ def tile_dpfpattention_pb_kernel(tc, x, wv, beta, vo, k_bytes, k_scale, W, out):
             for j in range(first, first + n):
                 wg_t[j] = (tile, first)
 
-        def wcopy(j, engine):
+        def wcopy(j, engine, a=0, e=QW):
             tile, first = wg_t[j]
             c, g = j // 2, j % 2
             part = min(c, 2)
-            rows = wr[part][:, g, :, QW * (c - part) : QW * (c - part + 1)]
-            interleave(engine, tile[:, QW * (j - first) : QW * (j - first + 1), :], rows)
+            rows = wr[part][:, g, :, QW * (c - part) + a : QW * (c - part) + e]
+            interleave(engine, tile[:, QW * (j - first) + a : QW * (j - first) + e, :], rows)
 
         def wcopy_chunk_on_gpsimd(c):
             tile, first = wg_t[2 * c]
@@ -299,21 +307,21 @@ def tile_dpfpattention_pb_kernel(tc, x, wv, beta, vo, k_bytes, k_scale, W, out):
                 op=MULT,
             )
 
-        factors = keep.tile([P, 2, PACK], F32, name="factors")
+        factors = [keep.tile([P, 2, PACK], F32, name="factors%d" % o) for o in range(QUADS // 2)]
         rest_t = {}
 
         def fetch_factors(o, a):
             nc.scalar.copy(
-                out=factors[:],
+                out=factors[o][:],
                 in_=bp_t[o // 2][:, :, o % 2, REP * a : REP * (a + 2) : REP].rearrange("p t h -> p h t"),
             )
 
-        def weigh_on_gpsimd(o, a, gate):
+        def weigh_on_gpsimd(o, a, gate=None):
             rest_t[o] = staging(2 * DH, gate)
             nc.gpsimd.tensor_tensor(
                 out=rest_t[o][:].rearrange("p (h d) t -> p h d t", h=2),
                 in0=tm_t[o][:, :, DH * a : DH * (a + 2)].rearrange("p t (h d) -> p h d t", h=2),
-                in1=factors[:].unsqueeze(2).to_broadcast([P, 2, DH, PACK]),
+                in1=factors[o][:].unsqueeze(2).to_broadcast([P, 2, DH, PACK]),
                 op=MULT,
             )
 
@@ -328,12 +336,12 @@ def tile_dpfpattention_pb_kernel(tc, x, wv, beta, vo, k_bytes, k_scale, W, out):
         o_t = {}
 
         def mm2(q, a=0, e=4):
-            if q % 2 == 0 and a == 0:
+            if q % 2 == 0 and q < QUADS - 2:
                 o_t[q] = pso.tile([P, 8, DH], F32, name="o")
                 o_t[q + 1] = o_t[q]
-            if q == QUADS - 1:
+            if q >= QUADS - 2:
                 o_t[(q, a)] = psv.tile([P, 8, DH], F32, name="v")
-            bank = o_t[(q, a)] if q == QUADS - 1 else o_t[q]
+            bank = o_t[(q, a)] if q >= QUADS - 2 else o_t[q]
             for h in range(a, e):
                 cols = slice(S * (4 * q + h), S * (4 * q + h + 1))
                 nc.tensor.matmul_mx(
@@ -348,14 +356,15 @@ def tile_dpfpattention_pb_kernel(tc, x, wv, beta, vo, k_bytes, k_scale, W, out):
 
         def finish(o, a=0, e=8):
             q = 2 * o + a // 4
-            bank = o_t[(q, a - 4)] if q == QUADS - 1 else o_t[q]
+            bank = o_t[(q, a % 4)] if q >= QUADS - 2 else o_t[q]
             nc.vector.tensor_tensor(out=ot[o][:, a:e, :], in0=bank[:, a:e, :], in1=wt[o][:, a:e, :], op=ADD)
             b, h0 = o % 2, 8 * (o // 2)
             nc.sync.dma_start(out=out[b, h0 + a : h0 + e].rearrange("h s d -> s h d"), in_=ot[o][:, a:e, :])
 
         constants()
         load_scale()
-        load_k(0)
+        load_first_k_pair(0)
+        load_first_k_pair(2)
         load_x(0, 0)
         load_beta()
         load_k(1)
@@ -375,12 +384,17 @@ def tile_dpfpattention_pb_kernel(tc, x, wv, beta, vo, k_bytes, k_scale, W, out):
         load_vo(3)
         load_k(3)
         load_k(4)
-        load_w(0)
         load_vo(4)
-        for q in range(5, QUADS):
-            load_k(q)
-            load_vo(q)
-            load_w(q - 4)
+        load_k(5)
+        load_vo(5)
+        load_w(0)
+        load_k(6)
+        load_vo(6)
+        load_vo(7)
+        load_k(7)
+        load_w(1)
+        load_w(2)
+        load_w(3)
 
         widen((0, 2), "V")
         widen((2, 2), "S")
@@ -460,49 +474,66 @@ def tile_dpfpattention_pb_kernel(tc, x, wv, beta, vo, k_bytes, k_scale, W, out):
             mm1(q, 0)
             mm1(q, 1)
         mm2(1)
-        for o in (2, 3):
-            first = 8 * o - 8
-            kstage(first, 8, gate="b")
-            kcopy((first, 6), "G")
-            widen((first + 6, 2), "S")
-            if o == 2:
-                widen((16, 6), "S", 0, 1)
-                kcopy((14, 2), "S")
-                widen((16, 6), "S", 1, 6)
-            else:
-                widen((24, 4), "S", 0, 1)
-                kcopy((22, 2), "S")
-                widen((24, 4), "S", 1, 4)
-                widen((29, 3), "S")
-                kstage(24, 4)
-                kcopy((24, 4), "S")
-                widen((28, 1), "S")
-            weigh(o - 1)
-            if o == 2:
-                bspread(1)
-            for q in (2 * o, 2 * o + 1):
-                subtract(q, 0)
-                subtract(q, 1)
-            finish(o - 2)
-            dquant(o - 1)
-            kquant(first, 8)
-            if o == 2:
-                for q in (6, 7):
-                    mm1(q, 0)
-                    mm1(q, 1)
-            mm2(2 * o - 2)
-            mm2(2 * o - 1)
-        kstage(28, 4, gate="b")
-        kcopy((29, 3), "G")
-        kcopy((28, 1), "S")
-        weigh(3)
+        kstage(8, 8, gate="b")
+        kcopy((8, 6), "G")
+        weigh(1)
+        bspread(1)
+        widen((14, 2), "S")
+        widen((16, 6), "S", 0, 1)
+        kcopy((14, 2), "S")
+        widen((16, 6), "S", 1, 5)
+        fetch_factors(3, 6)
+        widen((16, 6), "S", 5, 6)
+        for q in (4, 5):
+            subtract(q, 0)
+            subtract(q, 1)
+        finish(0)
+        dquant(1, 0, 4)
+        kquant(8, 8)
+        dquant(1, 4, 8)
+        for q in (6, 7):
+            mm1(q, 0)
+            mm1(q, 1)
+        mm2(2)
+        mm2(3)
+
+        kstage(16, 8, gate="b")
+        kcopy((16, 6), "G")
+        weigh(2)
+        widen((22, 2), "S")
+        kturn((22, 2))
+        widen((24, 2), "S")
+        kturn((24, 2))
+        widen((26, 2), "S")
+        kfetch((22, 2))
+        kturn((26, 2))
+        kstage(24, 4)
+        kfetch((24, 2))
+        widen((30, 2), "S")
+        kfetch((26, 2))
+        widen((28, 2), "S")
+        kstage(28, 4)
+        kcopy((30, 2), "S")
+        kcopy((28, 2), "S")
+        for q in (6, 7):
+            subtract(q, 0)
+            subtract(q, 1)
+        finish(1)
+        dquant(2, 0, 4)
+        kquant(16, 8)
+        dquant(2, 4, 8)
+        mm2(4)
+        mm2(5)
+        weigh_on_gpsimd(3, 6, "b")
+        weigh(3, 0, 6)
         finish(2)
         dquant(3, 0, 4)
         kquant(24, 4)
         mm2(6)
-        dquant(3, 4, 8)
+        dquant(3, 6, 8, from_gpsimd=True)
         kquant(30, 2)
         mm2(7, 2, 4)
+        dquant(3, 4, 6)
         kquant(28, 2)
         mm2(7, 0, 2)
         finish(3, 0, 4)

@@ -21,9 +21,13 @@ COPY = mybir.ActivationFunctionType.Copy
 P = 128
 PACK = 4
 QUADS = B * H // 4
+OCTETS = B * H // 8
 QW = 4 * DH
 WV_LOADS = ((0, QW), (QW, QW), (2 * QW, 2 * QW))
-REP = DH // 4
+COPY_RUN = 4
+BETA_RUN = 2
+REP = DH // BETA_RUN
+VECTOR, SCALAR, GPSIMD = "vector", "scalar", "gpsimd"
 
 
 def batch_and_chunk(q):
@@ -36,333 +40,357 @@ def tile_dpfpattention_pb_kernel(tc, x, wv, beta, vo, k_bytes, k_scale, W, out):
     with ExitStack() as ctx:
         keep = ctx.enter_context(tc.tile_pool(name="keep", bufs=1))
         work = ctx.enter_context(tc.tile_pool(name="work", bufs=4))
-        psx = ctx.enter_context(tc.psum_pool(name="psx", bufs=2))
-        psv = ctx.enter_context(tc.psum_pool(name="psv", bufs=4))
-        pso = ctx.enter_context(tc.psum_pool(name="pso", bufs=1))
-        psb = ctx.enter_context(tc.psum_pool(name="psb", bufs=1))
+        ps_turn = ctx.enter_context(tc.psum_pool(name="ps_turn", bufs=2))
+        ps_v = ctx.enter_context(tc.psum_pool(name="ps_v", bufs=4))
+        ps_out = ctx.enter_context(tc.psum_pool(name="ps_out", bufs=1))
+        ps_beta = ctx.enter_context(tc.psum_pool(name="ps_beta", bufs=1))
         ctx.enter_context(tc.manual_schedule())
 
-        ident = keep.tile([P, P], F32, name="ident")
-        identb = keep.tile([P, P], BF16, name="identb")
-        brow = keep.tile([P, N], BF16, name="brow")
-        pick = keep.tile([P, B * H, REP], BF16, name="pick")
-        ksc = keep.tile([P, PACK], F32, name="ksc")
-        xc = [[keep.tile([P, 2, 2 * P], U32, align_bytes=64, name="xc%d%d" % (b, u)) for u in range(2)] for b in range(B)]
-        xs = [[keep.tile([P, 2, 2 * P], U8, align_bytes=64, name="xs%d%d" % (b, u)) for u in range(2)] for b in range(B)]
-        wc = keep.tile([P, 8 * QW], U32, align_bytes=64, name="wc")
-        ws = keep.tile([P, 8 * QW], U8, align_bytes=64, name="ws")
-        kc = keep.tile([P, B * H * S], U32, align_bytes=64, name="kc")
-        ks = keep.tile([P, B * H * S], U8, align_bytes=64, name="ks")
-        dc = keep.tile([P, B * H * DH], U32, align_bytes=64, name="dc")
-        ds = keep.tile([P, B * H * DH], U8, align_bytes=64, name="ds")
-        kb = [keep.tile([P, 4, PACK * S], U8, name="kb%d" % q) for q in range(QUADS)]
-        vs = [keep.tile([P, 4, PACK, DH], BF16, name="vs%d" % q) for q in range(QUADS)]
-        wt = [keep.tile([P, 8, DH], BF16, name="wt%d" % o) for o in range(QUADS // 2)]
-        ot = [keep.tile([P, 8, DH], F32, name="ot%d" % o) for o in range(QUADS // 2)]
-        xr = [[keep.tile([P, 2, D], BF16, name="xr%d%d" % (b, u)) for u in range(2)] for b in range(B)]
-        wr = [keep.tile([P, 2, PACK, n], BF16, name="wr%d" % c0) for c0, n in WV_LOADS]
+        ident_f32 = keep.tile([P, P], F32, name="ident_f32")
+        ident_bf16 = keep.tile([P, P], BF16, name="ident_bf16")
+        beta_rows = keep.tile([P, N], BF16, name="beta_rows")
+        pick = [keep.tile([P, H, REP], BF16, name="pick%d" % b) for b in range(B)]
+        k_scales = keep.tile([P, PACK], F32, name="k_scales")
+        x_codes = [
+            [keep.tile([P, 2, 2 * P], U32, align_bytes=64, name="x_codes%d%d" % (b, u)) for u in range(2)]
+            for b in range(B)
+        ]
+        x_exps = [
+            [keep.tile([P, 2, 2 * P], U8, align_bytes=64, name="x_exps%d%d" % (b, u)) for u in range(2)]
+            for b in range(B)
+        ]
+        w_codes = keep.tile([P, 8 * QW], U32, align_bytes=64, name="w_codes")
+        w_exps = keep.tile([P, 8 * QW], U8, align_bytes=64, name="w_exps")
+        k_codes = keep.tile([P, B * H * S], U32, align_bytes=64, name="k_codes")
+        k_exps = keep.tile([P, B * H * S], U8, align_bytes=64, name="k_exps")
+        dv_codes = keep.tile([P, B * H * DH], U32, align_bytes=64, name="dv_codes")
+        dv_exps = keep.tile([P, B * H * DH], U8, align_bytes=64, name="dv_exps")
+        k_raw = [keep.tile([P, 4, PACK * S], U8, name="k_raw%d" % q) for q in range(QUADS)]
+        vo_sb = [keep.tile([P, 4, PACK, DH], BF16, name="vo_sb%d" % q) for q in range(QUADS)]
+        mem_sb = [keep.tile([P, 8, DH], BF16, name="mem_sb%d" % o) for o in range(OCTETS)]
+        out_sb = [keep.tile([P, 8, DH], F32, name="out_sb%d" % o) for o in range(OCTETS)]
+        x_sb = [[keep.tile([P, 2, D], BF16, name="x_sb%d%d" % (b, u)) for u in range(2)] for b in range(B)]
+        wv_sb = [keep.tile([P, 2, PACK, n], BF16, name="wv_sb%d" % c0) for c0, n in WV_LOADS]
 
-        def load_scale():
-            nc.sync.dma_start(out=ksc[:], in_=k_scale.rearrange("a c (p t) e -> p (a c t e)", t=PACK))
+
+        def load_k_scales():
+            nc.sync.dma_start(out=k_scales[:], in_=k_scale.rearrange("a c (p t) e -> p (a c t e)", t=PACK))
 
         def load_beta():
-            nc.sync.dma_start(out=brow[0 : B * H, :], in_=beta.rearrange("b h n -> (b h) n"))
+            nc.sync.dma_start(out=beta_rows[0 : B * H, :], in_=beta.rearrange("b h n -> (b h) n"))
 
         def load_k(q):
             b, c = batch_and_chunk(q)
-            h0 = 4 * c
             nc.sync.dma_start(
-                out=kb[q][:], in_=k_bytes[b, h0 : h0 + 4].rearrange("h (p t) s -> p h (t s)", t=PACK)
+                out=k_raw[q][:], in_=k_bytes[b, 4 * c : 4 * c + 4].rearrange("h (p t) s -> p h (t s)", t=PACK)
             )
 
         def load_first_k_pair(a):
             nc.sync.dma_start(
-                out=kb[0][:, a : a + 2], in_=k_bytes[0, a : a + 2].rearrange("h (p t) s -> p h (t s)", t=PACK)
+                out=k_raw[0][:, a : a + 2], in_=k_bytes[0, a : a + 2].rearrange("h (p t) s -> p h (t s)", t=PACK)
             )
 
         def load_vo(q):
             b, c = batch_and_chunk(q)
-            h0 = 4 * c
             nc.sync.dma_start(
-                out=vs[q][:].rearrange("p h t d -> p h (t d)"),
-                in_=vo[b, h0 : h0 + 4].rearrange("h (p t) d -> p h (t d)", t=PACK),
+                out=vo_sb[q][:].rearrange("p h t d -> p h (t d)"),
+                in_=vo[b, 4 * c : 4 * c + 4].rearrange("h (p t) d -> p h (t d)", t=PACK),
             )
 
         def load_x(b, u):
             nc.sync.dma_start(
-                out=xr[b][u][:], in_=x[b].rearrange("(m t) k -> m t k", t=PACK)[:, 2 * u : 2 * u + 2, :]
+                out=x_sb[b][u][:], in_=x[b].rearrange("(m t) k -> m t k", t=PACK)[:, 2 * u : 2 * u + 2, :]
             )
 
         def load_wv(part, g):
             c0, n = WV_LOADS[part]
             nc.sync.dma_start(
-                out=wr[part][:, g],
-                in_=wv.rearrange("(g p j) w -> g p j w", g=2, j=PACK)[g][:, :, c0 : c0 + n],
+                out=wv_sb[part][:, g],
+                in_=wv.rearrange("(g p t) w -> g p t w", g=2, t=PACK)[g][:, :, c0 : c0 + n],
             )
 
-        def load_w(o):
+        def load_memory(o):
             b, h0 = o % 2, 8 * (o // 2)
-            nc.sync.dma_start(out=wt[o][:], in_=W[b, h0 : h0 + 8].rearrange("h s d -> s h d"))
+            nc.sync.dma_start(out=mem_sb[o][:], in_=W[b, h0 : h0 + 8].rearrange("h s d -> s h d"))
 
-        def constants():
-            make_identity(nc, identb[:])
-            make_identity(nc, ident[:])
-            nc.vector.memset(brow[32:64, :], 0.0)
-            nc.vector.memset(brow[64:128, :], 0.0)
+        def make_constants():
+            make_identity(nc, ident_bf16[:])
+            make_identity(nc, ident_f32[:])
+            nc.vector.memset(beta_rows[32:64, :], 0.0)
+            nc.vector.memset(beta_rows[64:128, :], 0.0)
             nc.scalar.activation(
-                out=pick[:], in_=identb[:, 0 : B * H].unsqueeze(2).to_broadcast([P, B * H, REP]), func=COPY
+                out=pick[0][:], in_=ident_bf16[:, 0:H].unsqueeze(2).to_broadcast([P, H, REP]), func=COPY
             )
+            nc.vector.tensor_copy(
+                out=pick[1][:], in_=ident_bf16[:, H : 2 * H].unsqueeze(2).to_broadcast([P, H, REP])
+            )
+
 
         def staging(columns, gate):
             if gate:
                 return work.tile([P, columns, PACK], BF16, align_bytes=64, name="gate_" + gate, bufs=1)
             return work.tile([P, columns, PACK], BF16, align_bytes=64, name="stage%d" % columns, bufs=4)
 
-        kw_t = {}
-        kg_t = {}
-
-        def widen(group, engine, a=0, e=None):
-            first, n = group
-            if first not in kw_t:
-                kw_t[first] = work.tile([P, PACK, n, S], BF16, name="kw%d" % n, bufs=2 if n > 2 else 4)
-            for h in range(a, n if e is None else e):
-                for t in range(PACK):
-                    codes = kb[(first + h) // 4][:, (first + h) % 4, S * t : S * (t + 1)].bitcast(FP8)
-                    dst = kw_t[first][:, t, h, :]
-                    if engine == "V":
-                        nc.vector.tensor_scalar(out=dst, in0=codes, scalar1=ksc[:, t : t + 1], scalar2=None, op0=MULT)
-                    else:
-                        nc.scalar.activation(out=dst, in_=codes, func=COPY, scale=ksc[:, t : t + 1])
-
         def interleave(engine, dst, src):
-            if engine == "G":
+            if engine == GPSIMD:
                 nc.gpsimd.tensor_scalar(
                     out=dst, in0=src.rearrange("p t n -> p n t"), scalar1=1.0, scalar2=0.0, op0=MULT, op1=ADD
                 )
                 return
-            copy = nc.vector.tensor_copy if engine == "V" else nc.scalar.copy
-            copy(out=dst.rearrange("p (c i) t -> p c t i", i=4), in_=src.rearrange("p t (c i) -> p c t i", i=4))
+            copy = nc.vector.tensor_copy if engine == VECTOR else nc.scalar.copy
+            copy(
+                out=dst.rearrange("p (c i) t -> p c t i", i=COPY_RUN),
+                in_=src.rearrange("p t (c i) -> p c t i", i=COPY_RUN),
+            )
 
-        def kstage(first, n, gate=None):
+
+        k_planar = {}
+        k_staging = {}
+        k_banks = {}
+
+        def widen_k(group, engine, a=0, e=None):
+            first, n = group
+            if first not in k_planar:
+                k_planar[first] = work.tile([P, PACK, n, S], BF16, name="k_planar%d" % n, bufs=2 if n > 2 else 4)
+            for h in range(a, n if e is None else e):
+                for t in range(PACK):
+                    codes = k_raw[(first + h) // 4][:, (first + h) % 4, S * t : S * (t + 1)].bitcast(FP8)
+                    dst = k_planar[first][:, t, h, :]
+                    if engine == VECTOR:
+                        nc.vector.tensor_scalar(
+                            out=dst, in0=codes, scalar1=k_scales[:, t : t + 1], scalar2=None, op0=MULT
+                        )
+                    else:
+                        nc.scalar.activation(out=dst, in_=codes, func=COPY, scale=k_scales[:, t : t + 1])
+
+        def stage_k(first, n, gate=None):
             tile = staging(n * S, gate)
             for h in range(first, first + n):
-                kg_t[h] = (tile, first)
+                k_staging[h] = (tile, first)
 
-        def kstaged(first, n):
-            tile, base = kg_t[first]
+        def staged_k(first, n):
+            tile, base = k_staging[first]
             return tile[:, S * (first - base) : S * (first - base + n), :]
 
-        def kcopy(group, engine):
+        def interleave_k(group, engine):
             first, n = group
-            interleave(engine, kstaged(first, n), kw_t[first][:].rearrange("p t h s -> p t (h s)"))
+            interleave(engine, staged_k(first, n), k_planar[first][:].rearrange("p t h s -> p t (h s)"))
 
-        turned_t = {}
-
-        def kturn(group):
+        def interleave_k_on_tensor(group):
             first, n = group
-            bank = psx.tile([P, n * S, PACK], BF16, name="xt")
-            turned_t[first] = bank
+            bank = ps_turn.tile([P, n * S, PACK], BF16, name="turned")
+            k_banks[first] = bank
             for h in range(n):
                 nc.tensor.matmul(
                     bank[:, S * h : S * (h + 1), :].rearrange("p s t -> p t s"),
-                    lhsT=identb[:],
-                    rhs=kw_t[first][:, :, h, :],
+                    lhsT=ident_bf16[:],
+                    rhs=k_planar[first][:, :, h, :],
                     start=True,
                     stop=True,
                 )
 
-        def kfetch(group):
+        def fetch_k(group):
             first, n = group
-            nc.scalar.copy(out=kstaged(first, n), in_=turned_t[first][:])
+            nc.scalar.copy(out=staged_k(first, n), in_=k_banks[first][:])
 
-        def kquant(first, n):
+        def quantise_k(first, n):
             cols = slice(S * first, S * (first + n))
             nc.vector.quantize_mx(
-                out=kc[:, cols].bitcast(FP8X4), scales=ks[:, cols], in_=kstaged(first, n).rearrange("p n t -> p (n t)")
+                out=k_codes[:, cols].bitcast(FP8X4),
+                scales=k_exps[:, cols],
+                in_=staged_k(first, n).rearrange("p n t -> p (n t)"),
             )
 
-        xg_t = {}
-        xt_t = {}
 
-        def xtrans(b, u, g, spare_bank=False):
-            if spare_bank:
-                xt = pso.tile([P, 2, 2, P], F32, name="o")
-            else:
-                xt = psx.tile([P, 2, 2, P], F32, name="xt")
-            xt_t[(b, u, g)] = xt
+        x_staging = {}
+        x_banks = {}
+
+        def turn_x(b, u, g):
+            bank = ps_turn.tile([P, 2, 2, P], F32, name="turned")
+            x_banks[(b, u, g)] = bank
             for tt in range(2):
-                words = xr[b][u][:, tt, 512 * g : 512 * (g + 1)].bitcast(F32)
+                words = x_sb[b][u][:, tt, 512 * g : 512 * (g + 1)].bitcast(F32)
                 for e in range(2):
-                    nc.tensor.transpose(xt[:, tt, e, :], words[:, e::2], ident[:])
+                    nc.tensor.transpose(bank[:, tt, e, :], words[:, e::2], ident_f32[:])
 
-        def xcopy(b, u, g, gate=None):
+        def fetch_x(b, u, g, gate=None):
             if g == 0:
-                xg_t[(b, u)] = staging(N, gate)
+                x_staging[(b, u)] = staging(N, gate)
             nc.scalar.copy(
-                out=xg_t[(b, u)][:, 2 * P * g : 2 * P * (g + 1), :]
+                out=x_staging[(b, u)][:, 2 * P * g : 2 * P * (g + 1), :]
                 .rearrange("p n j -> p (n j)")
                 .bitcast(F32)
                 .rearrange("p (t m e) -> p t m e", t=2, e=2),
-                in_=xt_t[(b, u, g)][:].rearrange("p t e m -> p t m e"),
+                in_=x_banks[(b, u, g)][:].rearrange("p t e m -> p t m e"),
             )
 
-        def xquant(b, u):
+        def quantise_x(b, u):
             nc.vector.quantize_mx(
-                out=xc[b][u][:].rearrange("p g n -> p (g n)").bitcast(FP8X4),
-                scales=xs[b][u][:].rearrange("p g n -> p (g n)"),
-                in_=xg_t[(b, u)][:].rearrange("p n j -> p (n j)"),
+                out=x_codes[b][u][:].rearrange("p g n -> p (g n)").bitcast(FP8X4),
+                scales=x_exps[b][u][:].rearrange("p g n -> p (g n)"),
+                in_=x_staging[(b, u)][:].rearrange("p n j -> p (n j)"),
             )
 
-        wg_t = {}
 
-        def wstage(first, n, gate=None):
+        w_staging = {}
+
+        def stage_wv(first, n, gate=None):
             tile = staging(n * QW, gate)
             for j in range(first, first + n):
-                wg_t[j] = (tile, first)
+                w_staging[j] = (tile, first)
 
-        def wcopy(j, engine, a=0, e=QW):
-            tile, first = wg_t[j]
+        def interleave_wv(j, engine):
+            tile, first = w_staging[j]
             c, g = j // 2, j % 2
             part = min(c, 2)
-            rows = wr[part][:, g, :, QW * (c - part) + a : QW * (c - part) + e]
-            interleave(engine, tile[:, QW * (j - first) + a : QW * (j - first) + e, :], rows)
+            rows = wv_sb[part][:, g, :, QW * (c - part) : QW * (c - part + 1)]
+            interleave(engine, tile[:, QW * (j - first) : QW * (j - first + 1), :], rows)
 
-        def wcopy_chunk_on_gpsimd(c):
-            tile, first = wg_t[2 * c]
+        def interleave_wv_chunk_on_gpsimd(c):
+            tile, first = w_staging[2 * c]
             part = min(c, 2)
             nc.gpsimd.tensor_scalar(
-                out=tile[:, QW * (2 * c - first) : QW * (2 * c - first + 2), :].rearrange("p (g n) j -> p g n j", g=2),
-                in0=wr[part][:, :, :, QW * (c - part) : QW * (c - part + 1)].rearrange("p g j n -> p g n j"),
+                out=tile[:, QW * (2 * c - first) : QW * (2 * c - first + 2), :].rearrange("p (g n) t -> p g n t", g=2),
+                in0=wv_sb[part][:, :, :, QW * (c - part) : QW * (c - part + 1)].rearrange("p g t n -> p g n t"),
                 scalar1=1.0,
                 scalar2=0.0,
                 op0=MULT,
                 op1=ADD,
             )
 
-        def wquant(j, n):
-            tile, first = wg_t[j]
+        def quantise_wv(j, n):
+            tile, first = w_staging[j]
             cols = slice(QW * j, QW * (j + n))
             nc.vector.quantize_mx(
-                out=wc[:, cols].bitcast(FP8X4),
-                scales=ws[:, cols],
-                in_=tile[:, QW * (j - first) : QW * (j - first + n), :].rearrange("p n j -> p (n j)"),
+                out=w_codes[:, cols].bitcast(FP8X4),
+                scales=w_exps[:, cols],
+                in_=tile[:, QW * (j - first) : QW * (j - first + n), :].rearrange("p n t -> p (n t)"),
             )
 
-        bp_t = {}
 
-        def bspread(half):
-            bp = psb.tile([P, PACK, B, 8 * REP], BF16, name="bp")
-            bp_t[half] = bp
+        beta_banks = {}
+
+        def spread_beta(o):
+            bank = ps_beta.tile([P, PACK, 8 * REP], BF16, name="beta_bank")
+            beta_banks[o] = bank
+            b, h0 = o % 2, 8 * (o // 2)
             for t in range(PACK):
                 nc.tensor.matmul(
-                    bp[:, t],
-                    lhsT=brow[:, t::PACK],
-                    rhs=pick[:].rearrange("p (b h) c -> p b (h c)", b=B)[:, :, 8 * REP * half : 8 * REP * (half + 1)],
+                    bank[:, t],
+                    lhsT=beta_rows[:, t::PACK],
+                    rhs=pick[b][:, h0 : h0 + 8].rearrange("p h c -> p (h c)"),
                     start=True,
                     stop=True,
                 )
 
-        v_t = {}
+        v_banks = {}
 
-        def mm1(q, u):
+        def first_product(q, u):
             b, c = batch_and_chunk(q)
-            v = psv.tile([P, 2, QW], F32, name="v")
-            v_t[(q, u)] = v
+            bank = ps_v.tile([P, 2, QW], F32, name="v_bank")
+            v_banks[(q, u)] = bank
             for tt in range(2):
                 for g in range(2):
                     nc.tensor.matmul_mx(
-                        out=v[:, tt, :],
-                        lhsT=xc[b][u][:, g, P * tt : P * (tt + 1)].bitcast(FP8X4),
-                        lhsT_scale=xs[b][u][:, g, P * tt : P * (tt + 1)],
-                        rhs=wc[:, QW * (2 * c + g) : QW * (2 * c + g + 1)].bitcast(FP8X4),
-                        rhs_scale=ws[:, QW * (2 * c + g) : QW * (2 * c + g + 1)],
+                        out=bank[:, tt, :],
+                        lhsT=x_codes[b][u][:, g, P * tt : P * (tt + 1)].bitcast(FP8X4),
+                        lhsT_scale=x_exps[b][u][:, g, P * tt : P * (tt + 1)],
+                        rhs=w_codes[:, QW * (2 * c + g) : QW * (2 * c + g + 1)].bitcast(FP8X4),
+                        rhs_scale=w_exps[:, QW * (2 * c + g) : QW * (2 * c + g + 1)],
                         start=(g == 0),
                         stop=(g == 1),
                     )
 
-        tm_t = {}
-        dg_t = {}
+        diff = {}
+        dv_staging = {}
 
-        def subtract(q, u):
+        def subtract_vo(q, u):
             o = q // 2
-            if o not in tm_t:
-                tm_t[o] = work.tile([P, PACK, 2 * QW], F32, name="tm", bufs=2)
+            if o not in diff:
+                diff[o] = work.tile([P, PACK, 2 * QW], F32, name="diff", bufs=2)
             nc.vector.tensor_tensor(
-                out=tm_t[o][:, 2 * u : 2 * u + 2, QW * (q % 2) : QW * (q % 2 + 1)].rearrange("p t (h d) -> p t h d", h=4),
-                in0=v_t[(q, u)][:].rearrange("p t (h d) -> p t h d", h=4),
-                in1=vs[q][:, :, 2 * u : 2 * u + 2, :].rearrange("p h t d -> p t h d"),
+                out=diff[o][:, 2 * u : 2 * u + 2, QW * (q % 2) : QW * (q % 2 + 1)].rearrange(
+                    "p t (h d) -> p t h d", h=4
+                ),
+                in0=v_banks[(q, u)][:].rearrange("p t (h d) -> p t h d", h=4),
+                in1=vo_sb[q][:, :, 2 * u : 2 * u + 2, :].rearrange("p h t d -> p t h d"),
                 op=SUB,
             )
 
-        def weigh(o, a=0, e=8):
-            if o not in dg_t:
-                dg_t[o] = work.tile([P, 8, DH, PACK], BF16, align_bytes=64, name="dg", bufs=2)
+        def times_beta(o, a=0, e=8):
+            if o not in dv_staging:
+                dv_staging[o] = work.tile([P, 8, DH, PACK], BF16, align_bytes=64, name="dv_staging", bufs=2)
             nc.vector.tensor_tensor(
-                out=dg_t[o][:, a:e].rearrange("p h (c i) t -> p (h c) t i", i=4),
-                in0=tm_t[o][:, :, DH * a : DH * e].rearrange("p t (c i) -> p c t i", i=4),
-                in1=bp_t[o // 2][:, :, o % 2, REP * a : REP * e]
+                out=dv_staging[o][:, a:e].rearrange("p h (c i) t -> p (h c) t i", i=BETA_RUN),
+                in0=diff[o][:, :, DH * a : DH * e].rearrange("p t (c i) -> p c t i", i=BETA_RUN),
+                in1=beta_banks[o][:, :, REP * a : REP * e]
                 .rearrange("p t c -> p c t")
                 .unsqueeze(3)
-                .to_broadcast([P, (e - a) * REP, PACK, 4]),
+                .to_broadcast([P, (e - a) * REP, PACK, BETA_RUN]),
                 op=MULT,
             )
 
-        factors = [keep.tile([P, 2, PACK], F32, name="factors%d" % o) for o in range(QUADS // 2)]
-        rest_t = {}
-
-        def fetch_factors(o, a):
-            nc.scalar.copy(
-                out=factors[o][:],
-                in_=bp_t[o // 2][:, :, o % 2, REP * a : REP * (a + 2) : REP].rearrange("p t h -> p h t"),
-            )
-
-        def weigh_on_gpsimd(o, a, gate=None):
-            rest_t[o] = staging(2 * DH, gate)
-            nc.gpsimd.tensor_tensor(
-                out=rest_t[o][:].rearrange("p (h d) t -> p h d t", h=2),
-                in0=tm_t[o][:, :, DH * a : DH * (a + 2)].rearrange("p t (h d) -> p h d t", h=2),
-                in1=factors[o][:].unsqueeze(2).to_broadcast([P, 2, DH, PACK]),
-                op=MULT,
-            )
-
-        def dquant(o, a=0, e=8, from_gpsimd=False):
+        def quantise_dv_from(o, a, e, values):
             cols = slice(DH * (8 * o + a), DH * (8 * o + e))
-            if from_gpsimd:
-                values = rest_t[o][:].rearrange("p n t -> p (n t)")
-            else:
-                values = dg_t[o][:, a:e].rearrange("p h d t -> p (h d t)")
-            nc.vector.quantize_mx(out=dc[:, cols].bitcast(FP8X4), scales=ds[:, cols], in_=values)
+            nc.vector.quantize_mx(out=dv_codes[:, cols].bitcast(FP8X4), scales=dv_exps[:, cols], in_=values)
 
-        o_t = {}
+        def quantise_dv(o, a, e):
+            quantise_dv_from(o, a, e, dv_staging[o][:, a:e].rearrange("p h d t -> p (h d t)"))
 
-        def mm2(q, a=0, e=4):
-            if q % 2 == 0 and q < QUADS - 2:
-                o_t[q] = pso.tile([P, 8, DH], F32, name="o")
-                o_t[q + 1] = o_t[q]
+        last_beta = keep.tile([P, 2, PACK], F32, name="last_beta")
+        last_octet, last_pair = OCTETS - 1, 6
+
+        def fetch_last_beta():
+            nc.scalar.copy(
+                out=last_beta[:],
+                in_=beta_banks[last_octet][:, :, REP * last_pair : REP * (last_pair + 2) : REP].rearrange(
+                    "p t h -> p h t"
+                ),
+            )
+
+        def times_last_beta_on_gpsimd(gate):
+            tile = staging(2 * DH, gate)
+            nc.gpsimd.tensor_tensor(
+                out=tile[:].rearrange("p (h d) t -> p h d t", h=2),
+                in0=diff[last_octet][:, :, DH * last_pair : DH * (last_pair + 2)].rearrange(
+                    "p t (h d) -> p h d t", h=2
+                ),
+                in1=last_beta[:].unsqueeze(2).to_broadcast([P, 2, DH, PACK]),
+                op=MULT,
+            )
+            return tile
+
+
+        out_banks = {}
+
+        def second_product(q, a=0, e=4):
             if q >= QUADS - 2:
-                o_t[(q, a)] = psv.tile([P, 8, DH], F32, name="v")
-            bank = o_t[(q, a)] if q >= QUADS - 2 else o_t[q]
+                out_banks[(q, a)] = ps_v.tile([P, 8, DH], F32, name="v_bank")
+            elif q % 2 == 0:
+                out_banks[(q, a)] = ps_out.tile([P, 8, DH], F32, name="out_bank")
+                out_banks[(q + 1, a)] = out_banks[(q, a)]
             for h in range(a, e):
-                cols = slice(S * (4 * q + h), S * (4 * q + h + 1))
+                head = 4 * q + h
                 nc.tensor.matmul_mx(
-                    out=bank[:, 4 * (q % 2) + h, :],
-                    lhsT=kc[:, cols].bitcast(FP8X4),
-                    lhsT_scale=ks[:, cols],
-                    rhs=dc[:, DH * (4 * q + h) : DH * (4 * q + h + 1)].bitcast(FP8X4),
-                    rhs_scale=ds[:, DH * (4 * q + h) : DH * (4 * q + h + 1)],
+                    out=out_banks[(q, a)][:, 4 * (q % 2) + h, :],
+                    lhsT=k_codes[:, S * head : S * (head + 1)].bitcast(FP8X4),
+                    lhsT_scale=k_exps[:, S * head : S * (head + 1)],
+                    rhs=dv_codes[:, DH * head : DH * (head + 1)].bitcast(FP8X4),
+                    rhs_scale=dv_exps[:, DH * head : DH * (head + 1)],
                     start=True,
                     stop=True,
                 )
 
-        def finish(o, a=0, e=8):
-            q = 2 * o + a // 4
-            bank = o_t[(q, a % 4)] if q >= QUADS - 2 else o_t[q]
-            nc.vector.tensor_tensor(out=ot[o][:, a:e, :], in0=bank[:, a:e, :], in1=wt[o][:, a:e, :], op=ADD)
+        def add_memory_and_store(o, a=0, e=8):
+            bank = out_banks[(2 * o + a // 4, a % 4)]
+            nc.vector.tensor_tensor(out=out_sb[o][:, a:e, :], in0=bank[:, a:e, :], in1=mem_sb[o][:, a:e, :], op=ADD)
             b, h0 = o % 2, 8 * (o // 2)
-            nc.sync.dma_start(out=out[b, h0 + a : h0 + e].rearrange("h s d -> s h d"), in_=ot[o][:, a:e, :])
+            nc.sync.dma_start(out=out[b, h0 + a : h0 + e].rearrange("h s d -> s h d"), in_=out_sb[o][:, a:e, :])
 
-        constants()
-        load_scale()
+
+        make_constants()
+
+        load_k_scales()
         load_first_k_pair(0)
         load_first_k_pair(2)
         load_x(0, 0)
@@ -383,159 +411,159 @@ def tile_dpfpattention_pb_kernel(tc, x, wv, beta, vo, k_bytes, k_scale, W, out):
         load_wv(2, 1)
         load_vo(3)
         load_k(3)
-        load_k(4)
-        load_vo(4)
-        load_k(5)
-        load_vo(5)
-        load_w(0)
+        for q in (4, 5):
+            load_k(q)
+            load_vo(q)
+        load_memory(0)
         load_k(6)
         load_vo(6)
         load_vo(7)
         load_k(7)
-        load_w(1)
-        load_w(2)
-        load_w(3)
+        for o in range(1, OCTETS):
+            load_memory(o)
 
-        widen((0, 2), "V")
-        widen((2, 2), "S")
-        kstage(0, 4)
-        kcopy((0, 2), "V")
-        xtrans(0, 0, 0)
-        xtrans(0, 0, 1)
-        xcopy(0, 0, 0)
-        xcopy(0, 0, 1)
-        kcopy((2, 2), "V")
-        wstage(0, 2)
-        wcopy(0, "V")
-        kquant(0, 4)
-        xquant(0, 0)
-        widen((4, 2), "S")
-        xtrans(0, 1, 0)
-        xtrans(0, 1, 1)
-        xcopy(0, 1, 0)
-        xcopy(0, 1, 1)
-        wcopy(1, "V")
-        kstage(4, 2)
-        kcopy((4, 2), "V")
-        wquant(0, 2)
-        bspread(0)
-        mm1(0, 0)
-        xquant(0, 1)
-        mm1(0, 1)
-        kquant(4, 2)
-        wstage(2, 2, gate="a")
-        wcopy(2, "S")
-        wcopy(3, "S")
-        widen((6, 2), "S")
-        subtract(0, 0)
-        subtract(0, 1)
-        wquant(2, 2)
-        xtrans(1, 0, 0)
-        xtrans(1, 0, 1)
-        mm1(1, 0)
-        mm1(1, 1)
-        xcopy(1, 0, 0)
-        xcopy(1, 0, 1)
+        widen_k((0, 2), VECTOR)
+        widen_k((2, 2), SCALAR)
+        stage_k(0, 4)
+        interleave_k((0, 2), VECTOR)
+        for g in range(2):
+            turn_x(0, 0, g)
+        for g in range(2):
+            fetch_x(0, 0, g)
+        interleave_k((2, 2), VECTOR)
+        stage_wv(0, 2)
+        interleave_wv(0, VECTOR)
+        quantise_k(0, 4)
+        quantise_x(0, 0)
+        widen_k((4, 2), SCALAR)
+        for g in range(2):
+            turn_x(0, 1, g)
+        for g in range(2):
+            fetch_x(0, 1, g)
+        interleave_wv(1, VECTOR)
+        stage_k(4, 2)
+        interleave_k((4, 2), VECTOR)
+        quantise_wv(0, 2)
+        spread_beta(0)
+        first_product(0, 0)
+        quantise_x(0, 1)
+        first_product(0, 1)
+        quantise_k(4, 2)
+        stage_wv(2, 2, gate="a")
+        interleave_wv(2, SCALAR)
+        interleave_wv(3, SCALAR)
+        widen_k((6, 2), SCALAR)
+        for u in range(2):
+            subtract_vo(0, u)
+        quantise_wv(2, 2)
+        for g in range(2):
+            turn_x(1, 0, g)
+        for u in range(2):
+            first_product(1, u)
+        for g in range(2):
+            fetch_x(1, 0, g)
 
-        kstage(6, 2, gate="a")
-        kcopy((6, 2), "G")
-        xtrans(1, 1, 0)
-        xtrans(1, 1, 1)
-        widen((8, 6), "S", 0, 1)
-        xcopy(1, 1, 0, gate="b")
-        xcopy(1, 1, 1)
-        widen((8, 6), "S", 1, 3)
-        weigh(0, 0, 4)
-        subtract(1, 0)
-        subtract(1, 1)
-        xquant(1, 0)
-        mm1(2, 0)
-        mm1(3, 0)
-        kquant(6, 2)
-        dquant(0, 0, 4)
-        xquant(1, 1)
-        mm1(2, 1)
-        mm1(3, 1)
-        mm2(0)
+        stage_k(6, 2, gate="a")
+        interleave_k((6, 2), GPSIMD)
+        for g in range(2):
+            turn_x(1, 1, g)
+        widen_k((8, 6), SCALAR, 0, 1)
+        fetch_x(1, 1, 0, gate="b")
+        fetch_x(1, 1, 1)
+        widen_k((8, 6), SCALAR, 1, 3)
+        times_beta(0, 0, 4)
+        for u in range(2):
+            subtract_vo(1, u)
+        quantise_x(1, 0)
+        for q in (2, 3):
+            first_product(q, 0)
+        quantise_k(6, 2)
+        quantise_dv(0, 0, 4)
+        quantise_x(1, 1)
+        for q in (2, 3):
+            first_product(q, 1)
+        second_product(0)
 
-        wstage(4, 4, gate="b")
-        wcopy_chunk_on_gpsimd(3)
-        wcopy(4, "S")
-        wcopy(5, "S")
-        widen((8, 6), "S", 3, 6)
-        weigh(0, 4, 8)
-        subtract(2, 0)
-        subtract(3, 0)
-        subtract(2, 1)
-        subtract(3, 1)
-        dquant(0, 4, 8)
-        wquant(4, 4)
+        stage_wv(4, 4, gate="b")
+        interleave_wv_chunk_on_gpsimd(3)
+        interleave_wv(4, SCALAR)
+        interleave_wv(5, SCALAR)
+        widen_k((8, 6), SCALAR, 3, 6)
+        times_beta(0, 4, 8)
+        spread_beta(1)
+        for u in range(2):
+            for q in (2, 3):
+                subtract_vo(q, u)
+        quantise_dv(0, 4, 8)
+        quantise_wv(4, 4)
         for q in (4, 5):
-            mm1(q, 0)
-            mm1(q, 1)
-        mm2(1)
-        kstage(8, 8, gate="b")
-        kcopy((8, 6), "G")
-        weigh(1)
-        bspread(1)
-        widen((14, 2), "S")
-        widen((16, 6), "S", 0, 1)
-        kcopy((14, 2), "S")
-        widen((16, 6), "S", 1, 5)
-        fetch_factors(3, 6)
-        widen((16, 6), "S", 5, 6)
-        for q in (4, 5):
-            subtract(q, 0)
-            subtract(q, 1)
-        finish(0)
-        dquant(1, 0, 4)
-        kquant(8, 8)
-        dquant(1, 4, 8)
-        for q in (6, 7):
-            mm1(q, 0)
-            mm1(q, 1)
-        mm2(2)
-        mm2(3)
+            for u in range(2):
+                first_product(q, u)
+        second_product(1)
 
-        kstage(16, 8, gate="b")
-        kcopy((16, 6), "G")
-        weigh(2)
-        widen((22, 2), "S")
-        kturn((22, 2))
-        widen((24, 2), "S")
-        kturn((24, 2))
-        widen((26, 2), "S")
-        kfetch((22, 2))
-        kturn((26, 2))
-        kstage(24, 4)
-        kfetch((24, 2))
-        widen((30, 2), "S")
-        kfetch((26, 2))
-        widen((28, 2), "S")
-        kstage(28, 4)
-        kcopy((30, 2), "S")
-        kcopy((28, 2), "S")
+        stage_k(8, 8, gate="b")
+        interleave_k((8, 6), GPSIMD)
+        times_beta(1)
+        spread_beta(2)
+        widen_k((14, 2), SCALAR)
+        widen_k((16, 6), SCALAR, 0, 1)
+        interleave_k((14, 2), SCALAR)
+        widen_k((16, 6), SCALAR, 1, 6)
+        for q in (4, 5):
+            for u in range(2):
+                subtract_vo(q, u)
+        add_memory_and_store(0)
+        quantise_dv(1, 0, 4)
+        quantise_k(8, 8)
+        quantise_dv(1, 4, 8)
         for q in (6, 7):
-            subtract(q, 0)
-            subtract(q, 1)
-        finish(1)
-        dquant(2, 0, 4)
-        kquant(16, 8)
-        dquant(2, 4, 8)
-        mm2(4)
-        mm2(5)
-        weigh_on_gpsimd(3, 6, "b")
-        weigh(3, 0, 6)
-        finish(2)
-        dquant(3, 0, 4)
-        kquant(24, 4)
-        mm2(6)
-        dquant(3, 6, 8, from_gpsimd=True)
-        kquant(30, 2)
-        mm2(7, 2, 4)
-        dquant(3, 4, 6)
-        kquant(28, 2)
-        mm2(7, 0, 2)
-        finish(3, 0, 4)
-        finish(3, 6, 8)
-        finish(3, 4, 6)
+            for u in range(2):
+                first_product(q, u)
+        for q in (2, 3):
+            second_product(q)
+
+        stage_k(16, 8, gate="b")
+        interleave_k((16, 6), GPSIMD)
+        times_beta(2)
+        for first in (22, 24):
+            widen_k((first, 2), SCALAR)
+            interleave_k_on_tensor((first, 2))
+        spread_beta(3)
+        widen_k((26, 2), SCALAR)
+        fetch_k((22, 2))
+        interleave_k_on_tensor((26, 2))
+        widen_k((30, 2), SCALAR)
+        stage_k(24, 4)
+        fetch_k((24, 2))
+        fetch_last_beta()
+        widen_k((28, 2), SCALAR)
+        fetch_k((26, 2))
+        stage_k(28, 4)
+        interleave_k((30, 2), SCALAR)
+        interleave_k((28, 2), SCALAR)
+        for q in (6, 7):
+            for u in range(2):
+                subtract_vo(q, u)
+        add_memory_and_store(1)
+        quantise_dv(2, 0, 4)
+        quantise_k(16, 8)
+        quantise_dv(2, 4, 8)
+        for q in (4, 5):
+            second_product(q)
+
+        last_dv = times_last_beta_on_gpsimd("b")
+        times_beta(3, 0, last_pair)
+        add_memory_and_store(2)
+
+        quantise_dv(3, 0, 4)
+        quantise_k(24, 4)
+        second_product(6)
+        quantise_dv_from(last_octet, last_pair, 8, last_dv[:].rearrange("p n t -> p (n t)"))
+        quantise_k(30, 2)
+        second_product(7, 2, 4)
+        quantise_dv(3, 4, 6)
+        quantise_k(28, 2)
+        second_product(7, 0, 2)
+        add_memory_and_store(3, 0, 4)
+        add_memory_and_store(3, 6, 8)
+        add_memory_and_store(3, 4, 6)

@@ -151,7 +151,7 @@ def tile_dpfpattention_pb_kernel(tc, x, wv, beta, vo, k_bytes, k_scale, W, out):
         def widen_k(group, engine, a=0, e=None):
             first, n = group
             if first not in k_planar:
-                k_planar[first] = work.tile([P, PACK, n, S], BF16, name="k_planar%d" % n, bufs=2 if n > 2 else 4)
+                k_planar[first] = work.tile([P, PACK, n, S], BF16, name="k_planar%d" % n, bufs=2 if n > 2 else 5)
             for h in range(a, n if e is None else e):
                 for t in range(PACK):
                     codes = k_raw[(first + h) // 4][:, (first + h) % 4, S * t : S * (t + 1)].bitcast(FP8)
@@ -163,18 +163,22 @@ def tile_dpfpattention_pb_kernel(tc, x, wv, beta, vo, k_bytes, k_scale, W, out):
                     else:
                         nc.scalar.activation(out=dst, in_=codes, func=COPY, scale=k_scales[:, t : t + 1])
 
-        def stage_k(first, n, gate=None):
-            tile = staging(n * S, gate)
+        def stage_k(first, n, gate=None, spare=0):
+            tile = staging(n * S + spare, gate)
             for h in range(first, first + n):
                 k_staging[h] = (tile, first)
+            return tile[:, n * S :, :]
 
         def staged_k(first, n):
             tile, base = k_staging[first]
             return tile[:, S * (first - base) : S * (first - base + n), :]
 
-        def interleave_k(group, engine):
+        def interleave_k(group, engine, a=0, e=None):
             first, n = group
-            interleave(engine, staged_k(first, n), k_planar[first][:].rearrange("p t h s -> p t (h s)"))
+            e = n if e is None else e
+            interleave(
+                engine, staged_k(first + a, e - a), k_planar[first][:, :, a:e, :].rearrange("p t h s -> p t (h s)")
+            )
 
         def interleave_k_on_tensor(group):
             first, n = group
@@ -239,19 +243,40 @@ def tile_dpfpattention_pb_kernel(tc, x, wv, beta, vo, k_bytes, k_scale, W, out):
             for j in range(first, first + n):
                 w_staging[j] = (tile, first)
 
+        def wv_chunk(c):
+            part = min(c, 2)
+            return wv_sb[part][:, :, :, QW * (c - part) : QW * (c - part + 1)]
+
         def interleave_wv(j, engine):
             tile, first = w_staging[j]
             c, g = j // 2, j % 2
-            part = min(c, 2)
-            rows = wv_sb[part][:, g, :, QW * (c - part) : QW * (c - part + 1)]
+            rows = wv_chunk(c)[:, g]
             interleave(engine, tile[:, QW * (j - first) : QW * (j - first + 1), :], rows)
+
+        def interleave_wv_part(j, engine, a, e):
+            tile, first = w_staging[j]
+            c, g = j // 2, j % 2
+            rows = wv_chunk(c)[:, g, :, a:e]
+            interleave(engine, tile[:, QW * (j - first) + a : QW * (j - first) + e, :], rows)
+
+        def interleave_wv_pass_on_gpsimd(part, g):
+            tile, first = w_staging[4 * part]
+            nc.gpsimd.tensor_scalar(
+                out=tile[:, QW * (4 * part - first) : QW * (4 * part - first + 4), :].rearrange(
+                    "p (c g n) t -> p c g n t", c=2, g=2
+                )[:, :, g],
+                in0=wv_sb[part + 1][:, g].rearrange("p t (c n) -> p c n t", c=2),
+                scalar1=1.0,
+                scalar2=0.0,
+                op0=MULT,
+                op1=ADD,
+            )
 
         def interleave_wv_chunk_on_gpsimd(c):
             tile, first = w_staging[2 * c]
-            part = min(c, 2)
             nc.gpsimd.tensor_scalar(
                 out=tile[:, QW * (2 * c - first) : QW * (2 * c - first + 2), :].rearrange("p (g n) t -> p g n t", g=2),
-                in0=wv_sb[part][:, :, :, QW * (c - part) : QW * (c - part + 1)].rearrange("p g t n -> p g n t"),
+                in0=wv_chunk(c).rearrange("p g t n -> p g n t"),
                 scalar1=1.0,
                 scalar2=0.0,
                 op0=MULT,
@@ -317,62 +342,72 @@ def tile_dpfpattention_pb_kernel(tc, x, wv, beta, vo, k_bytes, k_scale, W, out):
                 op=SUB,
             )
 
-        def times_beta(o, a=0, e=8):
-            if o not in dv_staging:
-                dv_staging[o] = work.tile([P, 8, DH, PACK], BF16, align_bytes=64, name="dv_staging", bufs=2)
+        def stage_dv(q, tile=None):
+            if tile is None:
+                tile = work.tile([P, QW, PACK], BF16, align_bytes=64, name="dv_staging", bufs=2)[:]
+            dv_staging[q] = tile
+
+        def times_beta(q, a=0, e=4):
+            o, h0 = q // 2, 4 * (q % 2)
             nc.vector.tensor_tensor(
-                out=dv_staging[o][:, a:e].rearrange("p h (c i) t -> p (h c) t i", i=BETA_RUN),
-                in0=diff[o][:, :, DH * a : DH * e].rearrange("p t (c i) -> p c t i", i=BETA_RUN),
-                in1=beta_banks[o][:, :, REP * a : REP * e]
+                out=dv_staging[q][:, DH * a : DH * e, :].rearrange("p (c i) t -> p c t i", i=BETA_RUN),
+                in0=diff[o][:, :, DH * (h0 + a) : DH * (h0 + e)].rearrange("p t (c i) -> p c t i", i=BETA_RUN),
+                in1=beta_banks[o][:, :, REP * (h0 + a) : REP * (h0 + e)]
                 .rearrange("p t c -> p c t")
                 .unsqueeze(3)
                 .to_broadcast([P, (e - a) * REP, PACK, BETA_RUN]),
                 op=MULT,
             )
 
-        def quantise_dv_from(o, a, e, values):
-            cols = slice(DH * (8 * o + a), DH * (8 * o + e))
-            nc.vector.quantize_mx(out=dv_codes[:, cols].bitcast(FP8X4), scales=dv_exps[:, cols], in_=values)
-
-        def quantise_dv(o, a, e):
-            quantise_dv_from(o, a, e, dv_staging[o][:, a:e].rearrange("p h d t -> p (h d t)"))
-
-        last_beta = keep.tile([P, 2, PACK], F32, name="last_beta")
-        last_octet, last_pair = OCTETS - 1, 6
-
-        def fetch_last_beta():
-            nc.scalar.copy(
-                out=last_beta[:],
-                in_=beta_banks[last_octet][:, :, REP * last_pair : REP * (last_pair + 2) : REP].rearrange(
-                    "p t h -> p h t"
-                ),
+        def quantise_dv(q, a=0, e=4):
+            cols = slice(DH * (4 * q + a), DH * (4 * q + e))
+            nc.vector.quantize_mx(
+                out=dv_codes[:, cols].bitcast(FP8X4),
+                scales=dv_exps[:, cols],
+                in_=dv_staging[q][:, DH * a : DH * e, :].rearrange("p n t -> p (n t)"),
             )
 
-        def times_last_beta_on_gpsimd(gate):
-            tile = staging(2 * DH, gate)
+        beta_sb = keep.tile([P, PACK, B * H], BF16, name="beta_sb")
+        beta_turned = []
+
+        def turn_beta():
+            bank = ps_beta.tile([P, PACK, P], BF16, name="beta_bank")
+            beta_turned.append(bank)
+            for t in range(PACK):
+                nc.tensor.transpose(bank[:, t, :], beta_rows[:, t::PACK], ident_bf16[:])
+
+        def fetch_beta(engine):
+            copy = nc.vector.tensor_copy if engine == VECTOR else nc.scalar.copy
+            copy(out=beta_sb[:], in_=beta_turned[0][:, :, 0 : B * H])
+
+        def times_beta_on_gpsimd(q, a, e):
+            o, h0 = q // 2, 4 * (q % 2)
+            row = H * (o % 2) + 8 * (o // 2) + h0
             nc.gpsimd.tensor_tensor(
-                out=tile[:].rearrange("p (h d) t -> p h d t", h=2),
-                in0=diff[last_octet][:, :, DH * last_pair : DH * (last_pair + 2)].rearrange(
-                    "p t (h d) -> p h d t", h=2
-                ),
-                in1=last_beta[:].unsqueeze(2).to_broadcast([P, 2, DH, PACK]),
+                out=dv_staging[q][:, DH * a : DH * e, :].rearrange("p (h d) t -> p h d t", d=DH),
+                in0=diff[o][:, :, DH * (h0 + a) : DH * (h0 + e)].rearrange("p t (h d) -> p h d t", d=DH),
+                in1=beta_sb[:, :, row + a : row + e]
+                .rearrange("p t h -> p h t")
+                .unsqueeze(2)
+                .to_broadcast([P, e - a, DH, PACK]),
                 op=MULT,
             )
-            return tile
 
 
         out_banks = {}
 
+        def out_bank(pool, name, parts):
+            bank = pool.tile([P, 8, DH], F32, name=name)
+            at = 0
+            for q, a, e in parts:
+                out_banks[(q, a)] = bank[:, at:, :]
+                at += e - a
+
         def second_product(q, a=0, e=4):
-            if q >= QUADS - 2:
-                out_banks[(q, a)] = ps_v.tile([P, 8, DH], F32, name="v_bank")
-            elif q % 2 == 0:
-                out_banks[(q, a)] = ps_out.tile([P, 8, DH], F32, name="out_bank")
-                out_banks[(q + 1, a)] = out_banks[(q, a)]
             for h in range(a, e):
                 head = 4 * q + h
                 nc.tensor.matmul_mx(
-                    out=out_banks[(q, a)][:, 4 * (q % 2) + h, :],
+                    out=out_banks[(q, a)][:, h - a, :],
                     lhsT=k_codes[:, S * head : S * (head + 1)].bitcast(FP8X4),
                     lhsT_scale=k_exps[:, S * head : S * (head + 1)],
                     rhs=dv_codes[:, DH * head : DH * (head + 1)].bitcast(FP8X4),
@@ -381,11 +416,16 @@ def tile_dpfpattention_pb_kernel(tc, x, wv, beta, vo, k_bytes, k_scale, W, out):
                     stop=True,
                 )
 
-        def add_memory_and_store(o, a=0, e=8):
-            bank = out_banks[(2 * o + a // 4, a % 4)]
-            nc.vector.tensor_tensor(out=out_sb[o][:, a:e, :], in0=bank[:, a:e, :], in1=mem_sb[o][:, a:e, :], op=ADD)
-            b, h0 = o % 2, 8 * (o // 2)
-            nc.sync.dma_start(out=out[b, h0 + a : h0 + e].rearrange("h s d -> s h d"), in_=out_sb[o][:, a:e, :])
+        def add_memory_and_store(q, a=0, e=4):
+            o, h0 = q // 2, 4 * (q % 2)
+            heads = slice(h0 + a, h0 + e)
+            nc.vector.tensor_tensor(
+                out=out_sb[o][:, heads, :], in0=out_banks[(q, a)][:, 0 : e - a, :], in1=mem_sb[o][:, heads, :], op=ADD
+            )
+            b, first = o % 2, 8 * (o // 2) + h0
+            nc.sync.dma_start(
+                out=out[b, first + a : first + e].rearrange("h s d -> s h d"), in_=out_sb[o][:, heads, :]
+            )
 
 
         make_constants()
@@ -393,177 +433,217 @@ def tile_dpfpattention_pb_kernel(tc, x, wv, beta, vo, k_bytes, k_scale, W, out):
         load_k_scales()
         load_first_k_pair(0)
         load_first_k_pair(2)
+        load_k(1)
         load_x(0, 0)
         load_beta()
-        load_k(1)
+        load_k(2)
         load_wv(0, 0)
         load_x(0, 1)
         load_wv(0, 1)
         load_wv(1, 0)
         load_vo(0)
         load_wv(1, 1)
+        load_k(3)
         load_x(1, 0)
-        load_x(1, 1)
         load_vo(1)
-        load_k(2)
+        load_x(1, 1)
         load_wv(2, 0)
         load_vo(2)
         load_wv(2, 1)
         load_vo(3)
-        load_k(3)
-        for q in (4, 5):
-            load_k(q)
-            load_vo(q)
+        load_k(4)
         load_memory(0)
+        load_k(5)
+        load_vo(4)
+        load_vo(5)
         load_k(6)
+        load_memory(1)
         load_vo(6)
         load_vo(7)
         load_k(7)
-        for o in range(1, OCTETS):
+        for o in range(2, OCTETS):
             load_memory(o)
 
         widen_k((0, 2), VECTOR)
-        widen_k((2, 2), SCALAR)
+        widen_k((2, 2), SCALAR, 1, 2)
+        widen_k((2, 2), VECTOR, 0, 1)
         stage_k(0, 4)
         interleave_k((0, 2), VECTOR)
+        widen_k((4, 2), SCALAR)
+        interleave_k((2, 2), VECTOR)
+        widen_k((6, 2), SCALAR, 0, 1)
+        widen_k((6, 2), VECTOR, 1, 2)
+        stage_k(4, 4)
+        interleave_k((4, 2), VECTOR)
         for g in range(2):
             turn_x(0, 0, g)
+        turn_beta()
         for g in range(2):
             fetch_x(0, 0, g)
-        interleave_k((2, 2), VECTOR)
+        fetch_beta(SCALAR)
+        quantise_k(0, 4)
+        interleave_k((6, 2), VECTOR)
         stage_wv(0, 2)
         interleave_wv(0, VECTOR)
-        quantise_k(0, 4)
         quantise_x(0, 0)
-        widen_k((4, 2), SCALAR)
+        quantise_k(4, 4)
+        widen_k((8, 2), SCALAR)
+        widen_k((10, 2), SCALAR, 0, 1)
         for g in range(2):
             turn_x(0, 1, g)
-        for g in range(2):
-            fetch_x(0, 1, g)
+        fetch_x(0, 1, 0, gate="a")
+        fetch_x(0, 1, 1)
+        widen_k((10, 2), SCALAR, 1, 2)
         interleave_wv(1, VECTOR)
-        stage_k(4, 2)
-        interleave_k((4, 2), VECTOR)
+        stage_k(8, 4)
+        interleave_k((8, 2), VECTOR)
         quantise_wv(0, 2)
         spread_beta(0)
         first_product(0, 0)
         quantise_x(0, 1)
         first_product(0, 1)
-        quantise_k(4, 2)
-        stage_wv(2, 2, gate="a")
+        interleave_k((10, 2), VECTOR)
+
+        stage_wv(2, 1)
+        stage_wv(3, 1, gate="a")
+        interleave_wv(3, GPSIMD)
         interleave_wv(2, SCALAR)
-        interleave_wv(3, SCALAR)
-        widen_k((6, 2), SCALAR)
-        for u in range(2):
-            subtract_vo(0, u)
-        quantise_wv(2, 2)
+        widen_k((12, 4), SCALAR)
         for g in range(2):
             turn_x(1, 0, g)
-        for u in range(2):
-            first_product(1, u)
         for g in range(2):
             fetch_x(1, 0, g)
+        for u in range(2):
+            subtract_vo(0, u)
+        quantise_wv(2, 1)
+        quantise_wv(3, 1)
+        for u in range(2):
+            first_product(1, u)
+        quantise_k(8, 4)
 
-        stage_k(6, 2, gate="a")
-        interleave_k((6, 2), GPSIMD)
+        stage_k(12, 4, gate="a")
+        interleave_k((12, 4), GPSIMD, 0, 3)
         for g in range(2):
             turn_x(1, 1, g)
-        widen_k((8, 6), SCALAR, 0, 1)
-        fetch_x(1, 1, 0, gate="b")
-        fetch_x(1, 1, 1)
-        widen_k((8, 6), SCALAR, 1, 3)
-        times_beta(0, 0, 4)
+        for g in range(2):
+            fetch_x(1, 1, g)
+        interleave_k((12, 4), SCALAR, 3, 4)
+        stage_wv(4, 2)
+        interleave_wv(4, SCALAR)
+        stage_dv(0)
+        times_beta(0)
         for u in range(2):
             subtract_vo(1, u)
         quantise_x(1, 0)
         for q in (2, 3):
             first_product(q, 0)
-        quantise_k(6, 2)
-        quantise_dv(0, 0, 4)
         quantise_x(1, 1)
         for q in (2, 3):
             first_product(q, 1)
-        second_product(0)
+        quantise_k(12, 4)
+        quantise_dv(0)
 
-        stage_wv(4, 4, gate="b")
+        stage_wv(6, 2, gate="a")
         interleave_wv_chunk_on_gpsimd(3)
-        interleave_wv(4, SCALAR)
         interleave_wv(5, SCALAR)
-        widen_k((8, 6), SCALAR, 3, 6)
-        times_beta(0, 4, 8)
+        for first in (16, 18):
+            widen_k((first, 2), SCALAR)
+        stage_dv(1)
+        times_beta(1)
         spread_beta(1)
         for u in range(2):
             for q in (2, 3):
                 subtract_vo(q, u)
-        quantise_dv(0, 4, 8)
-        quantise_wv(4, 4)
-        for q in (4, 5):
-            for u in range(2):
-                first_product(q, u)
-        second_product(1)
+        for first in (16, 18):
+            interleave_k_on_tensor((first, 2))
+        quantise_wv(4, 2)
+        for u in range(2):
+            first_product(4, u)
+        quantise_wv(6, 2)
+        for u in range(2):
+            first_product(5, u)
+        quantise_dv(1)
+        out_bank(ps_out, "out_bank", [(0, 0, 4), (1, 0, 4)])
+        for q in (0, 1):
+            second_product(q)
 
-        stage_k(8, 8, gate="b")
-        interleave_k((8, 6), GPSIMD)
-        times_beta(1)
+        widen_k((20, 4), SCALAR, 0, 2)
+        stage_k(16, 4)
+        fetch_k((16, 2))
+        fetch_k((18, 2))
+        stage_dv(2, stage_k(20, 1, gate="a", spare=QW))
+        times_beta_on_gpsimd(2, 0, 4)
+        interleave_k((20, 4), GPSIMD, 0, 1)
+        widen_k((20, 4), SCALAR, 2, 4)
+        widen_k((24, 4), SCALAR, 0, 2)
+        stage_k(21, 3)
+        interleave_k((20, 4), SCALAR, 1, 4)
+        widen_k((24, 4), SCALAR, 2, 4)
+        stage_dv(3)
+        times_beta(3)
+
         spread_beta(2)
-        widen_k((14, 2), SCALAR)
-        widen_k((16, 6), SCALAR, 0, 1)
-        interleave_k((14, 2), SCALAR)
-        widen_k((16, 6), SCALAR, 1, 6)
         for q in (4, 5):
             for u in range(2):
                 subtract_vo(q, u)
-        add_memory_and_store(0)
-        quantise_dv(1, 0, 4)
-        quantise_k(8, 8)
-        quantise_dv(1, 4, 8)
         for q in (6, 7):
             for u in range(2):
                 first_product(q, u)
+        add_memory_and_store(0, 0, 8)
+        quantise_k(16, 4)
+        quantise_k(20, 1)
+        quantise_dv(2)
+        quantise_dv(3)
+        out_bank(ps_out, "out_bank", [(2, 0, 4), (3, 0, 4)])
         for q in (2, 3):
             second_product(q)
 
-        stage_k(16, 8, gate="b")
-        interleave_k((16, 6), GPSIMD)
-        times_beta(2)
-        for first in (22, 24):
-            widen_k((first, 2), SCALAR)
-            interleave_k_on_tensor((first, 2))
-        spread_beta(3)
-        widen_k((26, 2), SCALAR)
-        fetch_k((22, 2))
-        interleave_k_on_tensor((26, 2))
-        widen_k((30, 2), SCALAR)
-        stage_k(24, 4)
-        fetch_k((24, 2))
-        fetch_last_beta()
+        stage_dv(4, stage_k(24, 1, gate="a", spare=QW))
+        times_beta_on_gpsimd(4, 0, 4)
+        interleave_k((24, 4), GPSIMD, 0, 1)
         widen_k((28, 2), SCALAR)
-        fetch_k((26, 2))
+        interleave_k_on_tensor((28, 2))
+        stage_k(25, 3)
+        interleave_k((24, 4), SCALAR, 1, 4)
         stage_k(28, 4)
+        widen_k((30, 2), SCALAR)
+        fetch_k((28, 2))
         interleave_k((30, 2), SCALAR)
-        interleave_k((28, 2), SCALAR)
+        stage_dv(5)
+        times_beta(5)
+
+        spread_beta(3)
         for q in (6, 7):
             for u in range(2):
                 subtract_vo(q, u)
-        add_memory_and_store(1)
-        quantise_dv(2, 0, 4)
-        quantise_k(16, 8)
-        quantise_dv(2, 4, 8)
+        add_memory_and_store(2, 0, 8)
+        quantise_k(21, 1)
+        quantise_k(22, 2)
+        quantise_k(24, 1)
+        quantise_dv(4)
+        quantise_dv(5)
+        out_bank(ps_out, "out_bank", [(4, 0, 4), (5, 0, 4)])
         for q in (4, 5):
             second_product(q)
 
-        last_dv = times_last_beta_on_gpsimd("b")
-        times_beta(3, 0, last_pair)
-        add_memory_and_store(2)
-
-        quantise_dv(3, 0, 4)
-        quantise_k(24, 4)
+        stage_dv(7, staging(QW, "a")[:])
+        times_beta_on_gpsimd(7, 0, 3)
+        stage_dv(6)
+        times_beta(6)
+        add_memory_and_store(4, 0, 8)
+        times_beta(7, 3, 4)
+        quantise_k(25, 1)
+        quantise_k(26, 2)
+        quantise_dv(6)
+        out_bank(ps_v, "v_bank", [(6, 0, 4)])
         second_product(6)
-        quantise_dv_from(last_octet, last_pair, 8, last_dv[:].rearrange("p n t -> p (n t)"))
-        quantise_k(30, 2)
-        second_product(7, 2, 4)
-        quantise_dv(3, 4, 6)
         quantise_k(28, 2)
+        quantise_dv(7)
+        out_bank(ps_v, "v_bank", [(7, 0, 2)])
         second_product(7, 0, 2)
-        add_memory_and_store(3, 0, 4)
-        add_memory_and_store(3, 6, 8)
-        add_memory_and_store(3, 4, 6)
+        quantise_k(30, 2)
+        out_bank(ps_v, "v_bank", [(7, 2, 4)])
+        second_product(7, 2, 4)
+        add_memory_and_store(6)
+        add_memory_and_store(7, 0, 2)
+        add_memory_and_store(7, 2, 4)

@@ -27,6 +27,7 @@ WV_LOADS = ((0, QW), (QW, QW), (2 * QW, 2 * QW))
 COPY_RUN = 4
 BETA_RUN = 2
 REP = DH // BETA_RUN
+LINE = 4
 VECTOR, SCALAR, GPSIMD = "vector", "scalar", "gpsimd"
 
 
@@ -380,16 +381,29 @@ def tile_dpfpattention_pb_kernel(tc, x, wv, beta, vo, k_bytes, k_scale, W, out):
             copy = nc.vector.tensor_copy if engine == VECTOR else nc.scalar.copy
             copy(out=beta_sb[:], in_=beta_turned[0][:, :, 0 : B * H])
 
-        def times_beta_on_gpsimd(q, a, e):
-            o, h0 = q // 2, 4 * (q % 2)
-            row = H * (o % 2) + 8 * (o // 2) + h0
-            nc.gpsimd.tensor_tensor(
-                out=dv_staging[q][:, DH * a : DH * e, :].rearrange("p (h d) t -> p h d t", d=DH),
-                in0=diff[o][:, :, DH * (h0 + a) : DH * (h0 + e)].rearrange("p t (h d) -> p h d t", d=DH),
-                in1=beta_sb[:, :, row + a : row + e]
+        beta_runs = {}
+
+        def repeat_beta(q, n):
+            o = q // 2
+            row = H * (o % 2) + 8 * (o // 2) + 4 * (q % 2)
+            beta_runs[q] = keep.tile([P, n, DH // LINE, PACK], BF16, name="beta_runs%d" % q)
+            nc.scalar.copy(
+                out=beta_runs[q][:],
+                in_=beta_sb[:, :, row : row + n]
                 .rearrange("p t h -> p h t")
                 .unsqueeze(2)
-                .to_broadcast([P, e - a, DH, PACK]),
+                .to_broadcast([P, n, DH // LINE, PACK]),
+            )
+
+        def times_beta_on_gpsimd(q, n):
+            o, h0 = q // 2, 4 * (q % 2)
+            nc.gpsimd.tensor_tensor(
+                out=dv_staging[q][:, 0 : DH * n, :].rearrange("p (c i) t -> p c t i", i=LINE),
+                in0=diff[o][:, :, DH * h0 : DH * (h0 + n)].rearrange("p t (c i) -> p c t i", i=LINE),
+                in1=beta_runs[q][:]
+                .rearrange("p h c t -> p (h c) t")
+                .unsqueeze(3)
+                .to_broadcast([P, n * DH // LINE, PACK, LINE]),
                 op=MULT,
             )
 
@@ -492,17 +506,17 @@ def tile_dpfpattention_pb_kernel(tc, x, wv, beta, vo, k_bytes, k_scale, W, out):
         for g in range(2):
             turn_x(0, 1, g)
         fetch_x(0, 1, 0, gate="a")
-        fetch_x(0, 1, 1)
         widen_k((10, 2), SCALAR, 1, 2)
+        fetch_x(0, 1, 1)
         interleave_wv(1, VECTOR)
         stage_k(8, 4)
         interleave_k((8, 2), VECTOR)
         quantise_wv(0, 2)
         spread_beta(0)
         first_product(0, 0)
+        interleave_k((10, 2), VECTOR)
         quantise_x(0, 1)
         first_product(0, 1)
-        interleave_k((10, 2), VECTOR)
 
         stage_wv(2, 1)
         stage_wv(3, 1, gate="a")
@@ -523,6 +537,9 @@ def tile_dpfpattention_pb_kernel(tc, x, wv, beta, vo, k_bytes, k_scale, W, out):
 
         stage_k(12, 4, gate="a")
         interleave_k((12, 4), GPSIMD, 0, 3)
+        repeat_beta(2, 4)
+        repeat_beta(4, 4)
+        repeat_beta(7, 2)
         for g in range(2):
             turn_x(1, 1, g)
         for g in range(2):
@@ -572,7 +589,7 @@ def tile_dpfpattention_pb_kernel(tc, x, wv, beta, vo, k_bytes, k_scale, W, out):
         fetch_k((16, 2))
         fetch_k((18, 2))
         stage_dv(2, stage_k(20, 1, gate="a", spare=QW))
-        times_beta_on_gpsimd(2, 0, 4)
+        times_beta_on_gpsimd(2, 4)
         interleave_k((20, 4), GPSIMD, 0, 1)
         widen_k((20, 4), SCALAR, 2, 4)
         widen_k((24, 4), SCALAR, 0, 2)
@@ -599,7 +616,7 @@ def tile_dpfpattention_pb_kernel(tc, x, wv, beta, vo, k_bytes, k_scale, W, out):
             second_product(q)
 
         stage_dv(4, stage_k(24, 1, gate="a", spare=QW))
-        times_beta_on_gpsimd(4, 0, 4)
+        times_beta_on_gpsimd(4, 4)
         interleave_k((24, 4), GPSIMD, 0, 1)
         widen_k((28, 2), SCALAR)
         interleave_k_on_tensor((28, 2))
@@ -627,11 +644,11 @@ def tile_dpfpattention_pb_kernel(tc, x, wv, beta, vo, k_bytes, k_scale, W, out):
             second_product(q)
 
         stage_dv(7, staging(QW, "a")[:])
-        times_beta_on_gpsimd(7, 0, 3)
+        times_beta_on_gpsimd(7, 2)
         stage_dv(6)
         times_beta(6)
         add_memory_and_store(4, 0, 8)
-        times_beta(7, 3, 4)
+        times_beta(7, 2, 4)
         quantise_k(25, 1)
         quantise_k(26, 2)
         quantise_dv(6)

@@ -181,8 +181,8 @@ def tile_dpfpattention_pb_kernel(tc, x, wv, beta, vo, k_bytes, k_scale, W, out):
                 engine, staged_k(first + a, e - a), k_planar[first][:, :, a:e, :].rearrange("p t h s -> p t (h s)")
             )
 
-        def interleave_k_on_tensor(group):
-            first, n = group
+        def interleave_k_on_tensor(group, n=2):
+            first = group[0]
             bank = ps_turn.tile([P, n * S, PACK], BF16, name="turned")
             k_banks[first] = bank
             for h in range(n):
@@ -194,8 +194,8 @@ def tile_dpfpattention_pb_kernel(tc, x, wv, beta, vo, k_bytes, k_scale, W, out):
                     stop=True,
                 )
 
-        def fetch_k(group):
-            first, n = group
+        def fetch_k(group, n=2):
+            first = group[0]
             nc.scalar.copy(out=staged_k(first, n), in_=k_banks[first][:])
 
         def quantise_k(first, n):
@@ -296,15 +296,15 @@ def tile_dpfpattention_pb_kernel(tc, x, wv, beta, vo, k_bytes, k_scale, W, out):
 
         beta_banks = {}
 
-        def spread_beta(o):
+        def spread_beta(o, a=0):
             bank = ps_beta.tile([P, PACK, 8 * REP], BF16, name="beta_bank")
             beta_banks[o] = bank
             b, h0 = o % 2, 8 * (o // 2)
             for t in range(PACK):
                 nc.tensor.matmul(
-                    bank[:, t],
+                    bank[:, t, REP * a :],
                     lhsT=beta_rows[:, t::PACK],
-                    rhs=pick[b][:, h0 : h0 + 8].rearrange("p h c -> p (h c)"),
+                    rhs=pick[b][:, h0 + a : h0 + 8].rearrange("p h c -> p (h c)"),
                     start=True,
                     stop=True,
                 )
@@ -343,29 +343,29 @@ def tile_dpfpattention_pb_kernel(tc, x, wv, beta, vo, k_bytes, k_scale, W, out):
                 op=SUB,
             )
 
-        def stage_dv(q, tile=None):
-            if tile is None:
-                tile = work.tile([P, QW, PACK], BF16, align_bytes=64, name="dv_staging", bufs=2)[:]
-            dv_staging[q] = tile
+        def stage_dv(o, gate=None):
+            if gate:
+                dv_staging[o] = staging(2 * QW, gate)
+            else:
+                dv_staging[o] = work.tile([P, 2 * QW, PACK], BF16, align_bytes=64, name="dv_staging", bufs=1)
 
-        def times_beta(q, a=0, e=4):
-            o, h0 = q // 2, 4 * (q % 2)
+        def times_beta(o, a, e):
             nc.vector.tensor_tensor(
-                out=dv_staging[q][:, DH * a : DH * e, :].rearrange("p (c i) t -> p c t i", i=BETA_RUN),
-                in0=diff[o][:, :, DH * (h0 + a) : DH * (h0 + e)].rearrange("p t (c i) -> p c t i", i=BETA_RUN),
-                in1=beta_banks[o][:, :, REP * (h0 + a) : REP * (h0 + e)]
+                out=dv_staging[o][:, DH * a : DH * e, :].rearrange("p (c i) t -> p c t i", i=BETA_RUN),
+                in0=diff[o][:, :, DH * a : DH * e].rearrange("p t (c i) -> p c t i", i=BETA_RUN),
+                in1=beta_banks[o][:, :, REP * a : REP * e]
                 .rearrange("p t c -> p c t")
                 .unsqueeze(3)
                 .to_broadcast([P, (e - a) * REP, PACK, BETA_RUN]),
                 op=MULT,
             )
 
-        def quantise_dv(q, a=0, e=4):
-            cols = slice(DH * (4 * q + a), DH * (4 * q + e))
+        def quantise_dv(o, a, e):
+            cols = slice(DH * (8 * o + a), DH * (8 * o + e))
             nc.vector.quantize_mx(
                 out=dv_codes[:, cols].bitcast(FP8X4),
                 scales=dv_exps[:, cols],
-                in_=dv_staging[q][:, DH * a : DH * e, :].rearrange("p n t -> p (n t)"),
+                in_=dv_staging[o][:, DH * a : DH * e, :].rearrange("p n t -> p (n t)"),
             )
 
         beta_sb = keep.tile([P, PACK, B * H], BF16, name="beta_sb")
@@ -384,8 +384,8 @@ def tile_dpfpattention_pb_kernel(tc, x, wv, beta, vo, k_bytes, k_scale, W, out):
         beta_runs = {}
 
         def repeat_beta(q, n):
-            o = q // 2
-            row = H * (o % 2) + 8 * (o // 2) + 4 * (q % 2)
+            o = q
+            row = H * (o % 2) + 8 * (o // 2)
             beta_runs[q] = keep.tile([P, n, DH // LINE, PACK], BF16, name="beta_runs%d" % q)
             nc.scalar.copy(
                 out=beta_runs[q][:],
@@ -396,7 +396,7 @@ def tile_dpfpattention_pb_kernel(tc, x, wv, beta, vo, k_bytes, k_scale, W, out):
             )
 
         def times_beta_on_gpsimd(q, n):
-            o, h0 = q // 2, 4 * (q % 2)
+            o, h0 = q, 0
             nc.gpsimd.tensor_tensor(
                 out=dv_staging[q][:, 0 : DH * n, :].rearrange("p (c i) t -> p c t i", i=LINE),
                 in0=diff[o][:, :, DH * h0 : DH * (h0 + n)].rearrange("p t (c i) -> p c t i", i=LINE),
@@ -448,47 +448,46 @@ def tile_dpfpattention_pb_kernel(tc, x, wv, beta, vo, k_bytes, k_scale, W, out):
         load_first_k_pair(0)
         load_first_k_pair(2)
         load_k(1)
+        load_k(2)
         load_x(0, 0)
         load_beta()
-        load_k(2)
         load_wv(0, 0)
         load_x(0, 1)
         load_wv(0, 1)
         load_wv(1, 0)
         load_vo(0)
-        load_wv(1, 1)
         load_k(3)
+        load_wv(1, 1)
         load_x(1, 0)
         load_vo(1)
         load_x(1, 1)
         load_wv(2, 0)
+        load_k(4)
         load_vo(2)
         load_wv(2, 1)
         load_vo(3)
-        load_k(4)
-        load_memory(0)
         load_k(5)
         load_vo(4)
         load_vo(5)
+        load_memory(0)
         load_k(6)
-        load_memory(1)
         load_vo(6)
         load_vo(7)
         load_k(7)
-        for o in range(2, OCTETS):
+        for o in range(1, OCTETS):
             load_memory(o)
 
-        widen_k((0, 2), VECTOR)
-        widen_k((2, 2), SCALAR, 1, 2)
-        widen_k((2, 2), VECTOR, 0, 1)
+        for first in (0, 2):
+            widen_k((first, 2), VECTOR, 0, 1)
+            widen_k((first, 2), SCALAR, 1, 2)
         stage_k(0, 4)
         interleave_k((0, 2), VECTOR)
         widen_k((4, 2), SCALAR)
         interleave_k((2, 2), VECTOR)
-        widen_k((6, 2), SCALAR, 0, 1)
-        widen_k((6, 2), VECTOR, 1, 2)
+        widen_k((6, 2), VECTOR)
         stage_k(4, 4)
         interleave_k((4, 2), VECTOR)
+        widen_k((8, 2), SCALAR)
         for g in range(2):
             turn_x(0, 0, g)
         turn_beta()
@@ -499,14 +498,12 @@ def tile_dpfpattention_pb_kernel(tc, x, wv, beta, vo, k_bytes, k_scale, W, out):
         interleave_k((6, 2), VECTOR)
         stage_wv(0, 2)
         interleave_wv(0, VECTOR)
-        quantise_x(0, 0)
         quantise_k(4, 4)
-        widen_k((8, 2), SCALAR)
-        widen_k((10, 2), SCALAR, 0, 1)
+        quantise_x(0, 0)
+        widen_k((10, 2), SCALAR)
         for g in range(2):
             turn_x(0, 1, g)
         fetch_x(0, 1, 0, gate="a")
-        widen_k((10, 2), SCALAR, 1, 2)
         fetch_x(0, 1, 1)
         interleave_wv(1, VECTOR)
         stage_k(8, 4)
@@ -517,12 +514,15 @@ def tile_dpfpattention_pb_kernel(tc, x, wv, beta, vo, k_bytes, k_scale, W, out):
         interleave_k((10, 2), VECTOR)
         quantise_x(0, 1)
         first_product(0, 1)
+        quantise_k(8, 2)
 
         stage_wv(2, 1)
         stage_wv(3, 1, gate="a")
-        interleave_wv(3, GPSIMD)
+        interleave_wv_part(3, GPSIMD, 0, 192)
         interleave_wv(2, SCALAR)
-        widen_k((12, 4), SCALAR)
+        widen_k((12, 4), SCALAR, 0, 2)
+        interleave_wv_part(3, SCALAR, 192, QW)
+        widen_k((12, 4), SCALAR, 2, 4)
         for g in range(2):
             turn_x(1, 0, g)
         for g in range(2):
@@ -533,73 +533,72 @@ def tile_dpfpattention_pb_kernel(tc, x, wv, beta, vo, k_bytes, k_scale, W, out):
         quantise_wv(3, 1)
         for u in range(2):
             first_product(1, u)
-        quantise_k(8, 4)
+        quantise_k(10, 2)
 
-        stage_k(12, 4, gate="a")
+        stage_k(12, 3, gate="a")
         interleave_k((12, 4), GPSIMD, 0, 3)
-        repeat_beta(2, 4)
-        repeat_beta(4, 4)
-        repeat_beta(7, 2)
+        stage_k(15, 1)
+        interleave_k((12, 4), SCALAR, 3, 4)
+        repeat_beta(1, 5)
         for g in range(2):
             turn_x(1, 1, g)
         for g in range(2):
             fetch_x(1, 1, g)
-        interleave_k((12, 4), SCALAR, 3, 4)
-        stage_wv(4, 2)
-        interleave_wv(4, SCALAR)
         stage_dv(0)
-        times_beta(0)
+        times_beta(0, 0, 4)
         for u in range(2):
             subtract_vo(1, u)
         quantise_x(1, 0)
         for q in (2, 3):
             first_product(q, 0)
+        quantise_dv(0, 0, 4)
         quantise_x(1, 1)
         for q in (2, 3):
             first_product(q, 1)
-        quantise_k(12, 4)
-        quantise_dv(0)
+        quantise_k(12, 2)
+        quantise_k(14, 1)
+        quantise_k(15, 1)
 
-        stage_wv(6, 2, gate="a")
-        interleave_wv_chunk_on_gpsimd(3)
+        stage_wv(4, 4, gate="a")
+        interleave_wv_pass_on_gpsimd(1, 0)
+        widen_k((16, 2), SCALAR)
+        widen_k((18, 2), SCALAR, 0, 1)
         interleave_wv(5, SCALAR)
-        for first in (16, 18):
-            widen_k((first, 2), SCALAR)
-        stage_dv(1)
-        times_beta(1)
-        spread_beta(1)
+        interleave_wv(7, SCALAR)
+        widen_k((18, 2), SCALAR, 1, 2)
+        times_beta(0, 4, 8)
+        spread_beta(1, 5)
         for u in range(2):
             for q in (2, 3):
                 subtract_vo(q, u)
-        for first in (16, 18):
-            interleave_k_on_tensor((first, 2))
+        interleave_k_on_tensor((16, 2))
+        interleave_k_on_tensor((18, 2), 1)
         quantise_wv(4, 2)
         for u in range(2):
             first_product(4, u)
         quantise_wv(6, 2)
         for u in range(2):
             first_product(5, u)
-        quantise_dv(1)
+        quantise_dv(0, 4, 8)
         out_bank(ps_out, "out_bank", [(0, 0, 4), (1, 0, 4)])
         for q in (0, 1):
             second_product(q)
 
-        widen_k((20, 4), SCALAR, 0, 2)
+        stage_dv(1, gate="a")
+        times_beta_on_gpsimd(1, 5)
         stage_k(16, 4)
         fetch_k((16, 2))
-        fetch_k((18, 2))
-        stage_dv(2, stage_k(20, 1, gate="a", spare=QW))
-        times_beta_on_gpsimd(2, 4)
-        interleave_k((20, 4), GPSIMD, 0, 1)
-        widen_k((20, 4), SCALAR, 2, 4)
-        widen_k((24, 4), SCALAR, 0, 2)
-        stage_k(21, 3)
-        interleave_k((20, 4), SCALAR, 1, 4)
-        widen_k((24, 4), SCALAR, 2, 4)
-        stage_dv(3)
-        times_beta(3)
-
-        spread_beta(2)
+        fetch_k((18, 2), 1)
+        interleave_k((18, 2), SCALAR, 1, 2)
+        repeat_beta(2, 5)
+        repeat_beta(3, 2)
+        widen_k((20, 2), SCALAR)
+        widen_k((22, 2), SCALAR)
+        stage_k(20, 4)
+        interleave_k((20, 2), SCALAR)
+        widen_k((24, 2), SCALAR)
+        times_beta(1, 5, 8)
+        spread_beta(2, 5)
         for q in (4, 5):
             for u in range(2):
                 subtract_vo(q, u)
@@ -607,55 +606,51 @@ def tile_dpfpattention_pb_kernel(tc, x, wv, beta, vo, k_bytes, k_scale, W, out):
             for u in range(2):
                 first_product(q, u)
         add_memory_and_store(0, 0, 8)
-        quantise_k(16, 4)
-        quantise_k(20, 1)
-        quantise_dv(2)
-        quantise_dv(3)
+        quantise_k(18, 2)
+        quantise_dv(1, 0, 8)
+        quantise_k(16, 2)
         out_bank(ps_out, "out_bank", [(2, 0, 4), (3, 0, 4)])
         for q in (2, 3):
             second_product(q)
+        for first in (22, 24):
+            interleave_k_on_tensor((first, 2))
 
-        stage_dv(4, stage_k(24, 1, gate="a", spare=QW))
-        times_beta_on_gpsimd(4, 4)
-        interleave_k((24, 4), GPSIMD, 0, 1)
+        stage_dv(2, gate="a")
+        times_beta_on_gpsimd(2, 5)
+        widen_k((26, 2), SCALAR)
+        fetch_k((22, 2))
         widen_k((28, 2), SCALAR)
-        interleave_k_on_tensor((28, 2))
-        stage_k(25, 3)
-        interleave_k((24, 4), SCALAR, 1, 4)
-        stage_k(28, 4)
         widen_k((30, 2), SCALAR)
-        fetch_k((28, 2))
-        interleave_k((30, 2), SCALAR)
-        stage_dv(5)
-        times_beta(5)
-
-        spread_beta(3)
+        stage_k(24, 4)
+        fetch_k((24, 2))
+        interleave_k((26, 2), SCALAR)
+        stage_k(28, 4)
+        interleave_k((28, 2), SCALAR)
+        times_beta(2, 5, 8)
+        spread_beta(3, 2)
         for q in (6, 7):
             for u in range(2):
                 subtract_vo(q, u)
         add_memory_and_store(2, 0, 8)
-        quantise_k(21, 1)
         quantise_k(22, 2)
-        quantise_k(24, 1)
-        quantise_dv(4)
-        quantise_dv(5)
+        quantise_dv(2, 0, 8)
+        quantise_k(20, 2)
         out_bank(ps_out, "out_bank", [(4, 0, 4), (5, 0, 4)])
         for q in (4, 5):
             second_product(q)
+        interleave_k_on_tensor((30, 2))
+        fetch_k((30, 2))
 
-        stage_dv(7, staging(QW, "a")[:])
-        times_beta_on_gpsimd(7, 2)
-        stage_dv(6)
-        times_beta(6)
+        stage_dv(3, gate="a")
+        times_beta_on_gpsimd(3, 2)
+        times_beta(3, 2, 8)
         add_memory_and_store(4, 0, 8)
-        times_beta(7, 2, 4)
-        quantise_k(25, 1)
-        quantise_k(26, 2)
-        quantise_dv(6)
+        quantise_k(24, 4)
+        quantise_dv(3, 0, 4)
         out_bank(ps_v, "v_bank", [(6, 0, 4)])
         second_product(6)
         quantise_k(28, 2)
-        quantise_dv(7)
+        quantise_dv(3, 4, 8)
         out_bank(ps_v, "v_bank", [(7, 0, 2)])
         second_product(7, 0, 2)
         quantise_k(30, 2)

@@ -116,7 +116,7 @@ def tile_dpfpattention_pb_kernel(tc, x, wv, beta, vo, k_bytes, k_scale, W, out):
 
         def make_constants():
             make_identity(nc, ident_bf16[:])
-            make_identity(nc, ident_f32[:])
+            nc.scalar.activation(out=ident_f32[:], in_=ident_bf16[:], func=COPY)
             nc.vector.memset(beta_rows[32:64, :], 0.0)
             nc.vector.memset(beta_rows[64:128, :], 0.0)
             nc.scalar.activation(
@@ -448,9 +448,9 @@ def tile_dpfpattention_pb_kernel(tc, x, wv, beta, vo, k_bytes, k_scale, W, out):
         load_first_k_pair(0)
         load_first_k_pair(2)
         load_k(1)
+        load_beta()
         load_k(2)
         load_x(0, 0)
-        load_beta()
         load_wv(0, 0)
         load_x(0, 1)
         load_wv(0, 1)
@@ -469,8 +469,8 @@ def tile_dpfpattention_pb_kernel(tc, x, wv, beta, vo, k_bytes, k_scale, W, out):
         load_k(5)
         load_vo(4)
         load_vo(5)
-        load_memory(0)
         load_k(6)
+        load_memory(0)
         load_vo(6)
         load_vo(7)
         load_k(7)
@@ -488,12 +488,12 @@ def tile_dpfpattention_pb_kernel(tc, x, wv, beta, vo, k_bytes, k_scale, W, out):
         stage_k(4, 4)
         interleave_k((4, 2), VECTOR)
         widen_k((8, 2), SCALAR)
+        turn_beta()
+        fetch_beta(SCALAR)
         for g in range(2):
             turn_x(0, 0, g)
-        turn_beta()
         for g in range(2):
             fetch_x(0, 0, g)
-        fetch_beta(SCALAR)
         quantise_k(0, 4)
         interleave_k((6, 2), VECTOR)
         stage_wv(0, 2)
@@ -542,8 +542,8 @@ def tile_dpfpattention_pb_kernel(tc, x, wv, beta, vo, k_bytes, k_scale, W, out):
         repeat_beta(1, 5)
         for g in range(2):
             turn_x(1, 1, g)
-        for g in range(2):
-            fetch_x(1, 1, g)
+        fetch_x(1, 1, 0, gate="b")
+        fetch_x(1, 1, 1)
         stage_dv(0)
         times_beta(0, 0, 4)
         for u in range(2):
@@ -552,14 +552,14 @@ def tile_dpfpattention_pb_kernel(tc, x, wv, beta, vo, k_bytes, k_scale, W, out):
         for q in (2, 3):
             first_product(q, 0)
         quantise_dv(0, 0, 4)
+        quantise_k(12, 2)
+        quantise_k(14, 1)
         quantise_x(1, 1)
         for q in (2, 3):
             first_product(q, 1)
-        quantise_k(12, 2)
-        quantise_k(14, 1)
         quantise_k(15, 1)
 
-        stage_wv(4, 4, gate="a")
+        stage_wv(4, 4, gate="b")
         interleave_wv_pass_on_gpsimd(1, 0)
         widen_k((16, 2), SCALAR)
         widen_k((18, 2), SCALAR, 0, 1)
@@ -584,19 +584,17 @@ def tile_dpfpattention_pb_kernel(tc, x, wv, beta, vo, k_bytes, k_scale, W, out):
         for q in (0, 1):
             second_product(q)
 
-        stage_dv(1, gate="a")
+        stage_dv(1, gate="b")
         times_beta_on_gpsimd(1, 5)
         stage_k(16, 4)
-        fetch_k((16, 2))
-        fetch_k((18, 2), 1)
-        interleave_k((18, 2), SCALAR, 1, 2)
         repeat_beta(2, 5)
         repeat_beta(3, 2)
+        interleave_k((18, 2), SCALAR, 1, 2)
         widen_k((20, 2), SCALAR)
-        widen_k((22, 2), SCALAR)
-        stage_k(20, 4)
-        interleave_k((20, 2), SCALAR)
+        fetch_k((16, 2))
+        fetch_k((18, 2), 1)
         widen_k((24, 2), SCALAR)
+        widen_k((26, 2), SCALAR)
         times_beta(1, 5, 8)
         spread_beta(2, 5)
         for q in (4, 5):
@@ -612,36 +610,37 @@ def tile_dpfpattention_pb_kernel(tc, x, wv, beta, vo, k_bytes, k_scale, W, out):
         out_bank(ps_out, "out_bank", [(2, 0, 4), (3, 0, 4)])
         for q in (2, 3):
             second_product(q)
-        for first in (22, 24):
-            interleave_k_on_tensor((first, 2))
 
-        stage_dv(2, gate="a")
+        stage_dv(2, gate="b")
         times_beta_on_gpsimd(2, 5)
-        widen_k((26, 2), SCALAR)
-        fetch_k((22, 2))
-        widen_k((28, 2), SCALAR)
+        times_beta(2, 5, 8)
+        spread_beta(3, 2)
+        for first in (24, 26):
+            interleave_k_on_tensor((first, 2))
+        widen_k((22, 2), SCALAR)
+        stage_k(20, 4)
+        interleave_k((20, 2), SCALAR)
+        interleave_k((22, 2), SCALAR)
         widen_k((30, 2), SCALAR)
         stage_k(24, 4)
         fetch_k((24, 2))
-        interleave_k((26, 2), SCALAR)
+        widen_k((28, 2), SCALAR)
+        fetch_k((26, 2))
         stage_k(28, 4)
         interleave_k((28, 2), SCALAR)
-        times_beta(2, 5, 8)
-        spread_beta(3, 2)
         for q in (6, 7):
             for u in range(2):
                 subtract_vo(q, u)
         add_memory_and_store(2, 0, 8)
-        quantise_k(22, 2)
+        quantise_k(20, 4)
         quantise_dv(2, 0, 8)
-        quantise_k(20, 2)
         out_bank(ps_out, "out_bank", [(4, 0, 4), (5, 0, 4)])
         for q in (4, 5):
             second_product(q)
         interleave_k_on_tensor((30, 2))
         fetch_k((30, 2))
 
-        stage_dv(3, gate="a")
+        stage_dv(3, gate="b")
         times_beta_on_gpsimd(3, 2)
         times_beta(3, 2, 8)
         add_memory_and_store(4, 0, 8)

@@ -456,8 +456,8 @@ def tile_dpfpattention_pb_kernel(tc, x, wv, beta, vo, k_bytes, k_scale, W, out):
         load_wv(0, 1)
         load_wv(1, 0)
         load_vo(0)
-        load_k(3)
         load_wv(1, 1)
+        load_k(3)
         load_x(1, 0)
         load_vo(1)
         load_x(1, 1)
@@ -514,15 +514,17 @@ def tile_dpfpattention_pb_kernel(tc, x, wv, beta, vo, k_bytes, k_scale, W, out):
         interleave_k((10, 2), VECTOR)
         quantise_x(0, 1)
         first_product(0, 1)
-        quantise_k(8, 2)
+        quantise_k(8, 4)
 
-        stage_wv(2, 1)
-        stage_wv(3, 1, gate="a")
-        interleave_wv_part(3, GPSIMD, 0, 192)
-        interleave_wv(2, SCALAR)
-        widen_k((12, 4), SCALAR, 0, 2)
-        interleave_wv_part(3, SCALAR, 192, QW)
-        widen_k((12, 4), SCALAR, 2, 4)
+        stage_wv(2, 1, gate="a")
+        stage_wv(3, 1)
+        interleave_wv_part(2, GPSIMD, 0, 128)
+        interleave_wv_part(2, SCALAR, 128, QW)
+        repeat_beta(1, 4)
+        repeat_beta(2, 4)
+        repeat_beta(3, 2)
+        interleave_wv(3, SCALAR)
+        widen_k((12, 4), SCALAR)
         for g in range(2):
             turn_x(1, 0, g)
         for g in range(2):
@@ -533,13 +535,11 @@ def tile_dpfpattention_pb_kernel(tc, x, wv, beta, vo, k_bytes, k_scale, W, out):
         quantise_wv(3, 1)
         for u in range(2):
             first_product(1, u)
-        quantise_k(10, 2)
 
         stage_k(12, 3, gate="a")
         interleave_k((12, 4), GPSIMD, 0, 3)
         stage_k(15, 1)
         interleave_k((12, 4), SCALAR, 3, 4)
-        repeat_beta(1, 5)
         for g in range(2):
             turn_x(1, 1, g)
         fetch_x(1, 1, 0, gate="b")
@@ -551,13 +551,13 @@ def tile_dpfpattention_pb_kernel(tc, x, wv, beta, vo, k_bytes, k_scale, W, out):
         quantise_x(1, 0)
         for q in (2, 3):
             first_product(q, 0)
-        quantise_dv(0, 0, 4)
         quantise_k(12, 2)
         quantise_k(14, 1)
+        quantise_k(15, 1)
         quantise_x(1, 1)
         for q in (2, 3):
             first_product(q, 1)
-        quantise_k(15, 1)
+        quantise_dv(0, 0, 4)
 
         stage_wv(4, 4, gate="b")
         interleave_wv_pass_on_gpsimd(1, 0)
@@ -567,12 +567,11 @@ def tile_dpfpattention_pb_kernel(tc, x, wv, beta, vo, k_bytes, k_scale, W, out):
         interleave_wv(7, SCALAR)
         widen_k((18, 2), SCALAR, 1, 2)
         times_beta(0, 4, 8)
-        spread_beta(1, 5)
+        spread_beta(1, 4)
         for u in range(2):
             for q in (2, 3):
                 subtract_vo(q, u)
         interleave_k_on_tensor((16, 2))
-        interleave_k_on_tensor((18, 2), 1)
         quantise_wv(4, 2)
         for u in range(2):
             first_product(4, u)
@@ -585,24 +584,22 @@ def tile_dpfpattention_pb_kernel(tc, x, wv, beta, vo, k_bytes, k_scale, W, out):
             second_product(q)
 
         stage_dv(1, gate="b")
-        times_beta_on_gpsimd(1, 5)
+        times_beta_on_gpsimd(1, 4)
         stage_k(16, 4)
-        repeat_beta(2, 5)
-        repeat_beta(3, 2)
-        interleave_k((18, 2), SCALAR, 1, 2)
+        interleave_k((18, 2), SCALAR)
         widen_k((20, 2), SCALAR)
         fetch_k((16, 2))
-        fetch_k((18, 2), 1)
-        widen_k((24, 2), SCALAR)
-        widen_k((26, 2), SCALAR)
-        times_beta(1, 5, 8)
-        spread_beta(2, 5)
+        widen_k((22, 2), SCALAR)
+        times_beta(1, 4, 8)
+        spread_beta(2, 4)
         for q in (4, 5):
             for u in range(2):
                 subtract_vo(q, u)
         for q in (6, 7):
             for u in range(2):
                 first_product(q, u)
+        for first in (20, 22):
+            interleave_k_on_tensor((first, 2))
         add_memory_and_store(0, 0, 8)
         quantise_k(18, 2)
         quantise_dv(1, 0, 8)
@@ -612,33 +609,32 @@ def tile_dpfpattention_pb_kernel(tc, x, wv, beta, vo, k_bytes, k_scale, W, out):
             second_product(q)
 
         stage_dv(2, gate="b")
-        times_beta_on_gpsimd(2, 5)
-        times_beta(2, 5, 8)
+        times_beta_on_gpsimd(2, 4)
+        times_beta(2, 4, 8)
         spread_beta(3, 2)
-        for first in (24, 26):
-            interleave_k_on_tensor((first, 2))
-        widen_k((22, 2), SCALAR)
+        for first in (24, 26, 28):
+            widen_k((first, 2), SCALAR)
         stage_k(20, 4)
-        interleave_k((20, 2), SCALAR)
-        interleave_k((22, 2), SCALAR)
+        fetch_k((20, 2))
+        interleave_k_on_tensor((24, 2))
+        fetch_k((22, 2))
         widen_k((30, 2), SCALAR)
         stage_k(24, 4)
         fetch_k((24, 2))
-        widen_k((28, 2), SCALAR)
-        fetch_k((26, 2))
+        interleave_k((26, 2), SCALAR)
         stage_k(28, 4)
         interleave_k((28, 2), SCALAR)
+        interleave_k((30, 2), SCALAR)
         for q in (6, 7):
             for u in range(2):
                 subtract_vo(q, u)
         add_memory_and_store(2, 0, 8)
-        quantise_k(20, 4)
+        quantise_k(22, 2)
         quantise_dv(2, 0, 8)
+        quantise_k(20, 2)
         out_bank(ps_out, "out_bank", [(4, 0, 4), (5, 0, 4)])
         for q in (4, 5):
             second_product(q)
-        interleave_k_on_tensor((30, 2))
-        fetch_k((30, 2))
 
         stage_dv(3, gate="b")
         times_beta_on_gpsimd(3, 2)

@@ -28,6 +28,7 @@ COPY_RUN = 4
 BETA_RUN = 2
 REP = DH // BETA_RUN
 LINE = 4
+ON_GPSIMD = (0, 4, 4, 2)
 VECTOR, SCALAR, GPSIMD = "vector", "scalar", "gpsimd"
 
 
@@ -50,7 +51,7 @@ def tile_dpfpattention_pb_kernel(tc, x, wv, beta, vo, k_bytes, k_scale, W, out):
         ident_f32 = keep.tile([P, P], F32, name="ident_f32")
         ident_bf16 = keep.tile([P, P], BF16, name="ident_bf16")
         beta_rows = keep.tile([P, N], BF16, name="beta_rows")
-        pick = [keep.tile([P, H, REP], BF16, name="pick%d" % b) for b in range(B)]
+        pick = [keep.tile([P, 8 - ON_GPSIMD[o], REP], BF16, name="pick%d" % o) for o in range(OCTETS)]
         k_scales = keep.tile([P, PACK], F32, name="k_scales")
         x_codes = [
             [keep.tile([P, 2, 2 * P], U32, align_bytes=64, name="x_codes%d%d" % (b, u)) for u in range(2)]
@@ -119,12 +120,12 @@ def tile_dpfpattention_pb_kernel(tc, x, wv, beta, vo, k_bytes, k_scale, W, out):
             nc.scalar.activation(out=ident_f32[:], in_=ident_bf16[:], func=COPY)
             nc.vector.memset(beta_rows[32:64, :], 0.0)
             nc.vector.memset(beta_rows[64:128, :], 0.0)
-            nc.scalar.activation(
-                out=pick[0][:], in_=ident_bf16[:, 0:H].unsqueeze(2).to_broadcast([P, H, REP]), func=COPY
-            )
-            nc.vector.tensor_copy(
-                out=pick[1][:], in_=ident_bf16[:, H : 2 * H].unsqueeze(2).to_broadcast([P, H, REP])
-            )
+            for o in range(OCTETS):
+                row = H * (o % 2) + 8 * (o // 2)
+                n = 8 - ON_GPSIMD[o]
+                nc.vector.tensor_copy(
+                    out=pick[o][:], in_=ident_bf16[:, row + 8 - n : row + 8].unsqueeze(2).to_broadcast([P, n, REP])
+                )
 
 
         def staging(columns, gate):
@@ -260,6 +261,21 @@ def tile_dpfpattention_pb_kernel(tc, x, wv, beta, vo, k_bytes, k_scale, W, out):
             rows = wv_chunk(c)[:, g, :, a:e]
             interleave(engine, tile[:, QW * (j - first) + a : QW * (j - first) + e, :], rows)
 
+        w_halves = {}
+
+        def interleave_wv_half(j, half, engine, gate=None):
+            w_halves[(j, half)] = staging(P, gate)
+            rows = wv_chunk(j // 2)[:, j % 2, :, P * half : P * (half + 1)]
+            interleave(engine, w_halves[(j, half)][:], rows)
+
+        def quantise_wv_half(j, half):
+            cols = slice(QW * j + P * half, QW * j + P * (half + 1))
+            nc.vector.quantize_mx(
+                out=w_codes[:, cols].bitcast(FP8X4),
+                scales=w_exps[:, cols],
+                in_=w_halves[(j, half)][:].rearrange("p n t -> p (n t)"),
+            )
+
         def interleave_wv_pass_on_gpsimd(part, g):
             tile, first = w_staging[4 * part]
             nc.gpsimd.tensor_scalar(
@@ -304,7 +320,7 @@ def tile_dpfpattention_pb_kernel(tc, x, wv, beta, vo, k_bytes, k_scale, W, out):
                 nc.tensor.matmul(
                     bank[:, t, REP * a :],
                     lhsT=beta_rows[:, t::PACK],
-                    rhs=pick[b][:, h0 + a : h0 + 8].rearrange("p h c -> p (h c)"),
+                    rhs=pick[o][:].rearrange("p h c -> p (h c)"),
                     start=True,
                     stop=True,
                 )
@@ -326,6 +342,19 @@ def tile_dpfpattention_pb_kernel(tc, x, wv, beta, vo, k_bytes, k_scale, W, out):
                         start=(g == 0),
                         stop=(g == 1),
                     )
+
+        def keep_clock_up(pool, name):
+            bank = pool.tile([P, N], F32, name=name)
+            for a in range(2):
+                nc.tensor.matmul_mx(
+                    out=bank[:],
+                    lhsT=k_codes[:, 0:S].bitcast(FP8X4),
+                    lhsT_scale=k_exps[:, 0:S],
+                    rhs=k_codes[:, 0:N].bitcast(FP8X4),
+                    rhs_scale=k_exps[:, 0:N],
+                    start=True,
+                    stop=True,
+                )
 
         diff = {}
         dv_staging = {}
@@ -516,10 +545,9 @@ def tile_dpfpattention_pb_kernel(tc, x, wv, beta, vo, k_bytes, k_scale, W, out):
         first_product(0, 1)
         quantise_k(8, 4)
 
-        stage_wv(2, 1, gate="a")
         stage_wv(3, 1)
-        interleave_wv_part(2, GPSIMD, 0, 128)
-        interleave_wv_part(2, SCALAR, 128, QW)
+        interleave_wv_half(2, 0, GPSIMD, gate="a")
+        interleave_wv_half(2, 1, SCALAR)
         repeat_beta(1, 4)
         repeat_beta(2, 4)
         repeat_beta(3, 2)
@@ -531,7 +559,8 @@ def tile_dpfpattention_pb_kernel(tc, x, wv, beta, vo, k_bytes, k_scale, W, out):
             fetch_x(1, 0, g)
         for u in range(2):
             subtract_vo(0, u)
-        quantise_wv(2, 1)
+        quantise_wv_half(2, 1)
+        quantise_wv_half(2, 0)
         quantise_wv(3, 1)
         for u in range(2):
             first_product(1, u)
@@ -586,8 +615,8 @@ def tile_dpfpattention_pb_kernel(tc, x, wv, beta, vo, k_bytes, k_scale, W, out):
         stage_dv(1, gate="b")
         times_beta_on_gpsimd(1, 4)
         stage_k(16, 4)
-        interleave_k((18, 2), SCALAR)
         widen_k((20, 2), SCALAR)
+        interleave_k((18, 2), SCALAR)
         fetch_k((16, 2))
         widen_k((22, 2), SCALAR)
         times_beta(1, 4, 8)

@@ -28,7 +28,7 @@ COPY_RUN = 4
 BETA_RUN = 2
 REP = DH // BETA_RUN
 LINE = 4
-ON_GPSIMD = (0, 4, 4, 2)
+ON_GPSIMD = (0, 5, 5, 2)
 VECTOR, SCALAR, GPSIMD = "vector", "scalar", "gpsimd"
 
 
@@ -182,6 +182,14 @@ def tile_dpfpattention_pb_kernel(tc, x, wv, beta, vo, k_bytes, k_scale, W, out):
                 engine, staged_k(first + a, e - a), k_planar[first][:, :, a:e, :].rearrange("p t h s -> p t (h s)")
             )
 
+        def interleave_k_columns(group, engine, a, e):
+            first, n = group
+            interleave(
+                engine,
+                staged_k(first, n)[:, a:e, :],
+                k_planar[first][:].rearrange("p t h s -> p t (h s)")[:, :, a:e],
+            )
+
         def interleave_k_on_tensor(group, n=2):
             first = group[0]
             bank = ps_turn.tile([P, n * S, PACK], BF16, name="turned")
@@ -312,8 +320,8 @@ def tile_dpfpattention_pb_kernel(tc, x, wv, beta, vo, k_bytes, k_scale, W, out):
 
         beta_banks = {}
 
-        def spread_beta(o, a=0):
-            bank = ps_beta.tile([P, PACK, 8 * REP], BF16, name="beta_bank")
+        def spread_beta(o, a=0, pool=ps_beta, name="beta_bank"):
+            bank = pool.tile([P, PACK, 8 * REP], BF16, name=name)
             beta_banks[o] = bank
             b, h0 = o % 2, 8 * (o // 2)
             for t in range(PACK):
@@ -359,18 +367,32 @@ def tile_dpfpattention_pb_kernel(tc, x, wv, beta, vo, k_bytes, k_scale, W, out):
         diff = {}
         dv_staging = {}
 
+        paired = {}
+
         def subtract_vo(q, u):
             o = q // 2
             if o not in diff:
                 diff[o] = work.tile([P, PACK, 2 * QW], F32, name="diff", bufs=2)
-            nc.vector.tensor_tensor(
-                out=diff[o][:, 2 * u : 2 * u + 2, QW * (q % 2) : QW * (q % 2 + 1)].rearrange(
-                    "p t (h d) -> p t h d", h=4
-                ),
-                in0=v_banks[(q, u)][:].rearrange("p t (h d) -> p t h d", h=4),
-                in1=vo_sb[q][:, :, 2 * u : 2 * u + 2, :].rearrange("p h t d -> p t h d"),
-                op=SUB,
-            )
+                if ON_GPSIMD[o]:
+                    paired[o] = keep.tile([P, ON_GPSIMD[o], DH // 2, PACK, 2], F32, name="paired%d" % o)
+            slots = slice(2 * u, 2 * u + 2)
+            n = min(max(ON_GPSIMD[o] - 4 * (q % 2), 0), 4)
+            for h in range(n):
+                nc.vector.tensor_tensor(
+                    out=paired[o][:, 4 * (q % 2) + h, :, slots, :],
+                    in0=v_banks[(q, u)][:, :, DH * h : DH * (h + 1)].rearrange("p t (c i) -> p c t i", i=2),
+                    in1=vo_sb[q][:, h, slots, :].rearrange("p t (c i) -> p c t i", i=2),
+                    op=SUB,
+                )
+            if n < 4:
+                nc.vector.tensor_tensor(
+                    out=diff[o][:, slots, QW * (q % 2) + DH * n : QW * (q % 2 + 1)].rearrange(
+                        "p t (h d) -> p t h d", d=DH
+                    ),
+                    in0=v_banks[(q, u)][:, :, DH * n :].rearrange("p t (h d) -> p t h d", d=DH),
+                    in1=vo_sb[q][:, n:, slots, :].rearrange("p h t d -> p t h d"),
+                    op=SUB,
+                )
 
         def stage_dv(o, gate=None):
             if gate:
@@ -397,7 +419,7 @@ def tile_dpfpattention_pb_kernel(tc, x, wv, beta, vo, k_bytes, k_scale, W, out):
                 in_=dv_staging[o][:, DH * a : DH * e, :].rearrange("p n t -> p (n t)"),
             )
 
-        beta_sb = keep.tile([P, PACK, B * H], BF16, name="beta_sb")
+        beta_sb = keep.tile([P, B * H, PACK], F32, name="beta_sb")
         beta_turned = []
 
         def turn_beta():
@@ -408,31 +430,15 @@ def tile_dpfpattention_pb_kernel(tc, x, wv, beta, vo, k_bytes, k_scale, W, out):
 
         def fetch_beta(engine):
             copy = nc.vector.tensor_copy if engine == VECTOR else nc.scalar.copy
-            copy(out=beta_sb[:], in_=beta_turned[0][:, :, 0 : B * H])
+            copy(out=beta_sb[:], in_=beta_turned[0][:, :, 0 : B * H].rearrange("p t h -> p h t"))
 
-        beta_runs = {}
-
-        def repeat_beta(q, n):
-            o = q
+        def times_beta_on_gpsimd(o):
+            n = ON_GPSIMD[o]
             row = H * (o % 2) + 8 * (o // 2)
-            beta_runs[q] = keep.tile([P, n, DH // LINE, PACK], BF16, name="beta_runs%d" % q)
-            nc.scalar.copy(
-                out=beta_runs[q][:],
-                in_=beta_sb[:, :, row : row + n]
-                .rearrange("p t h -> p h t")
-                .unsqueeze(2)
-                .to_broadcast([P, n, DH // LINE, PACK]),
-            )
-
-        def times_beta_on_gpsimd(q, n):
-            o, h0 = q, 0
             nc.gpsimd.tensor_tensor(
-                out=dv_staging[q][:, 0 : DH * n, :].rearrange("p (c i) t -> p c t i", i=LINE),
-                in0=diff[o][:, :, DH * h0 : DH * (h0 + n)].rearrange("p t (c i) -> p c t i", i=LINE),
-                in1=beta_runs[q][:]
-                .rearrange("p h c t -> p (h c) t")
-                .unsqueeze(3)
-                .to_broadcast([P, n * DH // LINE, PACK, LINE]),
+                out=dv_staging[o][:, 0 : DH * n, :].rearrange("p (c i) t -> p c i t", i=2),
+                in0=paired[o][:].rearrange("p h c t i -> p (h c) i t"),
+                in1=beta_sb[:, row : row + n, :].unsqueeze(2).to_broadcast([P, n, DH, PACK]),
                 op=MULT,
             )
 
@@ -548,9 +554,6 @@ def tile_dpfpattention_pb_kernel(tc, x, wv, beta, vo, k_bytes, k_scale, W, out):
         stage_wv(3, 1)
         interleave_wv_half(2, 0, GPSIMD, gate="a")
         interleave_wv_half(2, 1, SCALAR)
-        repeat_beta(1, 4)
-        repeat_beta(2, 4)
-        repeat_beta(3, 2)
         interleave_wv(3, SCALAR)
         widen_k((12, 4), SCALAR)
         for g in range(2):
@@ -565,10 +568,9 @@ def tile_dpfpattention_pb_kernel(tc, x, wv, beta, vo, k_bytes, k_scale, W, out):
         for u in range(2):
             first_product(1, u)
 
-        stage_k(12, 3, gate="a")
-        interleave_k((12, 4), GPSIMD, 0, 3)
-        stage_k(15, 1)
-        interleave_k((12, 4), SCALAR, 3, 4)
+        stage_k(12, 4, gate="a")
+        interleave_k_columns((12, 4), GPSIMD, 0, 384)
+        interleave_k_columns((12, 4), SCALAR, 384, 4 * S)
         for g in range(2):
             turn_x(1, 1, g)
         fetch_x(1, 1, 0, gate="b")
@@ -580,9 +582,7 @@ def tile_dpfpattention_pb_kernel(tc, x, wv, beta, vo, k_bytes, k_scale, W, out):
         quantise_x(1, 0)
         for q in (2, 3):
             first_product(q, 0)
-        quantise_k(12, 2)
-        quantise_k(14, 1)
-        quantise_k(15, 1)
+        quantise_k(12, 4)
         quantise_x(1, 1)
         for q in (2, 3):
             first_product(q, 1)
@@ -596,7 +596,7 @@ def tile_dpfpattention_pb_kernel(tc, x, wv, beta, vo, k_bytes, k_scale, W, out):
         interleave_wv(7, SCALAR)
         widen_k((18, 2), SCALAR, 1, 2)
         times_beta(0, 4, 8)
-        spread_beta(1, 4)
+        spread_beta(1, 5)
         for u in range(2):
             for q in (2, 3):
                 subtract_vo(q, u)
@@ -613,22 +613,22 @@ def tile_dpfpattention_pb_kernel(tc, x, wv, beta, vo, k_bytes, k_scale, W, out):
             second_product(q)
 
         stage_dv(1, gate="b")
-        times_beta_on_gpsimd(1, 4)
+        times_beta_on_gpsimd(1)
         stage_k(16, 4)
         widen_k((20, 2), SCALAR)
         interleave_k((18, 2), SCALAR)
         fetch_k((16, 2))
         widen_k((22, 2), SCALAR)
-        times_beta(1, 4, 8)
-        spread_beta(2, 4)
+        widen_k((24, 2), SCALAR)
+        times_beta(1, 5, 8)
+        spread_beta(2, 5)
         for q in (4, 5):
             for u in range(2):
                 subtract_vo(q, u)
         for q in (6, 7):
             for u in range(2):
                 first_product(q, u)
-        for first in (20, 22):
-            interleave_k_on_tensor((first, 2))
+        interleave_k_on_tensor((20, 2))
         add_memory_and_store(0, 0, 8)
         quantise_k(18, 2)
         quantise_dv(1, 0, 8)
@@ -636,37 +636,40 @@ def tile_dpfpattention_pb_kernel(tc, x, wv, beta, vo, k_bytes, k_scale, W, out):
         out_bank(ps_out, "out_bank", [(2, 0, 4), (3, 0, 4)])
         for q in (2, 3):
             second_product(q)
+        interleave_k_on_tensor((24, 2))
 
         stage_dv(2, gate="b")
-        times_beta_on_gpsimd(2, 4)
-        times_beta(2, 4, 8)
+        times_beta_on_gpsimd(2)
+        times_beta(2, 5, 8)
         spread_beta(3, 2)
-        for first in (24, 26, 28):
-            widen_k((first, 2), SCALAR)
+        widen_k((26, 2), SCALAR)
         stage_k(20, 4)
+        interleave_k((22, 2), SCALAR)
         fetch_k((20, 2))
-        interleave_k_on_tensor((24, 2))
-        fetch_k((22, 2))
+        interleave_k_on_tensor((26, 2))
+        widen_k((28, 2), SCALAR)
         widen_k((30, 2), SCALAR)
         stage_k(24, 4)
         fetch_k((24, 2))
-        interleave_k((26, 2), SCALAR)
-        stage_k(28, 4)
-        interleave_k((28, 2), SCALAR)
-        interleave_k((30, 2), SCALAR)
         for q in (6, 7):
             for u in range(2):
                 subtract_vo(q, u)
         add_memory_and_store(2, 0, 8)
-        quantise_k(22, 2)
-        quantise_dv(2, 0, 8)
         quantise_k(20, 2)
+        quantise_dv(2, 0, 8)
+        quantise_k(22, 2)
         out_bank(ps_out, "out_bank", [(4, 0, 4), (5, 0, 4)])
         for q in (4, 5):
             second_product(q)
+        interleave_k_on_tensor((28, 2), 1)
+        stage_k(28, 4)
+        interleave_k((28, 2), SCALAR, 1, 2)
+        fetch_k((26, 2))
+        fetch_k((28, 2), 1)
+        interleave_k((30, 2), SCALAR)
 
         stage_dv(3, gate="b")
-        times_beta_on_gpsimd(3, 2)
+        times_beta_on_gpsimd(3)
         times_beta(3, 2, 8)
         add_memory_and_store(4, 0, 8)
         quantise_k(24, 4)

@@ -24,7 +24,7 @@ QUADS = B * H // 4
 OCTETS = B * H // 8
 QW = 4 * DH
 WV_LOADS = ((0, QW), (QW, QW), (2 * QW, 2 * QW))
-COPY_RUN = 4
+COPY_RUN = 2
 BETA_RUN = 2
 REP = DH // BETA_RUN
 LINE = 4
@@ -227,10 +227,11 @@ def tile_dpfpattention_pb_kernel(tc, x, wv, beta, vo, k_bytes, k_scale, W, out):
                 for e in range(2):
                     nc.tensor.transpose(bank[:, tt, e, :], words[:, e::2], ident_f32[:])
 
-        def fetch_x(b, u, g, gate=None):
-            if g == 0:
+        def fetch_x(b, u, g, gate=None, engine=SCALAR):
+            if (b, u) not in x_staging:
                 x_staging[(b, u)] = staging(N, gate)
-            nc.scalar.copy(
+            copy = nc.vector.tensor_copy if engine == VECTOR else nc.scalar.copy
+            copy(
                 out=x_staging[(b, u)][:, 2 * P * g : 2 * P * (g + 1), :]
                 .rearrange("p n j -> p (n j)")
                 .bitcast(F32)
@@ -663,10 +664,10 @@ def tile_dpfpattention_pb_kernel(tc, x, wv, beta, vo, k_bytes, k_scale, W, out):
             second_product(q)
         interleave_k_on_tensor((28, 2), 1)
         stage_k(28, 4)
-        interleave_k((28, 2), SCALAR, 1, 2)
         fetch_k((26, 2))
-        fetch_k((28, 2), 1)
         interleave_k((30, 2), SCALAR)
+        interleave_k((28, 2), SCALAR, 1, 2)
+        fetch_k((28, 2), 1)
 
         stage_dv(3, gate="b")
         times_beta_on_gpsimd(3)
@@ -676,13 +677,13 @@ def tile_dpfpattention_pb_kernel(tc, x, wv, beta, vo, k_bytes, k_scale, W, out):
         quantise_dv(3, 0, 4)
         out_bank(ps_v, "v_bank", [(6, 0, 4)])
         second_product(6)
-        quantise_k(28, 2)
-        quantise_dv(3, 4, 8)
-        out_bank(ps_v, "v_bank", [(7, 0, 2)])
-        second_product(7, 0, 2)
         quantise_k(30, 2)
+        quantise_dv(3, 4, 8)
         out_bank(ps_v, "v_bank", [(7, 2, 4)])
         second_product(7, 2, 4)
+        quantise_k(28, 2)
+        out_bank(ps_v, "v_bank", [(7, 0, 2)])
+        second_product(7, 0, 2)
         add_memory_and_store(6)
-        add_memory_and_store(7, 0, 2)
         add_memory_and_store(7, 2, 4)
+        add_memory_and_store(7, 0, 2)

@@ -72,7 +72,7 @@ def tile_dpfpattention_pb_kernel(tc, x, wv, beta, vo, k_bytes, k_scale, W, out):
         mem_sb = [keep.tile([P, 8, DH], BF16, name="mem_sb%d" % o) for o in range(OCTETS)]
         out_sb = [keep.tile([P, 8, DH], F32, name="out_sb%d" % o) for o in range(OCTETS)]
         x_sb = [[keep.tile([P, 2, D], BF16, name="x_sb%d%d" % (b, u)) for u in range(2)] for b in range(B)]
-        wv_sb = [keep.tile([P, 2, PACK, n], BF16, name="wv_sb%d" % c0) for c0, n in WV_LOADS]
+        wv_sb = [[keep.tile([P, PACK, n], BF16, name="wv_sb%d_%d" % (c0, g)) for g in range(2)] for c0, n in WV_LOADS]
 
 
         def load_k_scales():
@@ -107,7 +107,7 @@ def tile_dpfpattention_pb_kernel(tc, x, wv, beta, vo, k_bytes, k_scale, W, out):
         def load_wv(part, g):
             c0, n = WV_LOADS[part]
             nc.sync.dma_start(
-                out=wv_sb[part][:, g],
+                out=wv_sb[part][g][:],
                 in_=wv.rearrange("(g p t) w -> g p t w", g=2, t=PACK)[g][:, :, c0 : c0 + n],
             )
 
@@ -254,27 +254,22 @@ def tile_dpfpattention_pb_kernel(tc, x, wv, beta, vo, k_bytes, k_scale, W, out):
             for j in range(first, first + n):
                 w_staging[j] = (tile, first)
 
-        def wv_chunk(c):
+        def wv_piece(j):
+            c = j // 2
             part = min(c, 2)
-            return wv_sb[part][:, :, :, QW * (c - part) : QW * (c - part + 1)]
+            return wv_sb[part][j % 2][:, :, QW * (c - part) : QW * (c - part + 1)]
 
         def interleave_wv(j, engine):
             tile, first = w_staging[j]
             c, g = j // 2, j % 2
-            rows = wv_chunk(c)[:, g]
+            rows = wv_piece(j)
             interleave(engine, tile[:, QW * (j - first) : QW * (j - first + 1), :], rows)
-
-        def interleave_wv_part(j, engine, a, e):
-            tile, first = w_staging[j]
-            c, g = j // 2, j % 2
-            rows = wv_chunk(c)[:, g, :, a:e]
-            interleave(engine, tile[:, QW * (j - first) + a : QW * (j - first) + e, :], rows)
 
         w_halves = {}
 
         def interleave_wv_half(j, half, engine, gate=None):
             w_halves[(j, half)] = staging(P, gate)
-            rows = wv_chunk(j // 2)[:, j % 2, :, P * half : P * (half + 1)]
+            rows = wv_piece(j)[:, :, P * half : P * (half + 1)]
             interleave(engine, w_halves[(j, half)][:], rows)
 
         def quantise_wv_half(j, half):
@@ -285,29 +280,11 @@ def tile_dpfpattention_pb_kernel(tc, x, wv, beta, vo, k_bytes, k_scale, W, out):
                 in_=w_halves[(j, half)][:].rearrange("p n t -> p (n t)"),
             )
 
-        def interleave_wv_pass_on_gpsimd(part, g):
-            tile, first = w_staging[4 * part]
-            nc.gpsimd.tensor_scalar(
-                out=tile[:, QW * (4 * part - first) : QW * (4 * part - first + 4), :].rearrange(
-                    "p (c g n) t -> p c g n t", c=2, g=2
-                )[:, :, g],
-                in0=wv_sb[part + 1][:, g].rearrange("p t (c n) -> p c n t", c=2),
-                scalar1=1.0,
-                scalar2=0.0,
-                op0=MULT,
-                op1=ADD,
-            )
-
-        def interleave_wv_chunk_on_gpsimd(c):
-            tile, first = w_staging[2 * c]
-            nc.gpsimd.tensor_scalar(
-                out=tile[:, QW * (2 * c - first) : QW * (2 * c - first + 2), :].rearrange("p (g n) t -> p g n t", g=2),
-                in0=wv_chunk(c).rearrange("p g t n -> p g n t"),
-                scalar1=1.0,
-                scalar2=0.0,
-                op0=MULT,
-                op1=ADD,
-            )
+        def interleave_wv_pass_on_gpsimd(gate):
+            tile = staging(2 * QW, gate)
+            w_staging[4] = (tile, 4)
+            w_staging[6] = (tile, 5)
+            interleave(GPSIMD, tile[:], wv_sb[2][0][:])
 
         def quantise_wv(j, n):
             tile, first = w_staging[j]
@@ -373,7 +350,7 @@ def tile_dpfpattention_pb_kernel(tc, x, wv, beta, vo, k_bytes, k_scale, W, out):
         def subtract_vo(q, u):
             o = q // 2
             if o not in diff:
-                diff[o] = work.tile([P, PACK, 2 * QW], F32, name="diff", bufs=2)
+                diff[o] = work.tile([P, 2, PACK, QW], F32, name="diff", bufs=2)
                 if ON_GPSIMD[o]:
                     paired[o] = keep.tile([P, ON_GPSIMD[o], DH // 2, PACK, 2], F32, name="paired%d" % o)
             slots = slice(2 * u, 2 * u + 2)
@@ -387,7 +364,7 @@ def tile_dpfpattention_pb_kernel(tc, x, wv, beta, vo, k_bytes, k_scale, W, out):
                 )
             if n < 4:
                 nc.vector.tensor_tensor(
-                    out=diff[o][:, slots, QW * (q % 2) + DH * n : QW * (q % 2 + 1)].rearrange(
+                    out=diff[o][:, q % 2, slots, DH * n :].rearrange(
                         "p t (h d) -> p t h d", d=DH
                     ),
                     in0=v_banks[(q, u)][:, :, DH * n :].rearrange("p t (h d) -> p t h d", d=DH),
@@ -404,7 +381,9 @@ def tile_dpfpattention_pb_kernel(tc, x, wv, beta, vo, k_bytes, k_scale, W, out):
         def times_beta(o, a, e):
             nc.vector.tensor_tensor(
                 out=dv_staging[o][:, DH * a : DH * e, :].rearrange("p (c i) t -> p c t i", i=BETA_RUN),
-                in0=diff[o][:, :, DH * a : DH * e].rearrange("p t (c i) -> p c t i", i=BETA_RUN),
+                in0=diff[o][:, a // 4, :, DH * (a % 4) : DH * (a % 4 + e - a)].rearrange(
+                    "p t (c i) -> p c t i", i=BETA_RUN
+                ),
                 in1=beta_banks[o][:, :, REP * a : REP * e]
                 .rearrange("p t c -> p c t")
                 .unsqueeze(3)
@@ -556,7 +535,8 @@ def tile_dpfpattention_pb_kernel(tc, x, wv, beta, vo, k_bytes, k_scale, W, out):
         interleave_wv_half(2, 0, GPSIMD, gate="a")
         interleave_wv_half(2, 1, SCALAR)
         interleave_wv(3, SCALAR)
-        widen_k((12, 4), SCALAR)
+        widen_k((12, 3), SCALAR)
+        widen_k((15, 1), SCALAR)
         for g in range(2):
             turn_x(1, 0, g)
         for g in range(2):
@@ -570,8 +550,8 @@ def tile_dpfpattention_pb_kernel(tc, x, wv, beta, vo, k_bytes, k_scale, W, out):
             first_product(1, u)
 
         stage_k(12, 4, gate="a")
-        interleave_k_columns((12, 4), GPSIMD, 0, 384)
-        interleave_k_columns((12, 4), SCALAR, 384, 4 * S)
+        interleave_k((12, 3), GPSIMD)
+        interleave_k((15, 1), SCALAR)
         for g in range(2):
             turn_x(1, 1, g)
         fetch_x(1, 1, 0, gate="b")
@@ -589,8 +569,9 @@ def tile_dpfpattention_pb_kernel(tc, x, wv, beta, vo, k_bytes, k_scale, W, out):
             first_product(q, 1)
         quantise_dv(0, 0, 4)
 
-        stage_wv(4, 4, gate="b")
-        interleave_wv_pass_on_gpsimd(1, 0)
+        interleave_wv_pass_on_gpsimd("b")
+        stage_wv(5, 1)
+        stage_wv(7, 1)
         widen_k((16, 2), SCALAR)
         widen_k((18, 2), SCALAR, 0, 1)
         interleave_wv(5, SCALAR)
@@ -602,10 +583,12 @@ def tile_dpfpattention_pb_kernel(tc, x, wv, beta, vo, k_bytes, k_scale, W, out):
             for q in (2, 3):
                 subtract_vo(q, u)
         interleave_k_on_tensor((16, 2))
-        quantise_wv(4, 2)
+        quantise_wv(4, 1)
+        quantise_wv(5, 1)
         for u in range(2):
             first_product(4, u)
-        quantise_wv(6, 2)
+        quantise_wv(7, 1)
+        quantise_wv(6, 1)
         for u in range(2):
             first_product(5, u)
         quantise_dv(0, 4, 8)
@@ -671,7 +654,8 @@ def tile_dpfpattention_pb_kernel(tc, x, wv, beta, vo, k_bytes, k_scale, W, out):
 
         stage_dv(3, gate="b")
         times_beta_on_gpsimd(3)
-        times_beta(3, 2, 8)
+        times_beta(3, 2, 4)
+        times_beta(3, 4, 8)
         add_memory_and_store(4, 0, 8)
         quantise_k(24, 4)
         quantise_dv(3, 0, 4)

@@ -24,7 +24,7 @@ QUADS = B * H // 4
 OCTETS = B * H // 8
 QW = 4 * DH
 WV_LOADS = ((0, QW), (QW, QW), (2 * QW, 2 * QW))
-COPY_RUN = 2
+COPY_RUN = {"vector": 4, "scalar": 2}
 BETA_RUN = 2
 REP = DH // BETA_RUN
 LINE = 4
@@ -141,8 +141,8 @@ def tile_dpfpattention_pb_kernel(tc, x, wv, beta, vo, k_bytes, k_scale, W, out):
                 return
             copy = nc.vector.tensor_copy if engine == VECTOR else nc.scalar.copy
             copy(
-                out=dst.rearrange("p (c i) t -> p c t i", i=COPY_RUN),
-                in_=src.rearrange("p t (c i) -> p c t i", i=COPY_RUN),
+                out=dst.rearrange("p (c i) t -> p c t i", i=COPY_RUN[engine]),
+                in_=src.rearrange("p t (c i) -> p c t i", i=COPY_RUN[engine]),
             )
 
 

@@ -29,6 +29,7 @@ BETA_RUN = 2
 REP = DH // BETA_RUN
 LINE = 4
 ON_GPSIMD = (0, 5, 5, 2)
+ON_SCALAR = (0, 0, 0, 1)
 VECTOR, SCALAR, GPSIMD = "vector", "scalar", "gpsimd"
 
 
@@ -51,7 +52,7 @@ def tile_dpfpattention_pb_kernel(tc, x, wv, beta, vo, k_bytes, k_scale, W, out):
         ident_f32 = keep.tile([P, P], F32, name="ident_f32")
         ident_bf16 = keep.tile([P, P], BF16, name="ident_bf16")
         beta_rows = keep.tile([P, N], BF16, name="beta_rows")
-        pick = [keep.tile([P, 8 - ON_GPSIMD[o], REP], BF16, name="pick%d" % o) for o in range(OCTETS)]
+        pick = [keep.tile([P, 8 - ON_GPSIMD[o] - ON_SCALAR[o], REP], BF16, name="pick%d" % o) for o in range(OCTETS)]
         k_scales = keep.tile([P, PACK], F32, name="k_scales")
         x_codes = [
             [keep.tile([P, 2, 2 * P], U32, align_bytes=64, name="x_codes%d%d" % (b, u)) for u in range(2)]
@@ -122,9 +123,9 @@ def tile_dpfpattention_pb_kernel(tc, x, wv, beta, vo, k_bytes, k_scale, W, out):
             nc.vector.memset(beta_rows[64:128, :], 0.0)
             for o in range(OCTETS):
                 row = H * (o % 2) + 8 * (o // 2)
-                n = 8 - ON_GPSIMD[o]
+                a, e = ON_GPSIMD[o], 8 - ON_SCALAR[o]
                 nc.vector.tensor_copy(
-                    out=pick[o][:], in_=ident_bf16[:, row + 8 - n : row + 8].unsqueeze(2).to_broadcast([P, n, REP])
+                    out=pick[o][:], in_=ident_bf16[:, row + a : row + e].unsqueeze(2).to_broadcast([P, e - a, REP])
                 )
 
 
@@ -304,7 +305,7 @@ def tile_dpfpattention_pb_kernel(tc, x, wv, beta, vo, k_bytes, k_scale, W, out):
             b, h0 = o % 2, 8 * (o // 2)
             for t in range(PACK):
                 nc.tensor.matmul(
-                    bank[:, t, REP * a :],
+                    bank[:, t, REP * a : REP * (8 - ON_SCALAR[o])],
                     lhsT=beta_rows[:, t::PACK],
                     rhs=pick[o][:].rearrange("p h c -> p (h c)"),
                     start=True,
@@ -421,6 +422,24 @@ def tile_dpfpattention_pb_kernel(tc, x, wv, beta, vo, k_bytes, k_scale, W, out):
                 in1=beta_sb[:, row : row + n, :].unsqueeze(2).to_broadcast([P, n, DH, PACK]),
                 op=MULT,
             )
+
+        dv_planar = {}
+
+        def times_beta_on_scalar(o, h):
+            n = ON_SCALAR[o]
+            if o not in dv_planar:
+                dv_planar[o] = keep.tile([P, PACK, n * DH], BF16, name="dv_planar%d" % o)
+            row = H * (o % 2) + 8 * (o // 2) + h
+            for t in range(PACK):
+                nc.scalar.activation(
+                    out=dv_planar[o][:, t, DH * (h - 8 + n) : DH * (h - 7 + n)],
+                    in_=diff[o][:, 1, t, DH * (h - 4) : DH * (h - 3)],
+                    func=COPY,
+                    scale=beta_sb[:, row, t : t + 1],
+                )
+
+        def interleave_dv(o):
+            interleave(SCALAR, dv_staging[o][:, DH * (8 - ON_SCALAR[o]) :, :], dv_planar[o][:])
 
 
         out_banks = {}
@@ -579,8 +598,8 @@ def tile_dpfpattention_pb_kernel(tc, x, wv, beta, vo, k_bytes, k_scale, W, out):
         widen_k((18, 2), SCALAR, 1, 2)
         times_beta(0, 4, 8)
         spread_beta(1, 5)
-        for u in range(2):
-            for q in (2, 3):
+        for q in (2, 3):
+            for u in range(2):
                 subtract_vo(q, u)
         interleave_k_on_tensor((16, 2))
         quantise_wv(4, 1)
@@ -647,15 +666,17 @@ def tile_dpfpattention_pb_kernel(tc, x, wv, beta, vo, k_bytes, k_scale, W, out):
             second_product(q)
         interleave_k_on_tensor((28, 2), 1)
         stage_k(28, 4)
+        times_beta_on_scalar(3, 7)
         fetch_k((26, 2))
-        interleave_k((30, 2), SCALAR)
-        interleave_k((28, 2), SCALAR, 1, 2)
-        fetch_k((28, 2), 1)
 
         stage_dv(3, gate="b")
         times_beta_on_gpsimd(3)
+        interleave_k((30, 2), SCALAR)
+        interleave_dv(3)
+        interleave_k((28, 2), SCALAR, 1, 2)
+        fetch_k((28, 2), 1)
         times_beta(3, 2, 4)
-        times_beta(3, 4, 8)
+        times_beta(3, 4, 7)
         add_memory_and_store(4, 0, 8)
         quantise_k(24, 4)
         quantise_dv(3, 0, 4)

@@ -23,19 +23,21 @@ PACK = 4
 QUADS = B * H // 4
 OCTETS = B * H // 8
 QW = 4 * DH
-WV_LOADS = ((0, QW), (QW, QW), (2 * QW, 2 * QW))
-COPY_RUN = {"vector": 4, "scalar": 2}
-BETA_RUN = 2
-REP = DH // BETA_RUN
-LINE = 4
-ON_GPSIMD = (0, 5, 5, 2)
-ON_SCALAR = (0, 0, 0, 1)
+RUN = {"vector": 4, "scalar": 2}
+SCALE_RUN = 2
+STAGES = {256: 5, 512: 6}
+PLANARS = {1: 2, 2: 4, 3: 1}
+OCTET_ORDER = ((0, 0), (0, 8), (1, 0), (1, 8))
 VECTOR, SCALAR, GPSIMD = "vector", "scalar", "gpsimd"
 
 
 def batch_and_chunk(q):
-    o = q // 2
-    return o % 2, 2 * (o // 2) + q % 2
+    b, h0 = batch_and_head(q // 2)
+    return b, h0 // 4 + q % 2
+
+
+def batch_and_head(o):
+    return OCTET_ORDER[o]
 
 
 def tile_dpfpattention_pb_kernel(tc, x, wv, beta, vo, k_bytes, k_scale, W, out):
@@ -52,7 +54,6 @@ def tile_dpfpattention_pb_kernel(tc, x, wv, beta, vo, k_bytes, k_scale, W, out):
         ident_f32 = keep.tile([P, P], F32, name="ident_f32")
         ident_bf16 = keep.tile([P, P], BF16, name="ident_bf16")
         beta_rows = keep.tile([P, N], BF16, name="beta_rows")
-        pick = [keep.tile([P, 8 - ON_GPSIMD[o] - ON_SCALAR[o], REP], BF16, name="pick%d" % o) for o in range(OCTETS)]
         k_scales = keep.tile([P, PACK], F32, name="k_scales")
         x_codes = [
             [keep.tile([P, 2, 2 * P], U32, align_bytes=64, name="x_codes%d%d" % (b, u)) for u in range(2)]
@@ -62,8 +63,8 @@ def tile_dpfpattention_pb_kernel(tc, x, wv, beta, vo, k_bytes, k_scale, W, out):
             [keep.tile([P, 2, 2 * P], U8, align_bytes=64, name="x_exps%d%d" % (b, u)) for u in range(2)]
             for b in range(B)
         ]
-        w_codes = keep.tile([P, 8 * QW], U32, align_bytes=64, name="w_codes")
-        w_exps = keep.tile([P, 8 * QW], U8, align_bytes=64, name="w_exps")
+        w_codes = keep.tile([P, 2, D], U32, align_bytes=64, name="w_codes")
+        w_exps = keep.tile([P, 2, D], U8, align_bytes=64, name="w_exps")
         k_codes = keep.tile([P, B * H * S], U32, align_bytes=64, name="k_codes")
         k_exps = keep.tile([P, B * H * S], U8, align_bytes=64, name="k_exps")
         dv_codes = keep.tile([P, B * H * DH], U32, align_bytes=64, name="dv_codes")
@@ -71,9 +72,8 @@ def tile_dpfpattention_pb_kernel(tc, x, wv, beta, vo, k_bytes, k_scale, W, out):
         k_raw = [keep.tile([P, 4, PACK * S], U8, name="k_raw%d" % q) for q in range(QUADS)]
         vo_sb = [keep.tile([P, 4, PACK, DH], BF16, name="vo_sb%d" % q) for q in range(QUADS)]
         mem_sb = [keep.tile([P, 8, DH], BF16, name="mem_sb%d" % o) for o in range(OCTETS)]
-        out_sb = [keep.tile([P, 8, DH], F32, name="out_sb%d" % o) for o in range(OCTETS)]
         x_sb = [[keep.tile([P, 2, D], BF16, name="x_sb%d%d" % (b, u)) for u in range(2)] for b in range(B)]
-        wv_sb = [[keep.tile([P, PACK, n], BF16, name="wv_sb%d_%d" % (c0, g)) for g in range(2)] for c0, n in WV_LOADS]
+        wv_sb = {}
 
 
         def load_k_scales():
@@ -82,15 +82,10 @@ def tile_dpfpattention_pb_kernel(tc, x, wv, beta, vo, k_bytes, k_scale, W, out):
         def load_beta():
             nc.sync.dma_start(out=beta_rows[0 : B * H, :], in_=beta.rearrange("b h n -> (b h) n"))
 
-        def load_k(q):
+        def load_k(q, a=0, e=4):
             b, c = batch_and_chunk(q)
             nc.sync.dma_start(
-                out=k_raw[q][:], in_=k_bytes[b, 4 * c : 4 * c + 4].rearrange("h (p t) s -> p h (t s)", t=PACK)
-            )
-
-        def load_first_k_pair(a):
-            nc.sync.dma_start(
-                out=k_raw[0][:, a : a + 2], in_=k_bytes[0, a : a + 2].rearrange("h (p t) s -> p h (t s)", t=PACK)
+                out=k_raw[q][:, a:e], in_=k_bytes[b, 4 * c + a : 4 * c + e].rearrange("h (p t) s -> p h (t s)", t=PACK)
             )
 
         def load_vo(q):
@@ -105,15 +100,17 @@ def tile_dpfpattention_pb_kernel(tc, x, wv, beta, vo, k_bytes, k_scale, W, out):
                 out=x_sb[b][u][:], in_=x[b].rearrange("(m t) k -> m t k", t=PACK)[:, 2 * u : 2 * u + 2, :]
             )
 
-        def load_wv(part, g):
-            c0, n = WV_LOADS[part]
+        def load_wv(g, c, n):
+            tile = keep.tile([P, PACK, n * QW], BF16, name="wv_sb%d_%d" % (g, c))
+            for j in range(n):
+                wv_sb[(g, c + j)] = tile[:, :, QW * j : QW * (j + 1)]
+            wv_sb[(g, c, n)] = tile
             nc.sync.dma_start(
-                out=wv_sb[part][g][:],
-                in_=wv.rearrange("(g p t) w -> g p t w", g=2, t=PACK)[g][:, :, c0 : c0 + n],
+                out=tile[:], in_=wv.rearrange("(g p t) w -> g p t w", g=2, t=PACK)[g][:, :, QW * c : QW * (c + n)]
             )
 
         def load_memory(o):
-            b, h0 = o % 2, 8 * (o // 2)
+            b, h0 = batch_and_head(o)
             nc.sync.dma_start(out=mem_sb[o][:], in_=W[b, h0 : h0 + 8].rearrange("h s d -> s h d"))
 
         def make_constants():
@@ -121,18 +118,35 @@ def tile_dpfpattention_pb_kernel(tc, x, wv, beta, vo, k_bytes, k_scale, W, out):
             nc.scalar.activation(out=ident_f32[:], in_=ident_bf16[:], func=COPY)
             nc.vector.memset(beta_rows[32:64, :], 0.0)
             nc.vector.memset(beta_rows[64:128, :], 0.0)
-            for o in range(OCTETS):
-                row = H * (o % 2) + 8 * (o // 2)
-                a, e = ON_GPSIMD[o], 8 - ON_SCALAR[o]
-                nc.vector.tensor_copy(
-                    out=pick[o][:], in_=ident_bf16[:, row + a : row + e].unsqueeze(2).to_broadcast([P, e - a, REP])
+
+
+        factors = {}
+        beta_sb = keep.tile([P, B * H, PACK], F32, name="beta_sb")
+
+        def place_scales():
+            bank = ps_out.tile([P, PACK], F32, name="out_bank")
+            factors["scale"] = bank
+            nc.tensor.matmul(bank[:], lhsT=ident_f32[:], rhs=k_scales[:], start=True, stop=True)
+
+        def place_beta():
+            both = ps_beta.tile([P, B * H + 1, PACK], F32, name="beta_bank")
+            bank = both[:, 0 : B * H, :]
+            factors["beta"] = bank
+            factors["late scale"] = both[:, B * H, :]
+            nc.tensor.matmul(both[:, B * H, :], lhsT=ident_f32[:], rhs=k_scales[:], start=True, stop=True)
+            for t in range(PACK):
+                nc.tensor.matmul(
+                    bank[:, :, t], lhsT=beta_rows[:, t::PACK], rhs=ident_bf16[:, 0 : B * H], start=True, stop=True
                 )
 
+        def fetch_beta():
+            nc.scalar.copy(out=beta_sb[:], in_=factors["beta"][:])
 
-        def staging(columns, gate):
+
+        def staging(columns, gate=None):
             if gate:
                 return work.tile([P, columns, PACK], BF16, align_bytes=64, name="gate_" + gate, bufs=1)
-            return work.tile([P, columns, PACK], BF16, align_bytes=64, name="stage%d" % columns, bufs=4)
+            return work.tile([P, columns, PACK], BF16, align_bytes=64, name="stage%d" % columns, bufs=STAGES[columns])
 
         def interleave(engine, dst, src):
             if engine == GPSIMD:
@@ -142,19 +156,51 @@ def tile_dpfpattention_pb_kernel(tc, x, wv, beta, vo, k_bytes, k_scale, W, out):
                 return
             copy = nc.vector.tensor_copy if engine == VECTOR else nc.scalar.copy
             copy(
-                out=dst.rearrange("p (c i) t -> p c t i", i=COPY_RUN[engine]),
-                in_=src.rearrange("p t (c i) -> p c t i", i=COPY_RUN[engine]),
+                out=dst.rearrange("p (c i) t -> p c t i", i=RUN[engine]),
+                in_=src.rearrange("p t (c i) -> p c t i", i=RUN[engine]),
             )
 
+        def turn(src, pool=ps_turn, name="turned"):
+            n = src.shape[2]
+            bank = pool.tile([P, n, PACK], BF16, name=name)
+            for a in range(0, n, P):
+                nc.tensor.matmul(
+                    bank[:, a : a + P, :].rearrange("p s t -> p t s"),
+                    lhsT=ident_bf16[:],
+                    rhs=src[:, :, a : a + P],
+                    start=True,
+                    stop=True,
+                )
+            return bank
 
+
+        k_wide = {}
         k_planar = {}
         k_staging = {}
         k_banks = {}
 
+        def cast_k(first, n):
+            tile = work.tile([P, n, PACK, S], BF16, name="k_wide%d" % n, bufs=3)
+            for h in range(n):
+                k_wide[first + h] = tile[:, h]
+            nc.scalar.copy(
+                out=tile[:].rearrange("p h t s -> p (h t s)"),
+                in_=k_raw[first // 4][:, first % 4 : first % 4 + n, :].rearrange("p h c -> p (h c)").bitcast(FP8),
+            )
+
+        def scale_k(first, n, table="scale"):
+            for h in range(first, first + n):
+                nc.vector.tensor_tensor(
+                    out=staged_k(h, 1).rearrange("p (c i) t -> p c t i", i=SCALE_RUN),
+                    in0=k_wide[h].rearrange("p t (c i) -> p c t i", i=SCALE_RUN),
+                    in1=factors[table][:].unsqueeze(1).unsqueeze(3).to_broadcast([P, S // SCALE_RUN, PACK, SCALE_RUN]),
+                    op=MULT,
+                )
+
         def widen_k(group, engine, a=0, e=None):
             first, n = group
             if first not in k_planar:
-                k_planar[first] = work.tile([P, PACK, n, S], BF16, name="k_planar%d" % n, bufs=2 if n > 2 else 5)
+                k_planar[first] = work.tile([P, PACK, n, S], BF16, name="k_planar%d" % n, bufs=PLANARS[n])
             for h in range(a, n if e is None else e):
                 for t in range(PACK):
                     codes = k_raw[(first + h) // 4][:, (first + h) % 4, S * t : S * (t + 1)].bitcast(FP8)
@@ -166,47 +212,28 @@ def tile_dpfpattention_pb_kernel(tc, x, wv, beta, vo, k_bytes, k_scale, W, out):
                     else:
                         nc.scalar.activation(out=dst, in_=codes, func=COPY, scale=k_scales[:, t : t + 1])
 
-        def stage_k(first, n, gate=None, spare=0):
-            tile = staging(n * S + spare, gate)
+        def stage_k(first, n, gate=None):
+            tile = staging(n * S, gate)
             for h in range(first, first + n):
                 k_staging[h] = (tile, first)
-            return tile[:, n * S :, :]
 
         def staged_k(first, n):
             tile, base = k_staging[first]
             return tile[:, S * (first - base) : S * (first - base + n), :]
 
+        def planar_k(group, a, e):
+            first, n = group
+            return k_planar[first][:, :, a : n if e is None else e, :].rearrange("p t h s -> p t (h s)")
+
         def interleave_k(group, engine, a=0, e=None):
-            first, n = group
-            e = n if e is None else e
-            interleave(
-                engine, staged_k(first + a, e - a), k_planar[first][:, :, a:e, :].rearrange("p t h s -> p t (h s)")
-            )
+            src = planar_k(group, a, e)
+            interleave(engine, staged_k(group[0] + a, src.shape[2] // S), src)
 
-        def interleave_k_columns(group, engine, a, e):
-            first, n = group
-            interleave(
-                engine,
-                staged_k(first, n)[:, a:e, :],
-                k_planar[first][:].rearrange("p t h s -> p t (h s)")[:, :, a:e],
-            )
+        def turn_k(group, a=0, e=None, *bank):
+            k_banks[group[0] + a] = turn(planar_k(group, a, e), *bank)
 
-        def interleave_k_on_tensor(group, n=2):
-            first = group[0]
-            bank = ps_turn.tile([P, n * S, PACK], BF16, name="turned")
-            k_banks[first] = bank
-            for h in range(n):
-                nc.tensor.matmul(
-                    bank[:, S * h : S * (h + 1), :].rearrange("p s t -> p t s"),
-                    lhsT=ident_bf16[:],
-                    rhs=k_planar[first][:, :, h, :],
-                    start=True,
-                    stop=True,
-                )
-
-        def fetch_k(group, n=2):
-            first = group[0]
-            nc.scalar.copy(out=staged_k(first, n), in_=k_banks[first][:])
+        def fetch_k(first):
+            nc.scalar.copy(out=staged_k(first, k_banks[first].shape[1] // S), in_=k_banks[first][:])
 
         def quantise_k(first, n):
             cols = slice(S * first, S * (first + n))
@@ -220,8 +247,8 @@ def tile_dpfpattention_pb_kernel(tc, x, wv, beta, vo, k_bytes, k_scale, W, out):
         x_staging = {}
         x_banks = {}
 
-        def turn_x(b, u, g):
-            bank = ps_turn.tile([P, 2, 2, P], F32, name="turned")
+        def turn_x(b, u, g, pool=ps_turn, name="turned"):
+            bank = pool.tile([P, 2, 2, P], F32, name=name)
             x_banks[(b, u, g)] = bank
             for tt in range(2):
                 words = x_sb[b][u][:, tt, 512 * g : 512 * (g + 1)].bitcast(F32)
@@ -249,68 +276,36 @@ def tile_dpfpattention_pb_kernel(tc, x, wv, beta, vo, k_bytes, k_scale, W, out):
 
 
         w_staging = {}
+        w_banks = {}
 
-        def stage_wv(first, n, gate=None):
+        def stage_wv(g, c, n=1, gate=None):
             tile = staging(n * QW, gate)
-            for j in range(first, first + n):
-                w_staging[j] = (tile, first)
+            for j in range(n):
+                w_staging[(g, c + j)] = (tile, c)
 
-        def wv_piece(j):
-            c = j // 2
-            part = min(c, 2)
-            return wv_sb[part][j % 2][:, :, QW * (c - part) : QW * (c - part + 1)]
+        def staged_wv(g, c, n):
+            tile, base = w_staging[(g, c)]
+            return tile[:, QW * (c - base) : QW * (c - base + n), :]
 
-        def interleave_wv(j, engine):
-            tile, first = w_staging[j]
-            c, g = j // 2, j % 2
-            rows = wv_piece(j)
-            interleave(engine, tile[:, QW * (j - first) : QW * (j - first + 1), :], rows)
+        def interleave_wv(g, c, engine, n=1, a=0, e=None):
+            src = wv_sb[(g, c)] if n == 1 else wv_sb[(g, c, n)][:]
+            e = n * QW if e is None else e
+            interleave(engine, staged_wv(g, c, n)[:, a:e, :], src[:, :, a:e])
 
-        w_halves = {}
+        def turn_wv(g, c, *bank):
+            w_banks[(g, c)] = turn(wv_sb[(g, c)], *bank)
 
-        def interleave_wv_half(j, half, engine, gate=None):
-            w_halves[(j, half)] = staging(P, gate)
-            rows = wv_piece(j)[:, :, P * half : P * (half + 1)]
-            interleave(engine, w_halves[(j, half)][:], rows)
+        def fetch_wv(g, c):
+            nc.scalar.copy(out=staged_wv(g, c, 1), in_=w_banks[(g, c)][:])
 
-        def quantise_wv_half(j, half):
-            cols = slice(QW * j + P * half, QW * j + P * (half + 1))
+        def quantise_wv(g, c, n=1):
+            cols = slice(QW * c, QW * (c + n))
             nc.vector.quantize_mx(
-                out=w_codes[:, cols].bitcast(FP8X4),
-                scales=w_exps[:, cols],
-                in_=w_halves[(j, half)][:].rearrange("p n t -> p (n t)"),
+                out=w_codes[:, g, cols].bitcast(FP8X4),
+                scales=w_exps[:, g, cols],
+                in_=staged_wv(g, c, n).rearrange("p n t -> p (n t)"),
             )
 
-        def interleave_wv_pass_on_gpsimd(gate):
-            tile = staging(2 * QW, gate)
-            w_staging[4] = (tile, 4)
-            w_staging[6] = (tile, 5)
-            interleave(GPSIMD, tile[:], wv_sb[2][0][:])
-
-        def quantise_wv(j, n):
-            tile, first = w_staging[j]
-            cols = slice(QW * j, QW * (j + n))
-            nc.vector.quantize_mx(
-                out=w_codes[:, cols].bitcast(FP8X4),
-                scales=w_exps[:, cols],
-                in_=tile[:, QW * (j - first) : QW * (j - first + n), :].rearrange("p n t -> p (n t)"),
-            )
-
-
-        beta_banks = {}
-
-        def spread_beta(o, a=0, pool=ps_beta, name="beta_bank"):
-            bank = pool.tile([P, PACK, 8 * REP], BF16, name=name)
-            beta_banks[o] = bank
-            b, h0 = o % 2, 8 * (o // 2)
-            for t in range(PACK):
-                nc.tensor.matmul(
-                    bank[:, t, REP * a : REP * (8 - ON_SCALAR[o])],
-                    lhsT=beta_rows[:, t::PACK],
-                    rhs=pick[o][:].rearrange("p h c -> p (h c)"),
-                    start=True,
-                    stop=True,
-                )
 
         v_banks = {}
 
@@ -324,71 +319,44 @@ def tile_dpfpattention_pb_kernel(tc, x, wv, beta, vo, k_bytes, k_scale, W, out):
                         out=bank[:, tt, :],
                         lhsT=x_codes[b][u][:, g, P * tt : P * (tt + 1)].bitcast(FP8X4),
                         lhsT_scale=x_exps[b][u][:, g, P * tt : P * (tt + 1)],
-                        rhs=w_codes[:, QW * (2 * c + g) : QW * (2 * c + g + 1)].bitcast(FP8X4),
-                        rhs_scale=w_exps[:, QW * (2 * c + g) : QW * (2 * c + g + 1)],
+                        rhs=w_codes[:, g, QW * c : QW * (c + 1)].bitcast(FP8X4),
+                        rhs_scale=w_exps[:, g, QW * c : QW * (c + 1)],
                         start=(g == 0),
                         stop=(g == 1),
                     )
 
-        def keep_clock_up(pool, name):
-            bank = pool.tile([P, N], F32, name=name)
-            for a in range(2):
-                nc.tensor.matmul_mx(
-                    out=bank[:],
-                    lhsT=k_codes[:, 0:S].bitcast(FP8X4),
-                    lhsT_scale=k_exps[:, 0:S],
-                    rhs=k_codes[:, 0:N].bitcast(FP8X4),
-                    rhs_scale=k_exps[:, 0:N],
-                    start=True,
-                    stop=True,
-                )
-
         diff = {}
         dv_staging = {}
-
-        paired = {}
 
         def subtract_vo(q, u):
             o = q // 2
             if o not in diff:
-                diff[o] = work.tile([P, 2, PACK, QW], F32, name="diff", bufs=2)
-                if ON_GPSIMD[o]:
-                    paired[o] = keep.tile([P, ON_GPSIMD[o], DH // 2, PACK, 2], F32, name="paired%d" % o)
-            slots = slice(2 * u, 2 * u + 2)
-            n = min(max(ON_GPSIMD[o] - 4 * (q % 2), 0), 4)
-            for h in range(n):
-                nc.vector.tensor_tensor(
-                    out=paired[o][:, 4 * (q % 2) + h, :, slots, :],
-                    in0=v_banks[(q, u)][:, :, DH * h : DH * (h + 1)].rearrange("p t (c i) -> p c t i", i=2),
-                    in1=vo_sb[q][:, h, slots, :].rearrange("p t (c i) -> p c t i", i=2),
-                    op=SUB,
-                )
-            if n < 4:
-                nc.vector.tensor_tensor(
-                    out=diff[o][:, q % 2, slots, DH * n :].rearrange(
-                        "p t (h d) -> p t h d", d=DH
-                    ),
-                    in0=v_banks[(q, u)][:, :, DH * n :].rearrange("p t (h d) -> p t h d", d=DH),
-                    in1=vo_sb[q][:, n:, slots, :].rearrange("p h t d -> p t h d"),
-                    op=SUB,
-                )
-
-        def stage_dv(o, gate=None):
-            if gate:
-                dv_staging[o] = staging(2 * QW, gate)
-            else:
-                dv_staging[o] = work.tile([P, 2 * QW, PACK], BF16, align_bytes=64, name="dv_staging", bufs=1)
-
-        def times_beta(o, a, e):
+                diff[o] = work.tile([P, 2, 2 * QW, 2], F32, name="diff", bufs=2)
             nc.vector.tensor_tensor(
-                out=dv_staging[o][:, DH * a : DH * e, :].rearrange("p (c i) t -> p c t i", i=BETA_RUN),
-                in0=diff[o][:, a // 4, :, DH * (a % 4) : DH * (a % 4 + e - a)].rearrange(
-                    "p t (c i) -> p c t i", i=BETA_RUN
-                ),
-                in1=beta_banks[o][:, :, REP * a : REP * e]
-                .rearrange("p t c -> p c t")
-                .unsqueeze(3)
-                .to_broadcast([P, (e - a) * REP, PACK, BETA_RUN]),
+                out=diff[o][:, u, QW * (q % 2) : QW * (q % 2 + 1), :],
+                in0=v_banks[(q, u)][:].rearrange("p t c -> p c t"),
+                in1=vo_sb[q][:, :, 2 * u : 2 * u + 2, :].rearrange("p h t d -> p h d t"),
+                op=SUB,
+            )
+
+        def stage_dv(o, a, e, gate=None):
+            tile = staging(DH * (e - a), gate)
+            for h in range(a, e):
+                dv_staging[(o, h)] = (tile, a)
+
+        def staged_dv(o, a, e):
+            tile, base = dv_staging[(o, a)]
+            return tile[:, DH * (a - base) : DH * (e - base), :]
+
+        def times_beta(o, a, e, engine=VECTOR):
+            b, h0 = batch_and_head(o)
+            row = H * b + h0
+            table = factors["beta"] if engine == VECTOR else beta_sb
+            product = nc.vector.tensor_tensor if engine == VECTOR else nc.gpsimd.tensor_tensor
+            product(
+                out=staged_dv(o, a, e),
+                in0=diff[o][:, :, DH * a : DH * e, :].rearrange("p u c t -> p c u t"),
+                in1=table[:, row + a : row + e, :].unsqueeze(2).to_broadcast([P, e - a, DH, PACK]),
                 op=MULT,
             )
 
@@ -397,65 +365,19 @@ def tile_dpfpattention_pb_kernel(tc, x, wv, beta, vo, k_bytes, k_scale, W, out):
             nc.vector.quantize_mx(
                 out=dv_codes[:, cols].bitcast(FP8X4),
                 scales=dv_exps[:, cols],
-                in_=dv_staging[o][:, DH * a : DH * e, :].rearrange("p n t -> p (n t)"),
+                in_=staged_dv(o, a, e).rearrange("p n t -> p (n t)"),
             )
-
-        beta_sb = keep.tile([P, B * H, PACK], F32, name="beta_sb")
-        beta_turned = []
-
-        def turn_beta():
-            bank = ps_beta.tile([P, PACK, P], BF16, name="beta_bank")
-            beta_turned.append(bank)
-            for t in range(PACK):
-                nc.tensor.transpose(bank[:, t, :], beta_rows[:, t::PACK], ident_bf16[:])
-
-        def fetch_beta(engine):
-            copy = nc.vector.tensor_copy if engine == VECTOR else nc.scalar.copy
-            copy(out=beta_sb[:], in_=beta_turned[0][:, :, 0 : B * H].rearrange("p t h -> p h t"))
-
-        def times_beta_on_gpsimd(o):
-            n = ON_GPSIMD[o]
-            row = H * (o % 2) + 8 * (o // 2)
-            nc.gpsimd.tensor_tensor(
-                out=dv_staging[o][:, 0 : DH * n, :].rearrange("p (c i) t -> p c i t", i=2),
-                in0=paired[o][:].rearrange("p h c t i -> p (h c) i t"),
-                in1=beta_sb[:, row : row + n, :].unsqueeze(2).to_broadcast([P, n, DH, PACK]),
-                op=MULT,
-            )
-
-        dv_planar = {}
-
-        def times_beta_on_scalar(o, h):
-            n = ON_SCALAR[o]
-            if o not in dv_planar:
-                dv_planar[o] = keep.tile([P, PACK, n * DH], BF16, name="dv_planar%d" % o)
-            row = H * (o % 2) + 8 * (o // 2) + h
-            for t in range(PACK):
-                nc.scalar.activation(
-                    out=dv_planar[o][:, t, DH * (h - 8 + n) : DH * (h - 7 + n)],
-                    in_=diff[o][:, 1, t, DH * (h - 4) : DH * (h - 3)],
-                    func=COPY,
-                    scale=beta_sb[:, row, t : t + 1],
-                )
-
-        def interleave_dv(o):
-            interleave(SCALAR, dv_staging[o][:, DH * (8 - ON_SCALAR[o]) :, :], dv_planar[o][:])
 
 
         out_banks = {}
 
-        def out_bank(pool, name, parts):
-            bank = pool.tile([P, 8, DH], F32, name=name)
-            at = 0
-            for q, a, e in parts:
-                out_banks[(q, a)] = bank[:, at:, :]
-                at += e - a
-
-        def second_product(q, a=0, e=4):
+        def second_product(o, a, e, pool, name):
+            bank = pool.tile([P, e - a, DH], F32, name=name)
+            out_banks[(o, a)] = bank
             for h in range(a, e):
-                head = 4 * q + h
+                head = 8 * o + h
                 nc.tensor.matmul_mx(
-                    out=out_banks[(q, a)][:, h - a, :],
+                    out=bank[:, h - a, :],
                     lhsT=k_codes[:, S * head : S * (head + 1)].bitcast(FP8X4),
                     lhsT_scale=k_exps[:, S * head : S * (head + 1)],
                     rhs=dv_codes[:, DH * head : DH * (head + 1)].bitcast(FP8X4),
@@ -464,231 +386,212 @@ def tile_dpfpattention_pb_kernel(tc, x, wv, beta, vo, k_bytes, k_scale, W, out):
                     stop=True,
                 )
 
-        def add_memory_and_store(q, a=0, e=4):
-            o, h0 = q // 2, 4 * (q % 2)
-            heads = slice(h0 + a, h0 + e)
-            nc.vector.tensor_tensor(
-                out=out_sb[o][:, heads, :], in0=out_banks[(q, a)][:, 0 : e - a, :], in1=mem_sb[o][:, heads, :], op=ADD
-            )
-            b, first = o % 2, 8 * (o // 2) + h0
-            nc.sync.dma_start(
-                out=out[b, first + a : first + e].rearrange("h s d -> s h d"), in_=out_sb[o][:, heads, :]
-            )
+        def add_memory_and_store(o, a, e):
+            result = work.tile([P, e - a, DH], F32, name="result%d" % (e - a), bufs=2)
+            nc.vector.tensor_tensor(out=result[:], in0=out_banks[(o, a)][:], in1=mem_sb[o][:, a:e, :], op=ADD)
+            b, first = batch_and_head(o)
+            nc.sync.dma_start(out=out[b, first + a : first + e].rearrange("h s d -> s h d"), in_=result[:])
 
 
         make_constants()
-
         load_k_scales()
-        load_first_k_pair(0)
-        load_first_k_pair(2)
+        load_k(0, 0, 2)
+        load_k(0, 2, 4)
         load_k(1)
         load_beta()
         load_k(2)
+        load_wv(0, 0, 4)
         load_x(0, 0)
-        load_wv(0, 0)
         load_x(0, 1)
-        load_wv(0, 1)
-        load_wv(1, 0)
+        load_wv(1, 0, 4)
         load_vo(0)
-        load_wv(1, 1)
         load_k(3)
-        load_x(1, 0)
         load_vo(1)
-        load_x(1, 1)
-        load_wv(2, 0)
-        load_k(4)
+        load_x(1, 0)
         load_vo(2)
-        load_wv(2, 1)
+        load_k(4)
         load_vo(3)
+        load_x(1, 1)
         load_k(5)
         load_vo(4)
         load_vo(5)
         load_k(6)
         load_memory(0)
+        load_k(7)
         load_vo(6)
         load_vo(7)
-        load_k(7)
         for o in range(1, OCTETS):
             load_memory(o)
 
-        for first in (0, 2):
-            widen_k((first, 2), VECTOR, 0, 1)
-            widen_k((first, 2), SCALAR, 1, 2)
+        place_scales()
+        place_beta()
+        widen_k((0, 3), VECTOR)
         stage_k(0, 4)
-        interleave_k((0, 2), VECTOR)
-        widen_k((4, 2), SCALAR)
-        interleave_k((2, 2), VECTOR)
-        widen_k((6, 2), VECTOR)
         stage_k(4, 4)
-        interleave_k((4, 2), VECTOR)
-        widen_k((8, 2), SCALAR)
-        turn_beta()
-        fetch_beta(SCALAR)
-        for g in range(2):
-            turn_x(0, 0, g)
-        for g in range(2):
-            fetch_x(0, 0, g)
-        quantise_k(0, 4)
-        interleave_k((6, 2), VECTOR)
-        stage_wv(0, 2)
-        interleave_wv(0, VECTOR)
-        quantise_k(4, 4)
-        quantise_x(0, 0)
-        widen_k((10, 2), SCALAR)
-        for g in range(2):
-            turn_x(0, 1, g)
-        fetch_x(0, 1, 0, gate="a")
-        fetch_x(0, 1, 1)
-        interleave_wv(1, VECTOR)
         stage_k(8, 4)
-        interleave_k((8, 2), VECTOR)
-        quantise_wv(0, 2)
-        spread_beta(0)
-        first_product(0, 0)
-        interleave_k((10, 2), VECTOR)
-        quantise_x(0, 1)
-        first_product(0, 1)
-        quantise_k(8, 4)
-
-        stage_wv(3, 1)
-        interleave_wv_half(2, 0, GPSIMD, gate="a")
-        interleave_wv_half(2, 1, SCALAR)
-        interleave_wv(3, SCALAR)
-        widen_k((12, 3), SCALAR)
-        widen_k((15, 1), SCALAR)
-        for g in range(2):
-            turn_x(1, 0, g)
-        for g in range(2):
-            fetch_x(1, 0, g)
+        cast_k(3, 1)
+        interleave_k((0, 3), GPSIMD)
+        scale_k(3, 1)
+        cast_k(4, 1)
+        cast_k(5, 1)
+        cast_k(6, 2)
+        scale_k(4, 4)
+        cast_k(8, 2)
+        cast_k(10, 2)
+        fetch_beta()
+        stage_wv(0, 0, 2)
+        stage_wv(0, 2)
+        interleave_wv(0, 0, GPSIMD)
+        interleave_wv(0, 1, SCALAR)
+        interleave_wv(0, 2, SCALAR)
+        scale_k(8, 4)
         for u in range(2):
-            subtract_vo(0, u)
-        quantise_wv_half(2, 1)
-        quantise_wv_half(2, 0)
-        quantise_wv(3, 1)
+            for g in range(2):
+                turn_x(0, u, g, ps_v, "v_bank")
+        turn_wv(0, 3)
+        for u in range(2):
+            for g in range(2):
+                fetch_x(0, u, g)
+        quantise_k(0, 4)
+        quantise_k(4, 4)
+        quantise_k(8, 4)
+        quantise_wv(0, 0, 2)
+        stage_wv(1, 0)
+        stage_wv(1, 1, gate="a")
+        interleave_wv(1, 1, SCALAR)
+        quantise_x(0, 0)
+        interleave_wv(1, 0, VECTOR)
+        quantise_x(0, 1)
+        quantise_wv(1, 0)
+        for u in range(2):
+            first_product(0, u)
+        quantise_wv(1, 1)
         for u in range(2):
             first_product(1, u)
+        quantise_wv(0, 2)
 
-        stage_k(12, 4, gate="a")
-        interleave_k((12, 3), GPSIMD)
-        interleave_k((15, 1), SCALAR)
-        for g in range(2):
-            turn_x(1, 1, g)
-        fetch_x(1, 1, 0, gate="b")
-        fetch_x(1, 1, 1)
-        stage_dv(0)
-        times_beta(0, 0, 4)
+        stage_wv(1, 2, gate="a")
+        interleave_wv(1, 2, GPSIMD)
+        cast_k(12, 1)
+        stage_wv(0, 3)
+        fetch_wv(0, 3)
+        stage_wv(1, 3)
+        interleave_wv(1, 3, SCALAR)
+        widen_k((13, 3), SCALAR)
+        turn_x(1, 0, 0)
+        stage_k(12, 4)
+        scale_k(12, 1)
+        for u in range(2):
+            subtract_vo(0, u)
+        quantise_wv(1, 2)
+        for u in range(2):
+            first_product(2, u)
+        turn_x(1, 0, 1)
+        quantise_wv(0, 3)
+        quantise_wv(1, 3)
+
+
+        stage_dv(0, 0, 8, gate="a")
+        times_beta(0, 0, 4, GPSIMD)
+        widen_k((16, 2), SCALAR, 0, 1)
+        fetch_x(1, 0, 0)
+        interleave_k((13, 3), SCALAR, 0, 2)
+        fetch_x(1, 0, 1)
+        widen_k((16, 2), SCALAR, 1, 2)
+        interleave_k((13, 3), SCALAR, 2, 3)
         for u in range(2):
             subtract_vo(1, u)
+        for u in range(2):
+            first_product(3, u)
+        for u in range(2):
+            subtract_vo(2, u)
+        stage_dv(1, 0, 8, gate="b")
+        times_beta(1, 0, 2, GPSIMD)
+        for g in range(2):
+            turn_x(1, 1, g)
+        stage_k(16, 4)
+        turn_k((16, 2), 0, 2, ps_v, "v_bank")
+        times_beta(0, 4, 8)
+        for u in range(2):
+            subtract_vo(3, u)
+        fetch_x(1, 1, 0, gate="c")
+        fetch_x(1, 1, 1)
+        widen_k((18, 2), SCALAR)
+        fetch_k(16)
         quantise_x(1, 0)
-        for q in (2, 3):
-            first_product(q, 0)
+        first_product(4, 0)
+        first_product(5, 0)
         quantise_k(12, 4)
         quantise_x(1, 1)
-        for q in (2, 3):
-            first_product(q, 1)
-        quantise_dv(0, 0, 4)
+        turn_k((18, 2))
+        first_product(4, 1)
+        first_product(5, 1)
+        quantise_dv(0, 0, 8)
+        second_product(0, 0, 8, ps_out, "out_bank")
 
-        interleave_wv_pass_on_gpsimd("b")
-        stage_wv(5, 1)
-        stage_wv(7, 1)
-        widen_k((16, 2), SCALAR)
-        widen_k((18, 2), SCALAR, 0, 1)
-        interleave_wv(5, SCALAR)
-        interleave_wv(7, SCALAR)
-        widen_k((18, 2), SCALAR, 1, 2)
-        times_beta(0, 4, 8)
-        spread_beta(1, 5)
-        for q in (2, 3):
-            for u in range(2):
-                subtract_vo(q, u)
-        interleave_k_on_tensor((16, 2))
-        quantise_wv(4, 1)
-        quantise_wv(5, 1)
-        for u in range(2):
-            first_product(4, u)
-        quantise_wv(7, 1)
-        quantise_wv(6, 1)
-        for u in range(2):
-            first_product(5, u)
-        quantise_dv(0, 4, 8)
-        out_bank(ps_out, "out_bank", [(0, 0, 4), (1, 0, 4)])
-        for q in (0, 1):
-            second_product(q)
-
-        stage_dv(1, gate="b")
-        times_beta_on_gpsimd(1)
-        stage_k(16, 4)
+        stage_dv(1, 2, 6, gate="c")
+        times_beta(1, 2, 6, GPSIMD)
         widen_k((20, 2), SCALAR)
-        interleave_k((18, 2), SCALAR)
-        fetch_k((16, 2))
+        turn_k((20, 2))
+        fetch_k(18)
         widen_k((22, 2), SCALAR)
-        widen_k((24, 2), SCALAR)
-        times_beta(1, 5, 8)
-        spread_beta(2, 5)
-        for q in (4, 5):
-            for u in range(2):
+        stage_k(20, 4)
+        interleave_k((22, 2), SCALAR, 0, 1)
+        fetch_k(20)
+        interleave_k((22, 2), SCALAR, 1, 2)
+        times_beta(1, 6, 8)
+        for u in range(2):
+            for q in (4, 5):
                 subtract_vo(q, u)
         for q in (6, 7):
             for u in range(2):
                 first_product(q, u)
-        interleave_k_on_tensor((20, 2))
+        widen_k((24, 2), SCALAR)
         add_memory_and_store(0, 0, 8)
-        quantise_k(18, 2)
-        quantise_dv(1, 0, 8)
-        quantise_k(16, 2)
-        out_bank(ps_out, "out_bank", [(2, 0, 4), (3, 0, 4)])
-        for q in (2, 3):
-            second_product(q)
-        interleave_k_on_tensor((24, 2))
+        quantise_dv(1, 0, 2)
+        quantise_dv(1, 6, 8)
+        quantise_dv(1, 2, 6)
+        second_product(1, 0, 8, ps_out, "out_bank")
+        turn_k((24, 2))
+        quantise_k(16, 4)
 
-        stage_dv(2, gate="b")
-        times_beta_on_gpsimd(2)
-        times_beta(2, 5, 8)
-        spread_beta(3, 2)
+        stage_dv(2, 0, 8, gate="c")
+        times_beta(2, 0, 5, GPSIMD)
         widen_k((26, 2), SCALAR)
-        stage_k(20, 4)
-        interleave_k((22, 2), SCALAR)
-        fetch_k((20, 2))
-        interleave_k_on_tensor((26, 2))
-        widen_k((28, 2), SCALAR)
-        widen_k((30, 2), SCALAR)
+        turn_k((26, 2))
+        times_beta(2, 5, 8)
         stage_k(24, 4)
-        fetch_k((24, 2))
+        fetch_k(24)
+        widen_k((28, 2), SCALAR)
+        turn_k((28, 2))
+        fetch_k(26)
+        cast_k(30, 1)
+        stage_k(28, 4)
+        widen_k((31, 1), SCALAR)
+        fetch_k(28)
+        interleave_k((31, 1), SCALAR)
         for q in (6, 7):
             for u in range(2):
                 subtract_vo(q, u)
-        add_memory_and_store(2, 0, 8)
-        quantise_k(20, 2)
+        add_memory_and_store(1, 0, 8)
         quantise_dv(2, 0, 8)
-        quantise_k(22, 2)
-        out_bank(ps_out, "out_bank", [(4, 0, 4), (5, 0, 4)])
-        for q in (4, 5):
-            second_product(q)
-        interleave_k_on_tensor((28, 2), 1)
-        stage_k(28, 4)
-        times_beta_on_scalar(3, 7)
-        fetch_k((26, 2))
+        quantise_k(20, 4)
+        second_product(2, 0, 8, ps_out, "out_bank")
 
-        stage_dv(3, gate="b")
-        times_beta_on_gpsimd(3)
-        interleave_k((30, 2), SCALAR)
-        interleave_dv(3)
-        interleave_k((28, 2), SCALAR, 1, 2)
-        fetch_k((28, 2), 1)
-        times_beta(3, 2, 4)
-        times_beta(3, 4, 7)
-        add_memory_and_store(4, 0, 8)
+        stage_dv(3, 0, 8, gate="c")
+        times_beta(3, 0, 3, GPSIMD)
+        times_beta(3, 4, 8)
+        times_beta(3, 3, 4)
+        scale_k(30, 1, "late scale")
+        add_memory_and_store(2, 0, 8)
         quantise_k(24, 4)
         quantise_dv(3, 0, 4)
-        out_bank(ps_v, "v_bank", [(6, 0, 4)])
-        second_product(6)
-        quantise_k(30, 2)
-        quantise_dv(3, 4, 8)
-        out_bank(ps_v, "v_bank", [(7, 2, 4)])
-        second_product(7, 2, 4)
-        quantise_k(28, 2)
-        out_bank(ps_v, "v_bank", [(7, 0, 2)])
-        second_product(7, 0, 2)
-        add_memory_and_store(6)
-        add_memory_and_store(7, 2, 4)
-        add_memory_and_store(7, 0, 2)
+        second_product(3, 0, 4, ps_v, "v_bank")
+        quantise_k(28, 4)
+        quantise_dv(3, 4, 6)
+        second_product(3, 4, 6, ps_v, "v_bank")
+        quantise_dv(3, 6, 8)
+        second_product(3, 6, 8, ps_v, "v_bank")
+        add_memory_and_store(3, 0, 4)
+        add_memory_and_store(3, 4, 6)
+        add_memory_and_store(3, 6, 8)

@@ -25,9 +25,11 @@ OCTETS = B * H // 8
 QW = 4 * DH
 RUN = {"vector": 4, "scalar": 2}
 SCALE_RUN = 2
-STAGES = {256: 5, 512: 6}
-PLANARS = {1: 2, 2: 4, 3: 1}
+STAGES = {128: 1, 256: 5, 512: 6}
+PLANARS = {1: 2, 2: 6, 3: 1}
+WIDES = {1: 1, 2: 3, 3: 1}
 OCTET_ORDER = ((0, 0), (0, 8), (1, 0), (1, 8))
+JOINT = (0, 2, 4, 6)
 VECTOR, SCALAR, GPSIMD = "vector", "scalar", "gpsimd"
 
 
@@ -73,7 +75,7 @@ def tile_dpfpattention_pb_kernel(tc, x, wv, beta, vo, k_bytes, k_scale, W, out):
         vo_sb = [keep.tile([P, 4, PACK, DH], BF16, name="vo_sb%d" % q) for q in range(QUADS)]
         mem_sb = [keep.tile([P, 8, DH], BF16, name="mem_sb%d" % o) for o in range(OCTETS)]
         x_sb = [[keep.tile([P, 2, D], BF16, name="x_sb%d%d" % (b, u)) for u in range(2)] for b in range(B)]
-        wv_sb = {}
+        wv_sb = [keep.tile([P, PACK, D], BF16, name="wv_sb%d" % g) for g in range(2)]
 
 
         def load_k_scales():
@@ -100,14 +102,8 @@ def tile_dpfpattention_pb_kernel(tc, x, wv, beta, vo, k_bytes, k_scale, W, out):
                 out=x_sb[b][u][:], in_=x[b].rearrange("(m t) k -> m t k", t=PACK)[:, 2 * u : 2 * u + 2, :]
             )
 
-        def load_wv(g, c, n):
-            tile = keep.tile([P, PACK, n * QW], BF16, name="wv_sb%d_%d" % (g, c))
-            for j in range(n):
-                wv_sb[(g, c + j)] = tile[:, :, QW * j : QW * (j + 1)]
-            wv_sb[(g, c, n)] = tile
-            nc.sync.dma_start(
-                out=tile[:], in_=wv.rearrange("(g p t) w -> g p t w", g=2, t=PACK)[g][:, :, QW * c : QW * (c + n)]
-            )
+        def load_wv(g):
+            nc.sync.dma_start(out=wv_sb[g][:], in_=wv.rearrange("(g p t) w -> g p t w", g=2, t=PACK)[g])
 
         def load_memory(o):
             b, h0 = batch_and_head(o)
@@ -129,11 +125,8 @@ def tile_dpfpattention_pb_kernel(tc, x, wv, beta, vo, k_bytes, k_scale, W, out):
             nc.tensor.matmul(bank[:], lhsT=ident_f32[:], rhs=k_scales[:], start=True, stop=True)
 
         def place_beta():
-            both = ps_beta.tile([P, B * H + 1, PACK], F32, name="beta_bank")
-            bank = both[:, 0 : B * H, :]
+            bank = ps_beta.tile([P, B * H, PACK], F32, name="beta_bank")
             factors["beta"] = bank
-            factors["late scale"] = both[:, B * H, :]
-            nc.tensor.matmul(both[:, B * H, :], lhsT=ident_f32[:], rhs=k_scales[:], start=True, stop=True)
             for t in range(PACK):
                 nc.tensor.matmul(
                     bank[:, :, t], lhsT=beta_rows[:, t::PACK], rhs=ident_bf16[:, 0 : B * H], start=True, stop=True
@@ -151,23 +144,23 @@ def tile_dpfpattention_pb_kernel(tc, x, wv, beta, vo, k_bytes, k_scale, W, out):
         def interleave(engine, dst, src):
             if engine == GPSIMD:
                 nc.gpsimd.tensor_scalar(
-                    out=dst, in0=src.rearrange("p t n -> p n t"), scalar1=1.0, scalar2=0.0, op0=MULT, op1=ADD
+                    out=dst, in0=src.rearrange("p h t n -> p h n t"), scalar1=1.0, scalar2=0.0, op0=MULT, op1=ADD
                 )
                 return
             copy = nc.vector.tensor_copy if engine == VECTOR else nc.scalar.copy
             copy(
                 out=dst.rearrange("p (c i) t -> p c t i", i=RUN[engine]),
-                in_=src.rearrange("p t (c i) -> p c t i", i=RUN[engine]),
+                in_=src.rearrange("p h t (c i) -> p h c t i", i=RUN[engine]),
             )
 
         def turn(src, pool=ps_turn, name="turned"):
-            n = src.shape[2]
-            bank = pool.tile([P, n, PACK], BF16, name=name)
-            for a in range(0, n, P):
+            n = src.shape[1]
+            bank = pool.tile([P, n * P, PACK], BF16, name=name)
+            for a in range(n):
                 nc.tensor.matmul(
-                    bank[:, a : a + P, :].rearrange("p s t -> p t s"),
+                    bank[:, P * a : P * (a + 1), :].rearrange("p s t -> p t s"),
                     lhsT=ident_bf16[:],
-                    rhs=src[:, :, a : a + P],
+                    rhs=src[:, a],
                     start=True,
                     stop=True,
                 )
@@ -180,7 +173,7 @@ def tile_dpfpattention_pb_kernel(tc, x, wv, beta, vo, k_bytes, k_scale, W, out):
         k_banks = {}
 
         def cast_k(first, n):
-            tile = work.tile([P, n, PACK, S], BF16, name="k_wide%d" % n, bufs=3)
+            tile = work.tile([P, n, PACK, S], BF16, name="k_wide%d" % n, bufs=WIDES[n])
             for h in range(n):
                 k_wide[first + h] = tile[:, h]
             nc.scalar.copy(
@@ -200,11 +193,11 @@ def tile_dpfpattention_pb_kernel(tc, x, wv, beta, vo, k_bytes, k_scale, W, out):
         def widen_k(group, engine, a=0, e=None):
             first, n = group
             if first not in k_planar:
-                k_planar[first] = work.tile([P, PACK, n, S], BF16, name="k_planar%d" % n, bufs=PLANARS[n])
+                k_planar[first] = work.tile([P, n, PACK, S], BF16, name="k_planar%d" % n, bufs=PLANARS[n])
             for h in range(a, n if e is None else e):
                 for t in range(PACK):
                     codes = k_raw[(first + h) // 4][:, (first + h) % 4, S * t : S * (t + 1)].bitcast(FP8)
-                    dst = k_planar[first][:, t, h, :]
+                    dst = k_planar[first][:, h, t, :]
                     if engine == VECTOR:
                         nc.vector.tensor_scalar(
                             out=dst, in0=codes, scalar1=k_scales[:, t : t + 1], scalar2=None, op0=MULT
@@ -223,11 +216,11 @@ def tile_dpfpattention_pb_kernel(tc, x, wv, beta, vo, k_bytes, k_scale, W, out):
 
         def planar_k(group, a, e):
             first, n = group
-            return k_planar[first][:, :, a : n if e is None else e, :].rearrange("p t h s -> p t (h s)")
+            return k_planar[first][:, a : n if e is None else e]
 
         def interleave_k(group, engine, a=0, e=None):
             src = planar_k(group, a, e)
-            interleave(engine, staged_k(group[0] + a, src.shape[2] // S), src)
+            interleave(engine, staged_k(group[0] + a, src.shape[1]), src)
 
         def turn_k(group, a=0, e=None, *bank):
             k_banks[group[0] + a] = turn(planar_k(group, a, e), *bank)
@@ -278,62 +271,63 @@ def tile_dpfpattention_pb_kernel(tc, x, wv, beta, vo, k_bytes, k_scale, W, out):
         w_staging = {}
         w_banks = {}
 
-        def stage_wv(g, c, n=1, gate=None):
-            tile = staging(n * QW, gate)
-            for j in range(n):
-                w_staging[(g, c + j)] = (tile, c)
+        def stage_wv(g, a, e, gate=None):
+            tile = staging(e - a, gate)
+            for column in range(a, e, DH):
+                w_staging[(g, column)] = (tile, a)
 
-        def staged_wv(g, c, n):
-            tile, base = w_staging[(g, c)]
-            return tile[:, QW * (c - base) : QW * (c - base + n), :]
+        def staged_wv(g, a, e):
+            tile, base = w_staging[(g, a)]
+            return tile[:, a - base : e - base, :]
 
-        def interleave_wv(g, c, engine, n=1, a=0, e=None):
-            src = wv_sb[(g, c)] if n == 1 else wv_sb[(g, c, n)][:]
-            e = n * QW if e is None else e
-            interleave(engine, staged_wv(g, c, n)[:, a:e, :], src[:, :, a:e])
+        def interleave_wv(g, a, e, engine):
+            interleave(engine, staged_wv(g, a, e), wv_sb[g][:, :, a:e].unsqueeze(1))
 
-        def turn_wv(g, c, *bank):
-            w_banks[(g, c)] = turn(wv_sb[(g, c)], *bank)
+        def turn_wv(g, a, e):
+            w_banks[(g, a)] = turn(wv_sb[g][:, :, a:e].rearrange("p t (j n) -> p j t n", n=P))
 
-        def fetch_wv(g, c):
-            nc.scalar.copy(out=staged_wv(g, c, 1), in_=w_banks[(g, c)][:])
+        def fetch_wv(g, a, e):
+            nc.scalar.copy(out=staged_wv(g, a, e), in_=w_banks[(g, a)][:])
 
-        def quantise_wv(g, c, n=1):
-            cols = slice(QW * c, QW * (c + n))
+        def quantise_wv(g, a, e):
             nc.vector.quantize_mx(
-                out=w_codes[:, g, cols].bitcast(FP8X4),
-                scales=w_exps[:, g, cols],
-                in_=staged_wv(g, c, n).rearrange("p n t -> p (n t)"),
+                out=w_codes[:, g, a:e].bitcast(FP8X4),
+                scales=w_exps[:, g, a:e],
+                in_=staged_wv(g, a, e).rearrange("p n t -> p (n t)"),
             )
 
 
         v_banks = {}
 
-        def first_product(q, u):
+        def first_product(q, u, passes=(0, 1)):
             b, c = batch_and_chunk(q)
-            bank = ps_v.tile([P, 2, QW], F32, name="v_bank")
-            v_banks[(q, u)] = bank
-            for tt in range(2):
-                for g in range(2):
+            if (q, u) not in v_banks:
+                v_banks[(q, u)] = ps_v.tile([P, 2, QW], F32, name="v_bank")
+            bank = v_banks[(q, u)]
+            for g in passes:
+                for tt in range(2):
                     nc.tensor.matmul_mx(
                         out=bank[:, tt, :],
                         lhsT=x_codes[b][u][:, g, P * tt : P * (tt + 1)].bitcast(FP8X4),
                         lhsT_scale=x_exps[b][u][:, g, P * tt : P * (tt + 1)],
                         rhs=w_codes[:, g, QW * c : QW * (c + 1)].bitcast(FP8X4),
                         rhs_scale=w_exps[:, g, QW * c : QW * (c + 1)],
-                        start=(g == 0),
-                        stop=(g == 1),
+                        start=(g == 0 and tt == 0),
+                        stop=(g == 1 and tt == 1),
                     )
 
         diff = {}
         dv_staging = {}
 
         def subtract_vo(q, u):
-            o = q // 2
-            if o not in diff:
-                diff[o] = work.tile([P, 2, 2 * QW, 2], F32, name="diff", bufs=2)
+            if q not in diff:
+                n = 2 if q in JOINT else 1
+                tile = work.tile([P, 2, n * QW, 2], F32, name="diff%d" % n, bufs=4 // n)
+                for j in range(n):
+                    diff[q + j] = (tile, q)
+            tile, base = diff[q]
             nc.vector.tensor_tensor(
-                out=diff[o][:, u, QW * (q % 2) : QW * (q % 2 + 1), :],
+                out=tile[:, u, QW * (q - base) : QW * (q - base + 1), :],
                 in0=v_banks[(q, u)][:].rearrange("p t c -> p c t"),
                 in1=vo_sb[q][:, :, 2 * u : 2 * u + 2, :].rearrange("p h t d -> p h d t"),
                 op=SUB,
@@ -353,9 +347,11 @@ def tile_dpfpattention_pb_kernel(tc, x, wv, beta, vo, k_bytes, k_scale, W, out):
             row = H * b + h0
             table = factors["beta"] if engine == VECTOR else beta_sb
             product = nc.vector.tensor_tensor if engine == VECTOR else nc.gpsimd.tensor_tensor
+            tile, base = diff[2 * o + a // 4]
+            at = DH * (8 * o + a - 4 * base)
             product(
                 out=staged_dv(o, a, e),
-                in0=diff[o][:, :, DH * a : DH * e, :].rearrange("p u c t -> p c u t"),
+                in0=tile[:, :, at : at + DH * (e - a), :].rearrange("p u c t -> p c u t"),
                 in1=table[:, row + a : row + e, :].unsqueeze(2).to_broadcast([P, e - a, DH, PACK]),
                 op=MULT,
             )
@@ -397,21 +393,22 @@ def tile_dpfpattention_pb_kernel(tc, x, wv, beta, vo, k_bytes, k_scale, W, out):
         load_k_scales()
         load_k(0, 0, 2)
         load_k(0, 2, 4)
-        load_k(1)
+        load_k(1, 0, 2)
+        load_k(1, 2, 4)
         load_beta()
         load_k(2)
-        load_wv(0, 0, 4)
         load_x(0, 0)
         load_x(0, 1)
-        load_wv(1, 0, 4)
+        load_wv(0)
+        load_wv(1)
         load_vo(0)
-        load_k(3)
-        load_vo(1)
         load_x(1, 0)
-        load_vo(2)
-        load_k(4)
-        load_vo(3)
+        load_vo(1)
+        load_k(3)
         load_x(1, 1)
+        load_k(4)
+        load_vo(2)
+        load_vo(3)
         load_k(5)
         load_vo(4)
         load_vo(5)
@@ -432,157 +429,152 @@ def tile_dpfpattention_pb_kernel(tc, x, wv, beta, vo, k_bytes, k_scale, W, out):
         cast_k(3, 1)
         interleave_k((0, 3), GPSIMD)
         scale_k(3, 1)
-        cast_k(4, 1)
-        cast_k(5, 1)
+        cast_k(4, 2)
         cast_k(6, 2)
+        widen_k((8, 1), SCALAR)
+        interleave_k((8, 1), GPSIMD)
         scale_k(4, 4)
-        cast_k(8, 2)
-        cast_k(10, 2)
-        fetch_beta()
-        stage_wv(0, 0, 2)
-        stage_wv(0, 2)
-        interleave_wv(0, 0, GPSIMD)
-        interleave_wv(0, 1, SCALAR)
-        interleave_wv(0, 2, SCALAR)
-        scale_k(8, 4)
+        cast_k(9, 2)
+        widen_k((11, 1), SCALAR)
+        interleave_k((11, 1), SCALAR)
+        scale_k(9, 2)
         for u in range(2):
             for g in range(2):
                 turn_x(0, u, g, ps_v, "v_bank")
-        turn_wv(0, 3)
         for u in range(2):
             for g in range(2):
                 fetch_x(0, u, g)
+        turn_wv(0, 768, 1024)
+        stage_wv(0, 0, 512)
+        stage_wv(0, 512, 768)
+        interleave_wv(0, 384, 512, SCALAR)
+        interleave_wv(0, 512, 768, SCALAR)
         quantise_k(0, 4)
         quantise_k(4, 4)
-        quantise_k(8, 4)
-        quantise_wv(0, 0, 2)
-        stage_wv(1, 0)
-        stage_wv(1, 1, gate="a")
-        interleave_wv(1, 1, SCALAR)
         quantise_x(0, 0)
-        interleave_wv(1, 0, VECTOR)
+        interleave_wv(0, 0, 384, VECTOR)
         quantise_x(0, 1)
-        quantise_wv(1, 0)
+        quantise_wv(0, 0, 512)
+        for q in (0, 1):
+            for u in range(2):
+                first_product(q, u, (0,))
+        stage_wv(1, 0, 256)
+        stage_wv(1, 256, 512, gate="b")
+        interleave_wv(1, 256, 512, SCALAR)
+        stage_wv(0, 768, 1024, gate="d")
+        fetch_wv(0, 768, 1024)
+        interleave_wv(1, 0, 256, VECTOR)
+        quantise_wv(0, 512, 768)
+        quantise_wv(1, 0, 256)
         for u in range(2):
-            first_product(0, u)
-        quantise_wv(1, 1)
-        for u in range(2):
-            first_product(1, u)
-        quantise_wv(0, 2)
-
-        stage_wv(1, 2, gate="a")
-        interleave_wv(1, 2, GPSIMD)
-        cast_k(12, 1)
-        stage_wv(0, 3)
-        fetch_wv(0, 3)
-        stage_wv(1, 3)
-        interleave_wv(1, 3, SCALAR)
-        widen_k((13, 3), SCALAR)
+            first_product(0, u, (1,))
+        quantise_wv(1, 256, 512)
         turn_x(1, 0, 0)
-        stage_k(12, 4)
-        scale_k(12, 1)
         for u in range(2):
-            subtract_vo(0, u)
-        quantise_wv(1, 2)
-        for u in range(2):
-            first_product(2, u)
+            first_product(1, u, (1,))
         turn_x(1, 0, 1)
-        quantise_wv(0, 3)
-        quantise_wv(1, 3)
+        quantise_k(8, 4)
 
-
-        stage_dv(0, 0, 8, gate="a")
-        times_beta(0, 0, 4, GPSIMD)
-        widen_k((16, 2), SCALAR, 0, 1)
-        fetch_x(1, 0, 0)
-        interleave_k((13, 3), SCALAR, 0, 2)
-        fetch_x(1, 0, 1)
-        widen_k((16, 2), SCALAR, 1, 2)
-        interleave_k((13, 3), SCALAR, 2, 3)
+        stage_wv(1, 768, 1024, gate="b")
+        interleave_wv(1, 768, 1024, GPSIMD)
+        stage_wv(1, 512, 768)
+        interleave_wv(1, 512, 768, SCALAR)
+        fetch_beta()
+        cast_k(14, 2)
+        for q in (0, 1):
+            for u in range(2):
+                subtract_vo(q, u)
         for u in range(2):
-            subtract_vo(1, u)
+            first_product(2, u, (0,))
+        for g in range(2):
+            fetch_x(1, 0, g)
+        turn_x(1, 1, 0)
+        widen_k((12, 2), SCALAR)
+        fetch_x(1, 1, 0, gate="c")
+        quantise_wv(1, 512, 768)
+        for u in range(2):
+            first_product(2, u, (1,))
+        turn_x(1, 1, 1)
+        quantise_wv(0, 768, 1024)
+        quantise_wv(1, 768, 1024)
         for u in range(2):
             first_product(3, u)
-        for u in range(2):
-            subtract_vo(2, u)
-        stage_dv(1, 0, 8, gate="b")
-        times_beta(1, 0, 2, GPSIMD)
-        for g in range(2):
-            turn_x(1, 1, g)
-        stage_k(16, 4)
-        turn_k((16, 2), 0, 2, ps_v, "v_bank")
-        times_beta(0, 4, 8)
-        for u in range(2):
-            subtract_vo(3, u)
-        fetch_x(1, 1, 0, gate="c")
+
+        stage_dv(0, 0, 8, gate="d")
+        times_beta(0, 0, 6, GPSIMD)
+        turn_k((12, 2))
+        widen_k((16, 2), SCALAR, 0, 1)
         fetch_x(1, 1, 1)
+        widen_k((16, 2), SCALAR, 1, 2)
+        turn_k((16, 2))
         widen_k((18, 2), SCALAR)
+        stage_k(12, 4)
+        scale_k(14, 2)
+        times_beta(0, 6, 8)
+        for q in (2, 3):
+            for u in range(2):
+                subtract_vo(q, u)
+        widen_k((20, 2), SCALAR)
+        fetch_k(12)
+        stage_k(16, 4)
         fetch_k(16)
         quantise_x(1, 0)
         first_product(4, 0)
         first_product(5, 0)
-        quantise_k(12, 4)
         quantise_x(1, 1)
-        turn_k((18, 2))
         first_product(4, 1)
         first_product(5, 1)
         quantise_dv(0, 0, 8)
         second_product(0, 0, 8, ps_out, "out_bank")
+        turn_k((18, 2))
 
-        stage_dv(1, 2, 6, gate="c")
-        times_beta(1, 2, 6, GPSIMD)
-        widen_k((20, 2), SCALAR)
-        turn_k((20, 2))
-        fetch_k(18)
+        stage_dv(1, 0, 8, gate="c")
+        times_beta(1, 0, 5, GPSIMD)
+        times_beta(1, 5, 8)
         widen_k((22, 2), SCALAR)
         stage_k(20, 4)
-        interleave_k((22, 2), SCALAR, 0, 1)
-        fetch_k(20)
-        interleave_k((22, 2), SCALAR, 1, 2)
-        times_beta(1, 6, 8)
+        interleave_k((20, 2), SCALAR)
+        widen_k((24, 2), SCALAR)
+        fetch_k(18)
+        interleave_k((22, 2), SCALAR)
         for u in range(2):
             for q in (4, 5):
                 subtract_vo(q, u)
         for q in (6, 7):
             for u in range(2):
                 first_product(q, u)
-        widen_k((24, 2), SCALAR)
-        add_memory_and_store(0, 0, 8)
-        quantise_dv(1, 0, 2)
-        quantise_dv(1, 6, 8)
-        quantise_dv(1, 2, 6)
-        second_product(1, 0, 8, ps_out, "out_bank")
         turn_k((24, 2))
-        quantise_k(16, 4)
+        add_memory_and_store(0, 0, 8)
+        quantise_dv(1, 0, 8)
+        quantise_k(12, 4)
+        second_product(1, 0, 8, ps_out, "out_bank")
 
         stage_dv(2, 0, 8, gate="c")
         times_beta(2, 0, 5, GPSIMD)
-        widen_k((26, 2), SCALAR)
-        turn_k((26, 2))
         times_beta(2, 5, 8)
-        stage_k(24, 4)
-        fetch_k(24)
+        widen_k((26, 2), SCALAR)
         widen_k((28, 2), SCALAR)
-        turn_k((28, 2))
-        fetch_k(26)
-        cast_k(30, 1)
-        stage_k(28, 4)
-        widen_k((31, 1), SCALAR)
-        fetch_k(28)
-        interleave_k((31, 1), SCALAR)
         for q in (6, 7):
             for u in range(2):
                 subtract_vo(q, u)
+        turn_k((26, 2))
+        stage_k(24, 4)
+        fetch_k(24)
+        turn_k((28, 2), 0, 2, ps_v, "v_bank")
+        widen_k((30, 2), SCALAR)
+        fetch_k(26)
+        stage_k(28, 4)
+        interleave_k((30, 2), SCALAR)
+        fetch_k(28)
         add_memory_and_store(1, 0, 8)
-        quantise_dv(2, 0, 8)
         quantise_k(20, 4)
+        quantise_dv(2, 0, 8)
+        quantise_k(16, 4)
         second_product(2, 0, 8, ps_out, "out_bank")
-
         stage_dv(3, 0, 8, gate="c")
         times_beta(3, 0, 3, GPSIMD)
         times_beta(3, 4, 8)
         times_beta(3, 3, 4)
-        scale_k(30, 1, "late scale")
         add_memory_and_store(2, 0, 8)
         quantise_k(24, 4)
         quantise_dv(3, 0, 4)

@@ -25,9 +25,9 @@ OCTETS = B * H // 8
 QW = 4 * DH
 RUN = {"vector": 4, "scalar": 2}
 SCALE_RUN = 2
-STAGES = {128: 1, 256: 5, 512: 6}
+STAGES = {128: 1, 256: 6, 512: 7}
 PLANARS = {1: 2, 2: 6, 3: 1}
-WIDES = {1: 1, 2: 3, 3: 1}
+WIDES = {1: 3, 2: 3}
 OCTET_ORDER = ((0, 0), (0, 8), (1, 0), (1, 8))
 JOINT = (0, 2, 4, 6)
 VECTOR, SCALAR, GPSIMD = "vector", "scalar", "gpsimd"
@@ -125,8 +125,11 @@ def tile_dpfpattention_pb_kernel(tc, x, wv, beta, vo, k_bytes, k_scale, W, out):
             nc.tensor.matmul(bank[:], lhsT=ident_f32[:], rhs=k_scales[:], start=True, stop=True)
 
         def place_beta():
-            bank = ps_beta.tile([P, B * H, PACK], F32, name="beta_bank")
+            both = ps_beta.tile([P, B * H + 1, PACK], F32, name="beta_bank")
+            bank = both[:, 0 : B * H, :]
             factors["beta"] = bank
+            factors["late scale"] = both[:, B * H, :]
+            nc.tensor.matmul(both[:, B * H, :], lhsT=ident_f32[:], rhs=k_scales[:], start=True, stop=True)
             for t in range(PACK):
                 nc.tensor.matmul(
                     bank[:, :, t], lhsT=beta_rows[:, t::PACK], rhs=ident_bf16[:, 0 : B * H], start=True, stop=True
@@ -356,6 +359,23 @@ def tile_dpfpattention_pb_kernel(tc, x, wv, beta, vo, k_bytes, k_scale, W, out):
                 op=MULT,
             )
 
+        def times_beta_on_scalar(o, h):
+            b, h0 = batch_and_head(o)
+            tile, base = diff[2 * o + h // 4]
+            at = DH * (8 * o + h - 4 * base)
+            planar = work.tile([P, PACK, DH], BF16, name="dv_planar", bufs=2)
+            for t in range(PACK):
+                nc.scalar.activation(
+                    out=planar[:, t, :],
+                    in_=tile[:, t // 2, at : at + DH, t % 2],
+                    func=COPY,
+                    scale=beta_sb[:, H * b + h0 + h, t : t + 1],
+                )
+            return planar
+
+        def interleave_dv(o, h, planar):
+            interleave(SCALAR, staged_dv(o, h, h + 1), planar[:].unsqueeze(1))
+
         def quantise_dv(o, a, e):
             cols = slice(DH * (8 * o + a), DH * (8 * o + e))
             nc.vector.quantize_mx(
@@ -383,15 +403,16 @@ def tile_dpfpattention_pb_kernel(tc, x, wv, beta, vo, k_bytes, k_scale, W, out):
                 )
 
         def add_memory_and_store(o, a, e):
-            result = work.tile([P, e - a, DH], F32, name="result%d" % (e - a), bufs=2)
+            result = work.tile([P, e - a, DH], F32, name="result%d" % (e - a), bufs=4 if e - a == 2 else 2)
             nc.vector.tensor_tensor(out=result[:], in0=out_banks[(o, a)][:], in1=mem_sb[o][:, a:e, :], op=ADD)
             b, first = batch_and_head(o)
             nc.sync.dma_start(out=out[b, first + a : first + e].rearrange("h s d -> s h d"), in_=result[:])
 
 
-        make_constants()
+        load_k(0, 0, 1)
         load_k_scales()
-        load_k(0, 0, 2)
+        make_constants()
+        load_k(0, 1, 2)
         load_k(0, 2, 4)
         load_k(1, 0, 2)
         load_k(1, 2, 4)
@@ -402,9 +423,10 @@ def tile_dpfpattention_pb_kernel(tc, x, wv, beta, vo, k_bytes, k_scale, W, out):
         load_wv(0)
         load_wv(1)
         load_vo(0)
-        load_x(1, 0)
+        load_k(3, 0, 2)
         load_vo(1)
-        load_k(3)
+        load_x(1, 0)
+        load_k(3, 2, 4)
         load_x(1, 1)
         load_k(4)
         load_vo(2)
@@ -429,7 +451,8 @@ def tile_dpfpattention_pb_kernel(tc, x, wv, beta, vo, k_bytes, k_scale, W, out):
         cast_k(3, 1)
         interleave_k((0, 3), GPSIMD)
         scale_k(3, 1)
-        cast_k(4, 2)
+        cast_k(4, 1)
+        cast_k(5, 1)
         cast_k(6, 2)
         widen_k((8, 1), SCALAR)
         interleave_k((8, 1), GPSIMD)
@@ -461,7 +484,7 @@ def tile_dpfpattention_pb_kernel(tc, x, wv, beta, vo, k_bytes, k_scale, W, out):
         stage_wv(1, 0, 256)
         stage_wv(1, 256, 512, gate="b")
         interleave_wv(1, 256, 512, SCALAR)
-        stage_wv(0, 768, 1024, gate="d")
+        stage_wv(0, 768, 1024)
         fetch_wv(0, 768, 1024)
         interleave_wv(1, 0, 256, VECTOR)
         quantise_wv(0, 512, 768)
@@ -469,55 +492,52 @@ def tile_dpfpattention_pb_kernel(tc, x, wv, beta, vo, k_bytes, k_scale, W, out):
         for u in range(2):
             first_product(0, u, (1,))
         quantise_wv(1, 256, 512)
-        turn_x(1, 0, 0)
         for u in range(2):
             first_product(1, u, (1,))
-        turn_x(1, 0, 1)
+        for g in range(2):
+            turn_x(1, 0, g)
         quantise_k(8, 4)
 
         stage_wv(1, 768, 1024, gate="b")
         interleave_wv(1, 768, 1024, GPSIMD)
-        stage_wv(1, 512, 768)
+        stage_wv(1, 512, 768, gate="d")
         interleave_wv(1, 512, 768, SCALAR)
-        fetch_beta()
+        widen_k((12, 2), SCALAR)
         cast_k(14, 2)
+        fetch_beta()
+        for g in range(2):
+            fetch_x(1, 0, g)
         for q in (0, 1):
             for u in range(2):
                 subtract_vo(q, u)
         for u in range(2):
             first_product(2, u, (0,))
-        for g in range(2):
-            fetch_x(1, 0, g)
-        turn_x(1, 1, 0)
-        widen_k((12, 2), SCALAR)
-        fetch_x(1, 1, 0, gate="c")
         quantise_wv(1, 512, 768)
         for u in range(2):
             first_product(2, u, (1,))
-        turn_x(1, 1, 1)
         quantise_wv(0, 768, 1024)
         quantise_wv(1, 768, 1024)
         for u in range(2):
             first_product(3, u)
+        turn_x(1, 1, 0)
+        turn_x(1, 1, 1)
+        turn_k((12, 2), 0, 2, ps_out, "out_bank")
 
         stage_dv(0, 0, 8, gate="d")
         times_beta(0, 0, 6, GPSIMD)
-        turn_k((12, 2))
-        widen_k((16, 2), SCALAR, 0, 1)
-        fetch_x(1, 1, 1)
-        widen_k((16, 2), SCALAR, 1, 2)
-        turn_k((16, 2))
+        widen_k((16, 2), SCALAR)
         widen_k((18, 2), SCALAR)
+        fetch_x(1, 1, 0, gate="c")
+        fetch_x(1, 1, 1)
+        turn_k((16, 2))
         stage_k(12, 4)
-        scale_k(14, 2)
+        scale_k(14, 2, "late scale")
         times_beta(0, 6, 8)
         for q in (2, 3):
             for u in range(2):
                 subtract_vo(q, u)
         widen_k((20, 2), SCALAR)
         fetch_k(12)
-        stage_k(16, 4)
-        fetch_k(16)
         quantise_x(1, 0)
         first_product(4, 0)
         first_product(5, 0)
@@ -534,8 +554,9 @@ def tile_dpfpattention_pb_kernel(tc, x, wv, beta, vo, k_bytes, k_scale, W, out):
         widen_k((22, 2), SCALAR)
         stage_k(20, 4)
         interleave_k((20, 2), SCALAR)
+        stage_k(16, 4)
+        fetch_k(16)
         widen_k((24, 2), SCALAR)
-        fetch_k(18)
         interleave_k((22, 2), SCALAR)
         for u in range(2):
             for q in (4, 5):
@@ -543,24 +564,25 @@ def tile_dpfpattention_pb_kernel(tc, x, wv, beta, vo, k_bytes, k_scale, W, out):
         for q in (6, 7):
             for u in range(2):
                 first_product(q, u)
-        turn_k((24, 2))
         add_memory_and_store(0, 0, 8)
         quantise_dv(1, 0, 8)
         quantise_k(12, 4)
         second_product(1, 0, 8, ps_out, "out_bank")
+        turn_k((24, 2))
 
         stage_dv(2, 0, 8, gate="c")
         times_beta(2, 0, 5, GPSIMD)
         times_beta(2, 5, 8)
         widen_k((26, 2), SCALAR)
+        fetch_k(18)
+        turn_k((26, 2))
         widen_k((28, 2), SCALAR)
         for q in (6, 7):
             for u in range(2):
                 subtract_vo(q, u)
-        turn_k((26, 2))
+        turn_k((28, 2), 0, 1, ps_v, "v_bank")
         stage_k(24, 4)
         fetch_k(24)
-        turn_k((28, 2), 0, 2, ps_v, "v_bank")
         widen_k((30, 2), SCALAR)
         fetch_k(26)
         stage_k(28, 4)
@@ -571,19 +593,24 @@ def tile_dpfpattention_pb_kernel(tc, x, wv, beta, vo, k_bytes, k_scale, W, out):
         quantise_dv(2, 0, 8)
         quantise_k(16, 4)
         second_product(2, 0, 8, ps_out, "out_bank")
+        turn_k((28, 2), 1, 2, ps_v, "v_bank")
+        fetch_k(29)
         stage_dv(3, 0, 8, gate="c")
         times_beta(3, 0, 3, GPSIMD)
         times_beta(3, 4, 8)
         times_beta(3, 3, 4)
         add_memory_and_store(2, 0, 8)
         quantise_k(24, 4)
-        quantise_dv(3, 0, 4)
-        second_product(3, 0, 4, ps_v, "v_bank")
-        quantise_k(28, 4)
-        quantise_dv(3, 4, 6)
-        second_product(3, 4, 6, ps_v, "v_bank")
-        quantise_dv(3, 6, 8)
+        quantise_dv(3, 0, 2)
+        second_product(3, 0, 2, ps_v, "v_bank")
+        quantise_dv(3, 2, 4)
+        second_product(3, 2, 4, ps_v, "v_bank")
+        quantise_dv(3, 4, 8)
+        quantise_k(30, 2)
         second_product(3, 6, 8, ps_v, "v_bank")
-        add_memory_and_store(3, 0, 4)
-        add_memory_and_store(3, 4, 6)
+        quantise_k(28, 2)
+        second_product(3, 4, 6, ps_v, "v_bank")
+        add_memory_and_store(3, 0, 2)
+        add_memory_and_store(3, 2, 4)
         add_memory_and_store(3, 6, 8)
+        add_memory_and_store(3, 4, 6)

@@ -416,20 +416,20 @@ def tile_dpfpattention_pb_kernel(tc, x, wv, beta, vo, k_bytes, k_scale, W, out):
         load_k(0, 2, 4)
         load_k(1, 0, 2)
         load_k(1, 2, 4)
-        load_beta()
         load_k(2)
         load_x(0, 0)
         load_x(0, 1)
         load_wv(0)
         load_wv(1)
         load_vo(0)
+        load_beta()
         load_k(3, 0, 2)
         load_vo(1)
         load_x(1, 0)
         load_k(3, 2, 4)
-        load_x(1, 1)
         load_k(4)
         load_vo(2)
+        load_x(1, 1)
         load_vo(3)
         load_k(5)
         load_vo(4)
@@ -443,7 +443,6 @@ def tile_dpfpattention_pb_kernel(tc, x, wv, beta, vo, k_bytes, k_scale, W, out):
             load_memory(o)
 
         place_scales()
-        place_beta()
         widen_k((0, 3), VECTOR)
         stage_k(0, 4)
         stage_k(4, 4)
@@ -494,6 +493,7 @@ def tile_dpfpattention_pb_kernel(tc, x, wv, beta, vo, k_bytes, k_scale, W, out):
         quantise_wv(1, 256, 512)
         for u in range(2):
             first_product(1, u, (1,))
+        place_beta()
         for g in range(2):
             turn_x(1, 0, g)
         quantise_k(8, 4)
@@ -503,8 +503,8 @@ def tile_dpfpattention_pb_kernel(tc, x, wv, beta, vo, k_bytes, k_scale, W, out):
         stage_wv(1, 512, 768, gate="d")
         interleave_wv(1, 512, 768, SCALAR)
         widen_k((12, 2), SCALAR)
-        cast_k(14, 2)
         fetch_beta()
+        cast_k(14, 2)
         for g in range(2):
             fetch_x(1, 0, g)
         for q in (0, 1):
@@ -572,8 +572,10 @@ def tile_dpfpattention_pb_kernel(tc, x, wv, beta, vo, k_bytes, k_scale, W, out):
 
         stage_dv(2, 0, 8, gate="c")
         times_beta(2, 0, 5, GPSIMD)
-        times_beta(2, 5, 8)
+        times_beta(2, 5, 7)
+        planar = times_beta_on_scalar(2, 7)
         widen_k((26, 2), SCALAR)
+        interleave_dv(2, 7, planar)
         fetch_k(18)
         turn_k((26, 2))
         widen_k((28, 2), SCALAR)

@@ -26,7 +26,7 @@ QW = 4 * DH
 RUN = {"vector": 4, "scalar": 2}
 SCALE_RUN = 2
 STAGES = {128: 1, 256: 6, 512: 7}
-PLANARS = {1: 2, 2: 6, 3: 1}
+PLANARS = {1: 3, 2: 6, 3: 1}
 WIDES = {1: 3, 2: 3}
 OCTET_ORDER = ((0, 0), (0, 8), (1, 0), (1, 8))
 JOINT = (0, 2, 4, 6)
@@ -117,7 +117,7 @@ def tile_dpfpattention_pb_kernel(tc, x, wv, beta, vo, k_bytes, k_scale, W, out):
 
 
         factors = {}
-        beta_sb = keep.tile([P, B * H, PACK], F32, name="beta_sb")
+        beta_sb = keep.tile([P, B * H, 2, PACK], F32, name="beta_sb")
 
         def place_scales():
             bank = ps_out.tile([P, PACK], F32, name="out_bank")
@@ -136,7 +136,7 @@ def tile_dpfpattention_pb_kernel(tc, x, wv, beta, vo, k_bytes, k_scale, W, out):
                 )
 
         def fetch_beta():
-            nc.scalar.copy(out=beta_sb[:], in_=factors["beta"][:])
+            nc.scalar.copy(out=beta_sb[:], in_=factors["beta"][:].unsqueeze(2).to_broadcast([P, B * H, 2, PACK]))
 
 
         def staging(columns, gate=None):
@@ -348,14 +348,19 @@ def tile_dpfpattention_pb_kernel(tc, x, wv, beta, vo, k_bytes, k_scale, W, out):
         def times_beta(o, a, e, engine=VECTOR):
             b, h0 = batch_and_head(o)
             row = H * b + h0
-            table = factors["beta"] if engine == VECTOR else beta_sb
-            product = nc.vector.tensor_tensor if engine == VECTOR else nc.gpsimd.tensor_tensor
-            tile, base = diff[2 * o + a // 4]
-            at = DH * (8 * o + a - 4 * base)
+            first, last = int(DH * a), int(DH * e)
+            if engine == VECTOR:
+                product = nc.vector.tensor_tensor
+                rows = factors["beta"][:, row + first // DH : row + (last + DH - 1) // DH, :]
+            else:
+                product = nc.gpsimd.tensor_tensor
+                rows = beta_sb[:].rearrange("p h j t -> p (h j) t")[:, int(2 * (row + a)) : int(2 * (row + e)), :]
+            tile, base = diff[2 * o + first // QW]
+            at = DH * (8 * o - 4 * base)
             product(
-                out=staged_dv(o, a, e),
-                in0=tile[:, :, at : at + DH * (e - a), :].rearrange("p u c t -> p c u t"),
-                in1=table[:, row + a : row + e, :].unsqueeze(2).to_broadcast([P, e - a, DH, PACK]),
+                out=staged_dv(o, 0, 8)[:, first:last, :],
+                in0=tile[:, :, at + first : at + last, :].rearrange("p u c t -> p c u t"),
+                in1=rows.unsqueeze(2).to_broadcast([P, rows.shape[1], (last - first) // rows.shape[1], PACK]),
                 op=MULT,
             )
 
@@ -369,7 +374,7 @@ def tile_dpfpattention_pb_kernel(tc, x, wv, beta, vo, k_bytes, k_scale, W, out):
                     out=planar[:, t, :],
                     in_=tile[:, t // 2, at : at + DH, t % 2],
                     func=COPY,
-                    scale=beta_sb[:, H * b + h0 + h, t : t + 1],
+                    scale=beta_sb[:, H * b + h0 + h, 0, t : t + 1],
                 )
             return planar
 
@@ -412,8 +417,7 @@ def tile_dpfpattention_pb_kernel(tc, x, wv, beta, vo, k_bytes, k_scale, W, out):
         load_k(0, 0, 1)
         load_k_scales()
         make_constants()
-        load_k(0, 1, 2)
-        load_k(0, 2, 4)
+        load_k(0, 1, 4)
         load_k(1, 0, 2)
         load_k(1, 2, 4)
         load_k(2)
@@ -443,13 +447,13 @@ def tile_dpfpattention_pb_kernel(tc, x, wv, beta, vo, k_bytes, k_scale, W, out):
             load_memory(o)
 
         place_scales()
-        widen_k((0, 3), VECTOR)
+        widen_k((0, 1), VECTOR)
+        widen_k((1, 3), VECTOR)
         stage_k(0, 4)
         stage_k(4, 4)
         stage_k(8, 4)
-        cast_k(3, 1)
-        interleave_k((0, 3), GPSIMD)
-        scale_k(3, 1)
+        interleave_k((0, 1), SCALAR)
+        interleave_k((1, 3), GPSIMD)
         cast_k(4, 1)
         cast_k(5, 1)
         cast_k(6, 2)
@@ -524,7 +528,7 @@ def tile_dpfpattention_pb_kernel(tc, x, wv, beta, vo, k_bytes, k_scale, W, out):
         turn_k((12, 2), 0, 2, ps_out, "out_bank")
 
         stage_dv(0, 0, 8, gate="d")
-        times_beta(0, 0, 6, GPSIMD)
+        times_beta(0, 0, 6.5, GPSIMD)
         widen_k((16, 2), SCALAR)
         widen_k((18, 2), SCALAR)
         fetch_x(1, 1, 0, gate="c")
@@ -532,7 +536,8 @@ def tile_dpfpattention_pb_kernel(tc, x, wv, beta, vo, k_bytes, k_scale, W, out):
         turn_k((16, 2))
         stage_k(12, 4)
         scale_k(14, 2, "late scale")
-        times_beta(0, 6, 8)
+        times_beta(0, 6.5, 7)
+        times_beta(0, 7, 8)
         for q in (2, 3):
             for u in range(2):
                 subtract_vo(q, u)
@@ -591,9 +596,9 @@ def tile_dpfpattention_pb_kernel(tc, x, wv, beta, vo, k_bytes, k_scale, W, out):
         interleave_k((30, 2), SCALAR)
         fetch_k(28)
         add_memory_and_store(1, 0, 8)
-        quantise_k(20, 4)
-        quantise_dv(2, 0, 8)
         quantise_k(16, 4)
+        quantise_dv(2, 0, 8)
+        quantise_k(20, 4)
         second_product(2, 0, 8, ps_out, "out_bank")
         turn_k((28, 2), 1, 2, ps_v, "v_bank")
         fetch_k(29)

@@ -519,8 +519,8 @@ def tile_dpfpattention_pb_kernel(tc, x, wv, beta, vo, k_bytes, k_scale, W, out):
         quantise_wv(1, 512, 768)
         for u in range(2):
             first_product(2, u, (1,))
-        quantise_wv(0, 768, 1024)
         quantise_wv(1, 768, 1024)
+        quantise_wv(0, 768, 1024)
         for u in range(2):
             first_product(3, u)
         turn_x(1, 1, 0)
@@ -534,7 +534,7 @@ def tile_dpfpattention_pb_kernel(tc, x, wv, beta, vo, k_bytes, k_scale, W, out):
         fetch_x(1, 1, 0, gate="c")
         fetch_x(1, 1, 1)
         turn_k((16, 2))
-        stage_k(12, 4)
+        stage_k(12, 4, gate="b")
         scale_k(14, 2, "late scale")
         times_beta(0, 6.5, 7)
         times_beta(0, 7, 8)
@@ -554,8 +554,9 @@ def tile_dpfpattention_pb_kernel(tc, x, wv, beta, vo, k_bytes, k_scale, W, out):
         turn_k((18, 2))
 
         stage_dv(1, 0, 8, gate="c")
-        times_beta(1, 0, 5, GPSIMD)
-        times_beta(1, 5, 8)
+        times_beta(1, 0, 5.5, GPSIMD)
+        times_beta(1, 6, 8)
+        times_beta(1, 5.5, 6)
         widen_k((22, 2), SCALAR)
         stage_k(20, 4)
         interleave_k((20, 2), SCALAR)
@@ -570,12 +571,12 @@ def tile_dpfpattention_pb_kernel(tc, x, wv, beta, vo, k_bytes, k_scale, W, out):
             for u in range(2):
                 first_product(q, u)
         add_memory_and_store(0, 0, 8)
-        quantise_dv(1, 0, 8)
         quantise_k(12, 4)
+        quantise_dv(1, 0, 8)
         second_product(1, 0, 8, ps_out, "out_bank")
         turn_k((24, 2))
 
-        stage_dv(2, 0, 8, gate="c")
+        stage_dv(2, 0, 8, gate="b")
         times_beta(2, 0, 5, GPSIMD)
         times_beta(2, 5, 7)
         planar = times_beta_on_scalar(2, 7)
@@ -602,7 +603,7 @@ def tile_dpfpattention_pb_kernel(tc, x, wv, beta, vo, k_bytes, k_scale, W, out):
         second_product(2, 0, 8, ps_out, "out_bank")
         turn_k((28, 2), 1, 2, ps_v, "v_bank")
         fetch_k(29)
-        stage_dv(3, 0, 8, gate="c")
+        stage_dv(3, 0, 8, gate="b")
         times_beta(3, 0, 3, GPSIMD)
         times_beta(3, 4, 8)
         times_beta(3, 3, 4)

from contextlib import ExitStack

import concourse.mybir as mybir
from concourse.masks import make_identity

B, N, D, H, DH = 2, 512, 1024, 16, 64
S = 128
FLOPS = 2 * B * N * D * H * DH + 2 * B * H * N * S * DH

F32 = mybir.dt.float32
BF16 = mybir.dt.bfloat16
U32 = mybir.dt.uint32
U8 = mybir.dt.uint8
FP8 = mybir.dt.float8_e4m3fn
FP8X4 = mybir.dt.float8_e4m3fn_x4
MULT = mybir.AluOpType.mult
ADD = mybir.AluOpType.add
SUB = mybir.AluOpType.subtract
COPY = mybir.ActivationFunctionType.Copy

P = 128
PACK = 4
QUADS = B * H // 4
OCTETS = B * H // 8
QW = 4 * DH
RUN = {"vector": 4, "scalar": 2}
SCALE_RUN = 2
STAGES = {128: 1, 256: 6, 512: 7}
PLANARS = {1: 3, 2: 6, 3: 1}
WIDES = {1: 3, 2: 3}
OCTET_ORDER = ((0, 0), (0, 8), (1, 0), (1, 8))
JOINT = (0, 2, 4, 6)
VECTOR, SCALAR, GPSIMD = "vector", "scalar", "gpsimd"


def batch_and_chunk(q):
    b, h0 = batch_and_head(q // 2)
    return b, h0 // 4 + q % 2


def batch_and_head(o):
    return OCTET_ORDER[o]


def tile_dpfpattention_pb_kernel(tc, x, wv, beta, vo, k_bytes, k_scale, W, out):
    nc = tc.nc
    with ExitStack() as ctx:
        keep = ctx.enter_context(tc.tile_pool(name="keep", bufs=1))
        work = ctx.enter_context(tc.tile_pool(name="work", bufs=4))
        ps_turn = ctx.enter_context(tc.psum_pool(name="ps_turn", bufs=2))
        ps_v = ctx.enter_context(tc.psum_pool(name="ps_v", bufs=4))
        ps_out = ctx.enter_context(tc.psum_pool(name="ps_out", bufs=1))
        ps_beta = ctx.enter_context(tc.psum_pool(name="ps_beta", bufs=1))
        ctx.enter_context(tc.manual_schedule())

        ident_f32 = keep.tile([P, P], F32, name="ident_f32")
        ident_bf16 = keep.tile([P, P], BF16, name="ident_bf16")
        beta_rows = keep.tile([P, N], BF16, name="beta_rows")
        k_scales = keep.tile([P, PACK], F32, name="k_scales")
        x_codes = [
            [keep.tile([P, 2, 2 * P], U32, align_bytes=64, name="x_codes%d%d" % (b, u)) for u in range(2)]
            for b in range(B)
        ]
        x_exps = [
            [keep.tile([P, 2, 2 * P], U8, align_bytes=64, name="x_exps%d%d" % (b, u)) for u in range(2)]
            for b in range(B)
        ]
        w_codes = keep.tile([P, 2, D], U32, align_bytes=64, name="w_codes")
        w_exps = keep.tile([P, 2, D], U8, align_bytes=64, name="w_exps")
        k_codes = keep.tile([P, B * H * S], U32, align_bytes=64, name="k_codes")
        k_exps = keep.tile([P, B * H * S], U8, align_bytes=64, name="k_exps")
        dv_codes = keep.tile([P, B * H * DH], U32, align_bytes=64, name="dv_codes")
        dv_exps = keep.tile([P, B * H * DH], U8, align_bytes=64, name="dv_exps")
        k_raw = [keep.tile([P, 4, PACK * S], U8, name="k_raw%d" % q) for q in range(QUADS)]
        vo_sb = [keep.tile([P, 4, PACK, DH], BF16, name="vo_sb%d" % q) for q in range(QUADS)]
        mem_sb = [keep.tile([P, 8, DH], BF16, name="mem_sb%d" % o) for o in range(OCTETS)]
        x_sb = [[keep.tile([P, 2, D], BF16, name="x_sb%d%d" % (b, u)) for u in range(2)] for b in range(B)]
        wv_sb = [keep.tile([P, PACK, D], BF16, name="wv_sb%d" % g) for g in range(2)]


        def load_k_scales():
            nc.sync.dma_start(out=k_scales[:], in_=k_scale.rearrange("a c (p t) e -> p (a c t e)", t=PACK))

        def load_beta():
            nc.sync.dma_start(out=beta_rows[0 : B * H, :], in_=beta.rearrange("b h n -> (b h) n"))

        def load_k(q, a=0, e=4):
            b, c = batch_and_chunk(q)
            nc.sync.dma_start(
                out=k_raw[q][:, a:e], in_=k_bytes[b, 4 * c + a : 4 * c + e].rearrange("h (p t) s -> p h (t s)", t=PACK)
            )

        def load_vo(q):
            b, c = batch_and_chunk(q)
            nc.sync.dma_start(
                out=vo_sb[q][:].rearrange("p h t d -> p h (t d)"),
                in_=vo[b, 4 * c : 4 * c + 4].rearrange("h (p t) d -> p h (t d)", t=PACK),
            )

        def load_x(b, u):
            nc.sync.dma_start(
                out=x_sb[b][u][:], in_=x[b].rearrange("(m t) k -> m t k", t=PACK)[:, 2 * u : 2 * u + 2, :]
            )

        def load_wv(g):
            nc.sync.dma_start(out=wv_sb[g][:], in_=wv.rearrange("(g p t) w -> g p t w", g=2, t=PACK)[g])

        def load_memory(o):
            b, h0 = batch_and_head(o)
            nc.sync.dma_start(out=mem_sb[o][:], in_=W[b, h0 : h0 + 8].rearrange("h s d -> s h d"))

        def make_constants():
            make_identity(nc, ident_bf16[:])
            nc.scalar.activation(out=ident_f32[:], in_=ident_bf16[:], func=COPY)
            nc.vector.memset(beta_rows[32:64, :], 0.0)
            nc.vector.memset(beta_rows[64:128, :], 0.0)


        factors = {}
        beta_sb = keep.tile([P, B * H, 2, PACK], F32, name="beta_sb")

        def place_scales():
            bank = ps_out.tile([P, PACK], F32, name="out_bank")
            factors["scale"] = bank
            nc.tensor.matmul(bank[:], lhsT=ident_f32[:], rhs=k_scales[:], start=True, stop=True)

        def place_beta():
            both = ps_beta.tile([P, B * H + 1, PACK], F32, name="beta_bank")
            bank = both[:, 0 : B * H, :]
            factors["beta"] = bank
            factors["late scale"] = both[:, B * H, :]
            nc.tensor.matmul(both[:, B * H, :], lhsT=ident_f32[:], rhs=k_scales[:], start=True, stop=True)
            for t in range(PACK):
                nc.tensor.matmul(
                    bank[:, :, t], lhsT=beta_rows[:, t::PACK], rhs=ident_bf16[:, 0 : B * H], start=True, stop=True
                )

        def fetch_beta():
            nc.scalar.copy(out=beta_sb[:], in_=factors["beta"][:].unsqueeze(2).to_broadcast([P, B * H, 2, PACK]))


        def staging(columns, gate=None):
            if gate:
                return work.tile([P, columns, PACK], BF16, align_bytes=64, name="gate_" + gate, bufs=1)
            return work.tile([P, columns, PACK], BF16, align_bytes=64, name="stage%d" % columns, bufs=STAGES[columns])

        def interleave(engine, dst, src):
            if engine == GPSIMD:
                nc.gpsimd.tensor_scalar(
                    out=dst, in0=src.rearrange("p h t n -> p h n t"), scalar1=1.0, scalar2=0.0, op0=MULT, op1=ADD
                )
                return
            copy = nc.vector.tensor_copy if engine == VECTOR else nc.scalar.copy
            copy(
                out=dst.rearrange("p (c i) t -> p c t i", i=RUN[engine]),
                in_=src.rearrange("p h t (c i) -> p h c t i", i=RUN[engine]),
            )

        def turn(src, pool=ps_turn, name="turned"):
            n = src.shape[1]
            bank = pool.tile([P, n * P, PACK], BF16, name=name)
            for a in range(n):
                nc.tensor.matmul(
                    bank[:, P * a : P * (a + 1), :].rearrange("p s t -> p t s"),
                    lhsT=ident_bf16[:],
                    rhs=src[:, a],
                    start=True,
                    stop=True,
                )
            return bank


        k_wide = {}
        k_planar = {}
        k_staging = {}
        k_banks = {}

        def cast_k(first, n):
            tile = work.tile([P, n, PACK, S], BF16, name="k_wide%d" % n, bufs=WIDES[n])
            for h in range(n):
                k_wide[first + h] = tile[:, h]
            nc.scalar.copy(
                out=tile[:].rearrange("p h t s -> p (h t s)"),
                in_=k_raw[first // 4][:, first % 4 : first % 4 + n, :].rearrange("p h c -> p (h c)").bitcast(FP8),
            )

        def scale_k(first, n, table="scale"):
            for h in range(first, first + n):
                nc.vector.tensor_tensor(
                    out=staged_k(h, 1).rearrange("p (c i) t -> p c t i", i=SCALE_RUN),
                    in0=k_wide[h].rearrange("p t (c i) -> p c t i", i=SCALE_RUN),
                    in1=factors[table][:].unsqueeze(1).unsqueeze(3).to_broadcast([P, S // SCALE_RUN, PACK, SCALE_RUN]),
                    op=MULT,
                )

        def widen_k(group, engine, a=0, e=None):
            first, n = group
            if first not in k_planar:
                k_planar[first] = work.tile([P, n, PACK, S], BF16, name="k_planar%d" % n, bufs=PLANARS[n])
            for h in range(a, n if e is None else e):
                for t in range(PACK):
                    codes = k_raw[(first + h) // 4][:, (first + h) % 4, S * t : S * (t + 1)].bitcast(FP8)
                    dst = k_planar[first][:, h, t, :]
                    if engine == VECTOR:
                        nc.vector.tensor_scalar(
                            out=dst, in0=codes, scalar1=k_scales[:, t : t + 1], scalar2=None, op0=MULT
                        )
                    else:
                        nc.scalar.activation(out=dst, in_=codes, func=COPY, scale=k_scales[:, t : t + 1])

        def stage_k(first, n, gate=None):
            tile = staging(n * S, gate)
            for h in range(first, first + n):
                k_staging[h] = (tile, first)

        def staged_k(first, n):
            tile, base = k_staging[first]
            return tile[:, S * (first - base) : S * (first - base + n), :]

        def planar_k(group, a, e):
            first, n = group
            return k_planar[first][:, a : n if e is None else e]

        def interleave_k(group, engine, a=0, e=None):
            src = planar_k(group, a, e)
            interleave(engine, staged_k(group[0] + a, src.shape[1]), src)

        def turn_k(group, a=0, e=None, *bank):
            k_banks[group[0] + a] = turn(planar_k(group, a, e), *bank)

        def fetch_k(first):
            nc.scalar.copy(out=staged_k(first, k_banks[first].shape[1] // S), in_=k_banks[first][:])

        def quantise_k(first, n):
            cols = slice(S * first, S * (first + n))
            nc.vector.quantize_mx(
                out=k_codes[:, cols].bitcast(FP8X4),
                scales=k_exps[:, cols],
                in_=staged_k(first, n).rearrange("p n t -> p (n t)"),
            )


        x_staging = {}
        x_banks = {}

        def turn_x(b, u, g, pool=ps_turn, name="turned"):
            bank = pool.tile([P, 2, 2, P], F32, name=name)
            x_banks[(b, u, g)] = bank
            for tt in range(2):
                words = x_sb[b][u][:, tt, 512 * g : 512 * (g + 1)].bitcast(F32)
                for e in range(2):
                    nc.tensor.transpose(bank[:, tt, e, :], words[:, e::2], ident_f32[:])

        def fetch_x(b, u, g, gate=None, engine=SCALAR):
            if (b, u) not in x_staging:
                x_staging[(b, u)] = staging(N, gate)
            copy = nc.vector.tensor_copy if engine == VECTOR else nc.scalar.copy
            copy(
                out=x_staging[(b, u)][:, 2 * P * g : 2 * P * (g + 1), :]
                .rearrange("p n j -> p (n j)")
                .bitcast(F32)
                .rearrange("p (t m e) -> p t m e", t=2, e=2),
                in_=x_banks[(b, u, g)][:].rearrange("p t e m -> p t m e"),
            )

        def quantise_x(b, u):
            nc.vector.quantize_mx(
                out=x_codes[b][u][:].rearrange("p g n -> p (g n)").bitcast(FP8X4),
                scales=x_exps[b][u][:].rearrange("p g n -> p (g n)"),
                in_=x_staging[(b, u)][:].rearrange("p n j -> p (n j)"),
            )


        w_staging = {}
        w_banks = {}

        def stage_wv(g, a, e, gate=None):
            tile = staging(e - a, gate)
            for column in range(a, e, DH):
                w_staging[(g, column)] = (tile, a)

        def staged_wv(g, a, e):
            tile, base = w_staging[(g, a)]
            return tile[:, a - base : e - base, :]

        def interleave_wv(g, a, e, engine):
            interleave(engine, staged_wv(g, a, e), wv_sb[g][:, :, a:e].unsqueeze(1))

        def turn_wv(g, a, e):
            w_banks[(g, a)] = turn(wv_sb[g][:, :, a:e].rearrange("p t (j n) -> p j t n", n=P))

        def fetch_wv(g, a, e):
            nc.scalar.copy(out=staged_wv(g, a, e), in_=w_banks[(g, a)][:])

        def quantise_wv(g, a, e):
            nc.vector.quantize_mx(
                out=w_codes[:, g, a:e].bitcast(FP8X4),
                scales=w_exps[:, g, a:e],
                in_=staged_wv(g, a, e).rearrange("p n t -> p (n t)"),
            )


        v_banks = {}

        def first_product(q, u, passes=(0, 1)):
            b, c = batch_and_chunk(q)
            if (q, u) not in v_banks:
                v_banks[(q, u)] = ps_v.tile([P, 2, QW], F32, name="v_bank")
            bank = v_banks[(q, u)]
            for g in passes:
                for tt in range(2):
                    nc.tensor.matmul_mx(
                        out=bank[:, tt, :],
                        lhsT=x_codes[b][u][:, g, P * tt : P * (tt + 1)].bitcast(FP8X4),
                        lhsT_scale=x_exps[b][u][:, g, P * tt : P * (tt + 1)],
                        rhs=w_codes[:, g, QW * c : QW * (c + 1)].bitcast(FP8X4),
                        rhs_scale=w_exps[:, g, QW * c : QW * (c + 1)],
                        start=(g == 0 and tt == 0),
                        stop=(g == 1 and tt == 1),
                    )

        diff = {}
        dv_staging = {}

        def subtract_vo(q, u):
            if q not in diff:
                n = 2 if q in JOINT else 1
                tile = work.tile([P, 2, n * QW, 2], F32, name="diff%d" % n, bufs=4 // n)
                for j in range(n):
                    diff[q + j] = (tile, q)
            tile, base = diff[q]
            nc.vector.tensor_tensor(
                out=tile[:, u, QW * (q - base) : QW * (q - base + 1), :],
                in0=v_banks[(q, u)][:].rearrange("p t c -> p c t"),
                in1=vo_sb[q][:, :, 2 * u : 2 * u + 2, :].rearrange("p h t d -> p h d t"),
                op=SUB,
            )

        def stage_dv(o, a, e, gate=None):
            tile = staging(DH * (e - a), gate)
            for h in range(a, e):
                dv_staging[(o, h)] = (tile, a)

        def staged_dv(o, a, e):
            tile, base = dv_staging[(o, a)]
            return tile[:, DH * (a - base) : DH * (e - base), :]

        def times_beta(o, a, e, engine=VECTOR):
            b, h0 = batch_and_head(o)
            row = H * b + h0
            first, last = int(DH * a), int(DH * e)
            if engine == VECTOR:
                product = nc.vector.tensor_tensor
                rows = factors["beta"][:, row + first // DH : row + (last + DH - 1) // DH, :]
            else:
                product = nc.gpsimd.tensor_tensor
                rows = beta_sb[:].rearrange("p h j t -> p (h j) t")[:, int(2 * (row + a)) : int(2 * (row + e)), :]
            tile, base = diff[2 * o + first // QW]
            at = DH * (8 * o - 4 * base)
            product(
                out=staged_dv(o, 0, 8)[:, first:last, :],
                in0=tile[:, :, at + first : at + last, :].rearrange("p u c t -> p c u t"),
                in1=rows.unsqueeze(2).to_broadcast([P, rows.shape[1], (last - first) // rows.shape[1], PACK]),
                op=MULT,
            )

        def times_beta_on_scalar(o, h):
            b, h0 = batch_and_head(o)
            tile, base = diff[2 * o + h // 4]
            at = DH * (8 * o + h - 4 * base)
            planar = work.tile([P, PACK, DH], BF16, name="dv_planar", bufs=2)
            for t in range(PACK):
                nc.scalar.activation(
                    out=planar[:, t, :],
                    in_=tile[:, t // 2, at : at + DH, t % 2],
                    func=COPY,
                    scale=beta_sb[:, H * b + h0 + h, 0, t : t + 1],
                )
            return planar

        def interleave_dv(o, h, planar):
            interleave(SCALAR, staged_dv(o, h, h + 1), planar[:].unsqueeze(1))

        def quantise_dv(o, a, e):
            cols = slice(DH * (8 * o + a), DH * (8 * o + e))
            nc.vector.quantize_mx(
                out=dv_codes[:, cols].bitcast(FP8X4),
                scales=dv_exps[:, cols],
                in_=staged_dv(o, a, e).rearrange("p n t -> p (n t)"),
            )


        out_banks = {}

        def second_product(o, a, e, pool, name):
            bank = pool.tile([P, e - a, DH], F32, name=name)
            out_banks[(o, a)] = bank
            for h in range(a, e):
                head = 8 * o + h
                nc.tensor.matmul_mx(
                    out=bank[:, h - a, :],
                    lhsT=k_codes[:, S * head : S * (head + 1)].bitcast(FP8X4),
                    lhsT_scale=k_exps[:, S * head : S * (head + 1)],
                    rhs=dv_codes[:, DH * head : DH * (head + 1)].bitcast(FP8X4),
                    rhs_scale=dv_exps[:, DH * head : DH * (head + 1)],
                    start=True,
                    stop=True,
                )

        def add_memory_and_store(o, a, e):
            result = work.tile([P, e - a, DH], F32, name="result%d" % (e - a), bufs=4 if e - a == 2 else 2)
            nc.vector.tensor_tensor(out=result[:], in0=out_banks[(o, a)][:], in1=mem_sb[o][:, a:e, :], op=ADD)
            b, first = batch_and_head(o)
            nc.sync.dma_start(out=out[b, first + a : first + e].rearrange("h s d -> s h d"), in_=result[:])


        load_k(0, 0, 1)
        load_k_scales()
        make_constants()
        load_k(0, 1, 4)
        load_k(1, 0, 2)
        load_k(1, 2, 4)
        load_k(2)
        load_x(0, 0)
        load_x(0, 1)
        load_wv(0)
        load_wv(1)
        load_vo(0)
        load_beta()
        load_k(3, 0, 2)
        load_vo(1)
        load_x(1, 0)
        load_k(3, 2, 4)
        load_k(4)
        load_vo(2)
        load_x(1, 1)
        load_vo(3)
        load_k(5)
        load_vo(4)
        load_vo(5)
        load_k(6)
        load_memory(0)
        load_k(7)
        load_vo(6)
        load_vo(7)
        for o in range(1, OCTETS):
            load_memory(o)

        place_scales()
        widen_k((0, 1), VECTOR)
        widen_k((1, 3), VECTOR)
        stage_k(0, 4)
        stage_k(4, 4)
        stage_k(8, 4)
        interleave_k((0, 1), SCALAR)
        interleave_k((1, 3), GPSIMD)
        cast_k(4, 1)
        cast_k(5, 1)
        cast_k(6, 2)
        widen_k((8, 1), SCALAR)
        interleave_k((8, 1), GPSIMD)
        scale_k(4, 4)
        cast_k(9, 2)
        widen_k((11, 1), SCALAR)
        interleave_k((11, 1), SCALAR)
        scale_k(9, 2)
        for u in range(2):
            for g in range(2):
                turn_x(0, u, g, ps_v, "v_bank")
        for u in range(2):
            for g in range(2):
                fetch_x(0, u, g)
        turn_wv(0, 768, 1024)
        stage_wv(0, 0, 512)
        stage_wv(0, 512, 768)
        interleave_wv(0, 384, 512, SCALAR)
        interleave_wv(0, 512, 768, SCALAR)
        quantise_k(0, 4)
        quantise_k(4, 4)
        quantise_x(0, 0)
        interleave_wv(0, 0, 384, VECTOR)
        quantise_x(0, 1)
        quantise_wv(0, 0, 512)
        for q in (0, 1):
            for u in range(2):
                first_product(q, u, (0,))
        stage_wv(1, 0, 256)
        stage_wv(1, 256, 512, gate="b")
        interleave_wv(1, 256, 512, SCALAR)
        stage_wv(0, 768, 1024)
        fetch_wv(0, 768, 1024)
        interleave_wv(1, 0, 256, VECTOR)
        quantise_wv(0, 512, 768)
        quantise_wv(1, 0, 256)
        for u in range(2):
            first_product(0, u, (1,))
        quantise_wv(1, 256, 512)
        for u in range(2):
            first_product(1, u, (1,))
        place_beta()
        for g in range(2):
            turn_x(1, 0, g)
        quantise_k(8, 4)

        stage_wv(1, 768, 1024, gate="b")
        interleave_wv(1, 768, 1024, GPSIMD)
        stage_wv(1, 512, 768, gate="d")
        interleave_wv(1, 512, 768, SCALAR)
        widen_k((12, 2), SCALAR)
        fetch_beta()
        cast_k(14, 2)
        for g in range(2):
            fetch_x(1, 0, g)
        for q in (0, 1):
            for u in range(2):
                subtract_vo(q, u)
        for u in range(2):
            first_product(2, u, (0,))
        quantise_wv(1, 512, 768)
        for u in range(2):
            first_product(2, u, (1,))
        quantise_wv(1, 768, 1024)
        quantise_wv(0, 768, 1024)
        for u in range(2):
            first_product(3, u)
        turn_x(1, 1, 0)
        turn_x(1, 1, 1)
        turn_k((12, 2), 0, 2, ps_out, "out_bank")

        stage_dv(0, 0, 8, gate="d")
        times_beta(0, 0, 6.5, GPSIMD)
        widen_k((16, 2), SCALAR)
        widen_k((18, 2), SCALAR)
        fetch_x(1, 1, 0, gate="c")
        fetch_x(1, 1, 1)
        turn_k((16, 2))
        stage_k(12, 4, gate="b")
        scale_k(14, 2, "late scale")
        times_beta(0, 6.5, 7)
        times_beta(0, 7, 8)
        for q in (2, 3):
            for u in range(2):
                subtract_vo(q, u)
        widen_k((20, 2), SCALAR)
        fetch_k(12)
        quantise_x(1, 0)
        first_product(4, 0)
        first_product(5, 0)
        quantise_x(1, 1)
        first_product(4, 1)
        first_product(5, 1)
        quantise_dv(0, 0, 8)
        second_product(0, 0, 8, ps_out, "out_bank")
        turn_k((18, 2))

        stage_dv(1, 0, 8, gate="c")
        times_beta(1, 0, 5.5, GPSIMD)
        times_beta(1, 6, 8)
        times_beta(1, 5.5, 6)
        widen_k((22, 2), SCALAR)
        stage_k(20, 4)
        interleave_k((20, 2), SCALAR)
        stage_k(16, 4)
        fetch_k(16)
        widen_k((24, 2), SCALAR)
        interleave_k((22, 2), SCALAR)
        for u in range(2):
            for q in (4, 5):
                subtract_vo(q, u)
        for q in (6, 7):
            for u in range(2):
                first_product(q, u)
        add_memory_and_store(0, 0, 8)
        quantise_k(12, 4)
        quantise_dv(1, 0, 8)
        second_product(1, 0, 8, ps_out, "out_bank")
        turn_k((24, 2))

        stage_dv(2, 0, 8, gate="b")
        times_beta(2, 0, 5, GPSIMD)
        times_beta(2, 5, 7)
        planar = times_beta_on_scalar(2, 7)
        widen_k((26, 2), SCALAR)
        interleave_dv(2, 7, planar)
        fetch_k(18)
        turn_k((26, 2))
        widen_k((28, 2), SCALAR)
        for q in (6, 7):
            for u in range(2):
                subtract_vo(q, u)
        turn_k((28, 2), 0, 1, ps_v, "v_bank")
        stage_k(24, 4)
        fetch_k(24)
        widen_k((30, 2), SCALAR)
        fetch_k(26)
        stage_k(28, 4)
        interleave_k((30, 2), SCALAR)
        fetch_k(28)
        add_memory_and_store(1, 0, 8)
        quantise_k(16, 4)
        quantise_dv(2, 0, 8)
        quantise_k(20, 4)
        second_product(2, 0, 8, ps_out, "out_bank")
        turn_k((28, 2), 1, 2, ps_v, "v_bank")
        fetch_k(29)
        stage_dv(3, 0, 8, gate="b")
        times_beta(3, 0, 3, GPSIMD)
        times_beta(3, 4, 8)
        times_beta(3, 3, 4)
        add_memory_and_store(2, 0, 8)
        quantise_k(24, 4)
        quantise_dv(3, 0, 2)
        second_product(3, 0, 2, ps_v, "v_bank")
        quantise_dv(3, 2, 4)
        second_product(3, 2, 4, ps_v, "v_bank")
        quantise_dv(3, 4, 8)
        quantise_k(30, 2)
        second_product(3, 6, 8, ps_v, "v_bank")
        quantise_k(28, 2)
        second_product(3, 4, 6, ps_v, "v_bank")
        add_memory_and_store(3, 0, 2)
        add_memory_and_store(3, 2, 4)
        add_memory_and_store(3, 6, 8)
        add_memory_and_store(3, 4, 6)
